import numpy as np
import ml_dtypes


def mxq(x, axis, fmt="e4m3"):
    dtype, down = {"e4m3": (ml_dtypes.float8_e4m3fn, 7), "e5m2": (ml_dtypes.float8_e5m2, 14)}[fmt]
    v = np.moveaxis(np.asarray(x, np.float32).astype(ml_dtypes.bfloat16).astype(np.float64), axis, -1)
    blocks = v.reshape(v.shape[:-1] + (-1, 32))
    amax = np.abs(blocks).max(-1, keepdims=True)
    byte = np.maximum(np.where(amax > 0, np.frexp(amax)[1] - 1 + 127, 0) - down, 1)
    scale = np.exp2(byte - 127.0)
    codes = (blocks / scale).astype(np.float32).astype(dtype).astype(np.float64)
    return np.moveaxis((codes * scale).reshape(v.shape), -1, axis)


WIDE = False


def mx_kscale(k):
    if not WIDE:
        return np.ones(k)
    levels = np.array([10, -10, 5, -5, 0])
    if k % 512:
        return np.exp2(np.random.permutation(np.resize(levels, k // 32))).repeat(32)
    a = np.empty((k // 512, 16))
    for p in range(k // 512):
        a[p, :8] = np.random.permutation(np.resize(levels, 8))
        for g in range(8):
            far = levels[np.abs(levels - a[p, g]) >= 10]
            a[p, g + 8] = far[np.random.randint(len(far))]
    return np.exp2(a.ravel()).repeat(32)


BF16 = ml_dtypes.bfloat16


def bf(x):
    return np.asarray(x, np.float32).astype(BF16)


def f64(x):
    return np.asarray(x).astype(np.float64)


E2M1 = np.array([0.0, 0.5, 1.0, 1.5, 2.0, 3.0, 4.0, 6.0, -0.0, -0.5, -1.0, -1.5, -2.0, -3.0, -4.0, -6.0])


def pack_weight(w, fmt):
    k, n = w.shape
    w = f64(bf(w)).reshape(k // 32, 32, n)
    amax = np.abs(w).max(1)
    if fmt == "e4m3":
        byte = np.frexp(amax)[1] - 1 + 127 - 7
    else:
        mant, ex = np.frexp(amax / 6.0)
        byte = np.where(mant > 0.5, ex, ex - 1) + 127
    byte = np.clip(np.where(amax > 0, byte, 1), 1, 254)
    scaled = (w * np.exp2(127.0 - byte)[:, None, :]).reshape(k, n).astype(np.float32)
    by_word = np.ascontiguousarray(scaled.reshape(k // 512, 128, 4, n).transpose(0, 1, 3, 2))
    if fmt == "e4m3":
        words = by_word.astype(ml_dtypes.float8_e4m3fn).view(np.uint8)
    else:
        c = by_word.astype(ml_dtypes.float4_e2m1fn).view(np.uint8) & 0xF
        words = c[..., 0::2] | (c[..., 1::2] << 4)
    return np.ascontiguousarray(words), np.ascontiguousarray(byte.astype(np.uint8).reshape(k // 512, 16, n))


def unpack_weight(words, scales, fmt):
    g, p, n, _ = words.shape
    if fmt == "e4m3":
        vals = np.ascontiguousarray(words).view(ml_dtypes.float8_e4m3fn).astype(np.float64)
    else:
        nib = np.empty((g, p, n, 4), np.uint8)
        nib[..., 0::2] = words & 0xF
        nib[..., 1::2] = words >> 4
        vals = E2M1[nib]
    vals = vals * np.repeat(np.exp2(scales.astype(np.float64) - 127.0), 8, axis=1)[..., None]
    return vals.transpose(0, 1, 3, 2).reshape(g * 512, n)
def pack4(w):
    words, scales = pack_weight(w, "e2m1")
    return words.reshape(words.shape[0], 128, -1), scales


def unpack4(words, scales):
    return unpack_weight(words.reshape(words.shape[0], 128, -1, 2), scales, "e2m1")


N, M, D, F = 1024, 1024, 1024, 1024


def draw0():
    s, t = mx_kscale(N), mx_kscale(D)
    adj = bf((np.random.standard_normal((M, N)) / np.sqrt(D) + np.eye(M, N)) * s)
    x = bf(np.random.standard_normal((N, D)) / s[:, None] * t)
    words, scales = pack4(np.random.standard_normal((D, F)) * np.sqrt(2.0 / D) / t[:, None])
    return {"adj": adj,
            "x": x,
            "weight_words": words,
            "weight_scales": scales}


def core(adj, x, weight_words, weight_scales):
    ax = mxq(f64(adj), 1, "e4m3") @ mxq(f64(x), 0, "e4m3")
    return mxq(ax, 1, "e4m3") @ unpack4(weight_words, weight_scales)


def e4m3fn_bytes(y):
    return np.clip(np.asarray(y, np.float64), -448.0, 448.0).astype(np.float32).astype(ml_dtypes.float8_e4m3fn).view(np.uint8)


def e4m3fn_values(b):
    return np.asarray(b, np.uint8).view(ml_dtypes.float8_e4m3fn).astype(np.float64)


def setup_inputs():
    d = draw0()
    x0 = np.asarray(d['adj']).astype(np.float64)
    s = (np.max(np.abs(x0), axis=(0,), keepdims=True) / 448.0).astype(np.float32)
    out = {}
    for k, v in d.items():
        if k == 'adj':
            out['adj_bytes'] = e4m3fn_bytes(x0 / s.astype(np.float64))
            out['adj_scale'] = s
        else:
            out[k] = v
    return out


def reference(adj_bytes, adj_scale, x, weight_words, weight_scales):
    return core(e4m3fn_values(adj_bytes) * adj_scale.astype(np.float64), x, weight_words, weight_scales)

@@ -1,0 +1,324 @@
+from contextlib import ExitStack
+
+import concourse.mybir as mybir
+from concourse.masks import make_identity
+
+F32 = mybir.dt.float32
+BF16 = mybir.dt.bfloat16
+U32 = mybir.dt.uint32
+I32 = mybir.dt.int32
+U8 = mybir.dt.uint8
+FP8 = mybir.dt.float8_e4m3fn
+FP8X4 = mybir.dt.float8_e4m3fn_x4
+FP4X4 = mybir.dt.float4_e2m1fn_x4
+MULT = mybir.AluOpType.mult
+
+P = 128
+N = 1024
+NB = 8
+PERM_FROM = 4
+FLOPS = 2 * 2 * N * N * N
+
+
+def tile_graphconvolution_pb_w4_kernel(tc, adj_bytes, adj_scale, x, weight_words, weight_scales, out):
+    nc = tc.nc
+    with ExitStack() as ctx:
+        keep = ctx.enter_context(tc.tile_pool(name="keep", bufs=1))
+        rot = ctx.enter_context(tc.tile_pool(name="rot", bufs=8))
+        ps_t = ctx.enter_context(tc.psum_pool(name="ps_t", bufs=2))
+        ps_a = ctx.enter_context(tc.psum_pool(name="ps_a", bufs=3))
+        ps_o = ctx.enter_context(tc.psum_pool(name="ps_o", bufs=3))
+        ctx.enter_context(tc.manual_schedule())
+
+        sc_col = keep.tile([P, 2, 4], F32)
+        nc.sync.dma_start(out=sc_col[:], in_=adj_scale.rearrange("o (h p c) -> p (o h) c", h=2, c=4))
+
+        xraw = {}
+
+        def load_x(g, h):
+            t = keep.tile([P, 4, 512], BF16, name="xraw%d%d" % (g, h), align_bytes=64)
+            nc.sync.dma_start(out=t[:], in_=x[512 * g : 512 * g + 512, 512 * h : 512 * h + 512].rearrange("(p t) d -> p t d", t=4))
+            xraw[g, h] = t
+
+        adj8 = {}
+        rows = {}
+
+        def load_adj(first, n):
+            t = keep.tile([P, n, N], U8, name="adjb%d" % first, align_bytes=64)
+            r = slice(P * first, P * (first + n))
+            nc.sync.dma_start(out=t[:], in_=adj_bytes[r, :].rearrange("(p k) j -> p k j", k=n))
+            o = out[r, :].rearrange("(p k) f -> p k f", k=n)
+            for i in range(n):
+                adj8[first + i] = t[:, i, :]
+                rows[first + i] = o[:, i, :]
+
+        load_x(0, 0)
+        load_adj(0, 1)
+        load_x(1, 0)
+        load_x(0, 1)
+        load_adj(1, 1)
+        load_x(1, 1)
+        load_adj(2, 2)
+
+        wsc = keep.tile([P, 2, N], U8, align_bytes=64)
+        nc.vector.memset(wsc[:].rearrange("p g n -> p (g n)").bitcast(I32), 0)
+        for q in range(4):
+            nc.sync.dma_start(
+                out=wsc[32 * q : 32 * q + 4, :, :].bitcast(I32),
+                in_=weight_scales[:, 4 * q : 4 * q + 4, :].rearrange("g q n -> q g n").bitcast(I32),
+            )
+        w = keep.tile([P, 2, 2 * N], U8, align_bytes=64)
+        nc.sync.dma_start(out=w[:].bitcast(I32), in_=weight_words.rearrange("g p n -> p g n").bitcast(I32))
+        load_adj(4, 4)
+
+        ident = keep.tile([P, P], F32)
+        make_identity(nc, ident[:])
+        scbc = keep.tile([P, N], F32, align_bytes=64)
+        sc_banks = []
+
+        def sc_transposes():
+            for half in range(2):
+                bank = ps_t.tile([P, 4, P], F32, tag="tp")
+                for c in range(4):
+                    nc.tensor.transpose(bank[:, c, :], sc_col[:, half, c : c + 1].to_broadcast([P, P]), ident[:])
+                sc_banks.append(bank)
+
+        def sc_copy(half):
+            dst = scbc[:, 512 * half : 512 * half + 512].rearrange("q (p c) -> q p c", c=4)
+            src = sc_banks[half][:].rearrange("q c p -> q p c")
+            if half == 0:
+                nc.vector.tensor_copy(out=dst, in_=src)
+            else:
+                nc.scalar.copy(dst, src)
+
+
+        xcodes = keep.tile([P, 2, 2, 512], U32, align_bytes=64)
+        xscales = keep.tile([P, 2, 2, 512], U8, align_bytes=64)
+        xg = {}
+
+        def x_inter(eng, g, h, lo, hi):
+            if (g, h) not in xg:
+                t = keep.tile([P, 2048], BF16, name="xg%d%d" % (g, h), align_bytes=64)
+                xg[g, h] = t
+            src = xraw[g, h][:].rearrange("p t (m i a) -> p m a i t", i=2, a=4)[:, lo:hi]
+            dst = xg[g, h][:].rearrange("p (a m i t) -> p m a i t", a=4, i=2, t=4)[:, lo:hi]
+            if eng == "V":
+                nc.vector.tensor_copy(out=dst, in_=src)
+            else:
+                nc.scalar.copy(dst, src)
+
+        def x_quant(g, h):
+            nc.vector.quantize_mx(out=xcodes[:, h, g, :].bitcast(FP8X4), scales=xscales[:, h, g, :], in_=xg[g, h][:])
+
+        prods, banks, grouped, acodes, ascales = {}, {}, {}, {}, {}
+
+        def prod(b):
+            pr = rot.tile([P, N], BF16, align_bytes=64)
+            nc.vector.tensor_tensor(out=pr[:], in0=adj8[b].bitcast(FP8), in1=scbc[:], op=MULT)
+            prods[b] = pr
+
+        def perm(b):
+            if b >= PERM_FROM:
+                pr = prods[b]
+                pm = rot.tile([P, N], BF16, align_bytes=64)
+                nc.vector.tensor_copy(
+                    out=pm[:].bitcast(F32).rearrange("p (g u w) -> p g u w", g=2, u=2),
+                    in_=pr[:].bitcast(F32).rearrange("p (g w u) -> p g u w", g=2, u=2),
+                )
+                prods[b] = pm
+
+        def tp(b):
+            bank = ps_t.tile([P, 4, P], F32, tag="tp")
+            words = prods[b][:].bitcast(F32)
+            for g in range(2):
+                for u in range(2):
+                    lo = 256 * g
+                    if b >= PERM_FROM:
+                        cols = slice(lo + 128 * u, lo + 128 * u + 128)
+                    else:
+                        cols = slice(lo + u, lo + 256, 2)
+                    nc.tensor.transpose(bank[:, 2 * g + u, :], words[:, cols], ident[:])
+            banks[b] = bank
+
+        def tcopy(b):
+            gr = rot.tile([P, N], BF16, align_bytes=64)
+            nc.scalar.copy(
+                gr[:].bitcast(F32).rearrange("p (g r u) -> p g r u", g=2, u=2),
+                banks[b][:].rearrange("p (g u) r -> p g r u", u=2),
+            )
+            grouped[b] = gr
+
+        def aq(b):
+            ac = rot.tile([P, 256], U32, align_bytes=64)
+            asc = rot.tile([P, 256], U8, align_bytes=64)
+            nc.vector.quantize_mx(out=ac[:].bitcast(FP8X4), scales=asc[:], in_=grouped[b][:])
+            acodes[b] = ac
+            ascales[b] = asc
+
+        ax_ps, axg, axc, axs = {}, {}, {}, {}
+
+        def s1(b, h):
+            acc = ps_a.tile([P, 4, P], F32)
+            for a in range(4):
+                cols = slice(P * a, P * a + P)
+                for g in range(2):
+                    nc.tensor.matmul_mx(
+                        out=acc[:, a, :],
+                        lhsT=xcodes[:, h, g, cols].bitcast(FP8X4),
+                        lhsT_scale=xscales[:, h, g, cols],
+                        rhs=acodes[b][:, P * g : P * g + P].bitcast(FP8X4),
+                        rhs_scale=ascales[b][:, P * g : P * g + P],
+                        start=(g == 0),
+                        stop=(g == 1),
+                    )
+            ax_ps[b, h] = acc
+
+        def ax_copy(b, h):
+            axt = rot.tile([P, 512], BF16, name="axt%d" % h, align_bytes=64)
+            src = ax_ps[b, h][:].rearrange("p a r -> p r a")
+            dst = axt[:].rearrange("p (r a) -> p r a", a=4)
+            if b >= 2 and b % 2 == 1 and h == 0:
+                nc.vector.tensor_copy(out=dst, in_=src)
+            else:
+                nc.scalar.copy(dst, src)
+            axg[b, h] = axt
+
+        def axq(b, h):
+            if b not in axc:
+                cod = rot.tile([P, 256], U32, align_bytes=64)
+                sca = rot.tile([P, 256], U8, align_bytes=64)
+                axc[b] = cod
+                axs[b] = sca
+            cols = slice(P * h, P * h + P)
+            nc.vector.quantize_mx(out=axc[b][:, cols].bitcast(FP8X4), scales=axs[b][:, cols], in_=axg[b, h][:])
+
+        o_ps, o_sb = {}, {}
+
+        def s2(b, f):
+            acc = ps_o.tile([P, 512], F32, tag="acc")
+            for h in range(2):
+                cols = slice(P * h, P * h + P)
+                nc.tensor.matmul_mx(
+                    out=acc[:],
+                    lhsT=axc[b][:, cols].bitcast(FP8X4),
+                    lhsT_scale=axs[b][:, cols],
+                    rhs=w[:, h, 1024 * f : 1024 * f + 1024].bitcast(FP4X4),
+                    rhs_scale=wsc[:, h, 512 * f : 512 * f + 512],
+                    start=(h == 0),
+                    stop=(h == 1),
+                )
+            o_ps[b, f] = acc
+
+        def o_copy(b, f):
+            if f == 0:
+                ot = rot.tile([P, N], F32)
+                o_sb[b] = ot
+            if b == NB - 1 and f == 1:
+                for z in range(2):
+                    cols = slice(512 + 256 * z, 768 + 256 * z)
+                    part = o_ps[b, f][:, 256 * z : 256 * z + 256]
+                    if z == 0:
+                        nc.vector.tensor_copy(out=o_sb[b][:, cols], in_=part)
+                    else:
+                        nc.scalar.copy(o_sb[b][:, cols], part)
+                    nc.sync.dma_start(out=rows[b][:, cols], in_=o_sb[b][:, cols])
+                return
+            dst = o_sb[b][:, 512 * f : 512 * f + 512]
+            if f == 1:
+                nc.vector.tensor_copy(out=dst, in_=o_ps[b, f][:])
+            else:
+                nc.scalar.copy(dst, o_ps[b, f][:])
+            nc.sync.dma_start(out=rows[b][:, 512 * f : 512 * f + 512], in_=dst)
+
+        ones = keep.tile([P, 512], BF16, align_bytes=64)
+        nc.vector.memset(ones[:], 1.0)
+
+        def warm(n):
+            for i in range(n):
+                acc = ps_o.tile([P, 512], F32, tag="acc")
+                nc.tensor.matmul(acc[:], lhsT=ones[:, 0:P], rhs=ones[:], start=True, stop=True)
+
+        def s_xi(g, h, lo, hi):
+            x_inter("S", g, h, lo, hi)
+
+        def v_xi(g, h, lo, hi):
+            x_inter("V", g, h, lo, hi)
+
+        s_xi(0, 0, 0, 16)
+        sc_transposes()
+        v_xi(0, 0, 32, 64)
+        s_xi(0, 0, 16, 32)
+        sc_copy(0)
+        sc_copy(1)
+        x_quant(0, 0)
+        prod(0)
+        tp(0)
+        warm(2)
+        s_xi(1, 0, 16, 48)
+        s_xi(0, 1, 32, 48)
+        v_xi(0, 1, 48, 64)
+        s_xi(1, 0, 0, 16)
+        s_xi(0, 1, 0, 16)
+        s_xi(1, 1, 16, 32)
+        v_xi(1, 0, 48, 64)
+        prod(1)
+        tp(1)
+        warm(2)
+        prod(2)
+        tcopy(0)
+        prod(3)
+        tcopy(1)
+        aq(0)
+        s_xi(1, 1, 48, 64)
+        x_quant(1, 0)
+        tp(2)
+        warm(1)
+        v_xi(0, 1, 16, 32)
+        s_xi(1, 1, 0, 16)
+        aq(1)
+        tp(3)
+        warm(1)
+        s1(0, 0)
+        s1(1, 0)
+        x_quant(0, 1)
+        tcopy(2)
+        s_xi(1, 1, 32, 48)
+        aq(2)
+        s1(2, 0)
+        x_quant(1, 1)
+        ax_copy(0, 0)
+        s1(0, 1)
+        ax_copy(1, 0)
+        s1(1, 1)
+        prod(4)
+        axq(0, 0)
+        perm(4)
+        tp(4)
+        ax_copy(0, 1)
+        s1(2, 1)
+        ax_copy(1, 1)
+        tcopy(3)
+        axq(0, 1)
+
+        def at(fn, b, *args):
+            if 0 <= b < NB:
+                fn(b, *args)
+
+        for b in range(NB):
+            at(o_copy, b - 1, 0)
+            s2(b, 0)
+            at(axq, b + 1, 0)
+            at(axq, b + 1, 1)
+            s2(b, 1)
+            at(ax_copy, b + 2, 1)
+            at(aq, b + 3)
+            at(s1, b + 3, 1)
+            at(s1, b + 3, 0)
+            at(tcopy, b + 4)
+            at(prod, b + 5)
+            at(o_copy, b - 1, 1)
+            at(perm, b + 5)
+            at(tp, b + 5)
+            at(ax_copy, b + 2, 0)
+        o_copy(NB - 1, 0)
+        o_copy(NB - 1, 1)

@@ -230,14 +230,6 @@ def tile_graphconvolution_pb_w4_kernel(tc, adj_bytes, adj_scale, x, weight_words
                 nc.scalar.copy(dst, o_ps[b, f][:])
             nc.sync.dma_start(out=rows[b][:, 512 * f : 512 * f + 512], in_=dst)
 
-        ones = keep.tile([P, 512], BF16, align_bytes=64)
-        nc.vector.memset(ones[:], 1.0)
-
-        def warm(n):
-            for i in range(n):
-                acc = ps_o.tile([P, 512], F32, tag="acc")
-                nc.tensor.matmul(acc[:], lhsT=ones[:, 0:P], rhs=ones[:], start=True, stop=True)
-
         def s_xi(g, h, lo, hi):
             x_inter("S", g, h, lo, hi)
 
@@ -253,7 +245,6 @@ def tile_graphconvolution_pb_w4_kernel(tc, adj_bytes, adj_scale, x, weight_words
         x_quant(0, 0)
         prod(0)
         tp(0)
-        warm(2)
         s_xi(1, 0, 16, 48)
         s_xi(0, 1, 32, 48)
         v_xi(0, 1, 48, 64)
@@ -263,7 +254,6 @@ def tile_graphconvolution_pb_w4_kernel(tc, adj_bytes, adj_scale, x, weight_words
         v_xi(1, 0, 48, 64)
         prod(1)
         tp(1)
-        warm(2)
         prod(2)
         tcopy(0)
         prod(3)
@@ -272,12 +262,10 @@ def tile_graphconvolution_pb_w4_kernel(tc, adj_bytes, adj_scale, x, weight_words
         s_xi(1, 1, 48, 64)
         x_quant(1, 0)
         tp(2)
-        warm(1)
         v_xi(0, 1, 16, 32)
         s_xi(1, 1, 0, 16)
         aq(1)
         tp(3)
-        warm(1)
         s1(0, 0)
         s1(1, 0)
         x_quant(0, 1)

@@ -16,7 +16,6 @@ MULT = mybir.AluOpType.mult
 P = 128
 N = 1024
 NB = 8
-PERM_FROM = 4
 FLOPS = 2 * 2 * N * N * N
 
 
@@ -25,23 +24,42 @@ def tile_graphconvolution_pb_w4_kernel(tc, adj_bytes, adj_scale, x, weight_words
     with ExitStack() as ctx:
         keep = ctx.enter_context(tc.tile_pool(name="keep", bufs=1))
         rot = ctx.enter_context(tc.tile_pool(name="rot", bufs=8))
-        ps_t = ctx.enter_context(tc.psum_pool(name="ps_t", bufs=2))
-        ps_a = ctx.enter_context(tc.psum_pool(name="ps_a", bufs=3))
-        ps_o = ctx.enter_context(tc.psum_pool(name="ps_o", bufs=3))
+        psum = ctx.enter_context(tc.psum_pool(name="psum", bufs=1))
         ctx.enter_context(tc.manual_schedule())
 
-        sc_col = keep.tile([P, 2, 4], F32)
-        nc.sync.dma_start(out=sc_col[:], in_=adj_scale.rearrange("o (h p c) -> p (o h) c", h=2, c=4))
+        def copy(eng, dst, src):
+            if eng == "V":
+                nc.vector.tensor_copy(out=dst, in_=src)
+            else:
+                nc.scalar.copy(dst, src)
 
+        held = []
+        emptied = set()
+
+        def bank_is_free():
+            return len(held) < 8 or held[-8] in emptied
+
+        def take_bank(key, shape):
+            held.append(key)
+            return psum.tile(shape, F32, name="bank%d" % ((len(held) - 1) % 8))
+
+        def give_bank(key):
+            emptied.add(key)
+
+        sc = keep.tile([P, 2, 4], F32)
         xraw = {}
+        adj8 = {}
+        rows = {}
+        wsc = keep.tile([P, 2, N], U8, align_bytes=64)
+        w = keep.tile([P, 2, 2 * N], U8, align_bytes=64)
+
+        def load_sc():
+            nc.sync.dma_start(out=sc[:], in_=adj_scale.rearrange("o (g p c) -> p (o g) c", g=2, c=4))
 
         def load_x(g, h):
             t = keep.tile([P, 4, 512], BF16, name="xraw%d%d" % (g, h), align_bytes=64)
             nc.sync.dma_start(out=t[:], in_=x[512 * g : 512 * g + 512, 512 * h : 512 * h + 512].rearrange("(p t) d -> p t d", t=4))
             xraw[g, h] = t
-
-        adj8 = {}
-        rows = {}
 
         def load_adj(first, n):
             t = keep.tile([P, n, N], U8, name="adjb%d" % first, align_bytes=64)
@@ -52,100 +70,72 @@ def tile_graphconvolution_pb_w4_kernel(tc, adj_bytes, adj_scale, x, weight_words
                 adj8[first + i] = t[:, i, :]
                 rows[first + i] = o[:, i, :]
 
-        load_x(0, 0)
-        load_adj(0, 1)
-        load_x(1, 0)
-        load_x(0, 1)
-        load_adj(1, 1)
-        load_x(1, 1)
-        load_adj(2, 2)
-
-        wsc = keep.tile([P, 2, N], U8, align_bytes=64)
-        nc.vector.memset(wsc[:].rearrange("p g n -> p (g n)").bitcast(I32), 0)
-        for q in range(4):
-            nc.sync.dma_start(
-                out=wsc[32 * q : 32 * q + 4, :, :].bitcast(I32),
-                in_=weight_scales[:, 4 * q : 4 * q + 4, :].rearrange("g q n -> q g n").bitcast(I32),
-            )
-        w = keep.tile([P, 2, 2 * N], U8, align_bytes=64)
-        nc.sync.dma_start(out=w[:].bitcast(I32), in_=weight_words.rearrange("g p n -> p g n").bitcast(I32))
-        load_adj(4, 4)
+        def load_w():
+            for q in range(4):
+                nc.sync.dma_start(
+                    out=wsc[32 * q : 32 * q + 4, :, :].bitcast(I32),
+                    in_=weight_scales[:, 4 * q : 4 * q + 4, :].rearrange("g q n -> q g n").bitcast(I32),
+                )
+            nc.sync.dma_start(out=w[:].bitcast(I32), in_=weight_words.rearrange("g p n -> p g n").bitcast(I32))
 
         ident = keep.tile([P, P], F32)
-        make_identity(nc, ident[:])
-        scbc = keep.tile([P, N], F32, align_bytes=64)
-        sc_banks = []
-
-        def sc_transposes():
-            for half in range(2):
-                bank = ps_t.tile([P, 4, P], F32, tag="tp")
-                for c in range(4):
-                    nc.tensor.transpose(bank[:, c, :], sc_col[:, half, c : c + 1].to_broadcast([P, P]), ident[:])
-                sc_banks.append(bank)
-
-        def sc_copy(half):
-            dst = scbc[:, 512 * half : 512 * half + 512].rearrange("q (p c) -> q p c", c=4)
-            src = sc_banks[half][:].rearrange("q c p -> q p c")
-            if half == 0:
-                nc.vector.tensor_copy(out=dst, in_=src)
-            else:
-                nc.scalar.copy(dst, src)
-
+        one = keep.tile([P, 1], F32)
 
         xcodes = keep.tile([P, 2, 2, 512], U32, align_bytes=64)
         xscales = keep.tile([P, 2, 2, 512], U8, align_bytes=64)
         xg = {}
 
-        def x_inter(eng, g, h, lo, hi):
+        def xi(eng, g, h, lo, hi):
             if (g, h) not in xg:
                 t = keep.tile([P, 2048], BF16, name="xg%d%d" % (g, h), align_bytes=64)
                 xg[g, h] = t
             src = xraw[g, h][:].rearrange("p t (m i a) -> p m a i t", i=2, a=4)[:, lo:hi]
             dst = xg[g, h][:].rearrange("p (a m i t) -> p m a i t", a=4, i=2, t=4)[:, lo:hi]
-            if eng == "V":
-                nc.vector.tensor_copy(out=dst, in_=src)
-            else:
-                nc.scalar.copy(dst, src)
+            copy(eng, dst, src)
 
-        def x_quant(g, h):
+        def xq(g, h):
             nc.vector.quantize_mx(out=xcodes[:, h, g, :].bitcast(FP8X4), scales=xscales[:, h, g, :], in_=xg[g, h][:])
 
-        prods, banks, grouped, acodes, ascales = {}, {}, {}, {}, {}
+        wide, sorted_words, banks, grouped, acodes, ascales = {}, {}, {}, {}, {}, {}
 
-        def prod(b):
-            pr = rot.tile([P, N], BF16, align_bytes=64)
-            nc.vector.tensor_tensor(out=pr[:], in0=adj8[b].bitcast(FP8), in1=scbc[:], op=MULT)
-            prods[b] = pr
-
-        def perm(b):
-            if b >= PERM_FROM:
-                pr = prods[b]
-                pm = rot.tile([P, N], BF16, align_bytes=64)
-                nc.vector.tensor_copy(
-                    out=pm[:].bitcast(F32).rearrange("p (g u w) -> p g u w", g=2, u=2),
-                    in_=pr[:].bitcast(F32).rearrange("p (g w u) -> p g u w", g=2, u=2),
+        def widen(eng, b):
+            wd = rot.tile([P, N], BF16, align_bytes=64)
+            src = adj8[b].bitcast(FP8)
+            if eng == "V":
+                nc.vector.tensor_scalar(
+                    out=wd[:].rearrange("q (u m e) -> q m u e", u=2, e=2),
+                    in0=src.rearrange("q (m u e) -> q m u e", u=2, e=2),
+                    scalar1=one[:],
+                    scalar2=None,
+                    op0=MULT,
                 )
-                prods[b] = pm
+            else:
+                nc.scalar.copy(wd[:], src)
+            wide[b] = wd
+            sorted_words[b] = eng == "V"
 
         def tp(b):
-            bank = ps_t.tile([P, 4, P], F32, tag="tp")
-            words = prods[b][:].bitcast(F32)
+            bank = take_bank(("t", b), [P, 2, 2, P])
+            words = wide[b][:].bitcast(F32)
             for g in range(2):
                 for u in range(2):
                     lo = 256 * g
-                    if b >= PERM_FROM:
-                        cols = slice(lo + 128 * u, lo + 128 * u + 128)
+                    if sorted_words[b]:
+                        cols = slice(256 * u + 128 * g, 256 * u + 128 * g + 128)
                     else:
                         cols = slice(lo + u, lo + 256, 2)
-                    nc.tensor.transpose(bank[:, 2 * g + u, :], words[:, cols], ident[:])
+                    nc.tensor.transpose(bank[:, u, g, :], words[:, cols], ident[:])
             banks[b] = bank
 
-        def tcopy(b):
+        def scale(b):
             gr = rot.tile([P, N], BF16, align_bytes=64)
-            nc.scalar.copy(
-                gr[:].bitcast(F32).rearrange("p (g r u) -> p g r u", g=2, u=2),
-                banks[b][:].rearrange("p (g u) r -> p g r u", u=2),
+            nc.vector.tensor_tensor(
+                out=gr[:].rearrange("p (g r u e) -> p g r u e", g=2, u=2, e=2),
+                in0=banks[b][:].bitcast(BF16).rearrange("p u g (r e) -> p g r u e", e=2),
+                in1=sc[:].rearrange("p g (u e) -> p g u e", e=2).unsqueeze(2).to_broadcast([P, 2, P, 2, 2]),
+                op=MULT,
             )
+            give_bank(("t", b))
             grouped[b] = gr
 
         def aq(b):
@@ -157,156 +147,181 @@ def tile_graphconvolution_pb_w4_kernel(tc, adj_bytes, adj_scale, x, weight_words
 
         ax_ps, axg, axc, axs = {}, {}, {}, {}
 
-        def s1(b, h):
-            acc = ps_a.tile([P, 4, P], F32)
+        def s1g(b, h, g):
+            if g == 0:
+                ax_ps[b, h] = take_bank(("a", b, h), [P, 4, P])
             for a in range(4):
                 cols = slice(P * a, P * a + P)
-                for g in range(2):
-                    nc.tensor.matmul_mx(
-                        out=acc[:, a, :],
-                        lhsT=xcodes[:, h, g, cols].bitcast(FP8X4),
-                        lhsT_scale=xscales[:, h, g, cols],
-                        rhs=acodes[b][:, P * g : P * g + P].bitcast(FP8X4),
-                        rhs_scale=ascales[b][:, P * g : P * g + P],
-                        start=(g == 0),
-                        stop=(g == 1),
-                    )
-            ax_ps[b, h] = acc
+                nc.tensor.matmul_mx(
+                    out=ax_ps[b, h][:, a, :],
+                    lhsT=xcodes[:, h, g, cols].bitcast(FP8X4),
+                    lhsT_scale=xscales[:, h, g, cols],
+                    rhs=acodes[b][:, P * g : P * g + P].bitcast(FP8X4),
+                    rhs_scale=ascales[b][:, P * g : P * g + P],
+                    start=(g == 0 and a == 0),
+                    stop=(g == 1 and a == 3),
+                )
 
-        def ax_copy(b, h):
-            axt = rot.tile([P, 512], BF16, name="axt%d" % h, align_bytes=64)
-            src = ax_ps[b, h][:].rearrange("p a r -> p r a")
-            dst = axt[:].rearrange("p (r a) -> p r a", a=4)
-            if b >= 2 and b % 2 == 1 and h == 0:
-                nc.vector.tensor_copy(out=dst, in_=src)
-            else:
-                nc.scalar.copy(dst, src)
-            axg[b, h] = axt
+        def s1(b, h):
+            s1g(b, h, 0)
+            s1g(b, h, 1)
 
-        def axq(b, h):
+        def ax_copy(eng, b, h):
+            if b not in axg:
+                axt = rot.tile([P, 2, 512], BF16, align_bytes=64)
+                axg[b] = axt
+            copy(eng, axg[b][:, h, :].rearrange("p (r a) -> p r a", a=4), ax_ps[b, h][:].rearrange("p a r -> p r a"))
+            give_bank(("a", b, h))
+
+        def axq(b, lo, hi):
             if b not in axc:
                 cod = rot.tile([P, 256], U32, align_bytes=64)
                 sca = rot.tile([P, 256], U8, align_bytes=64)
                 axc[b] = cod
                 axs[b] = sca
-            cols = slice(P * h, P * h + P)
-            nc.vector.quantize_mx(out=axc[b][:, cols].bitcast(FP8X4), scales=axs[b][:, cols], in_=axg[b, h][:])
+            cols = slice(P * lo, P * hi)
+            nc.vector.quantize_mx(out=axc[b][:, cols].bitcast(FP8X4), scales=axs[b][:, cols], in_=axg[b][:, lo:hi, :].rearrange("p h n -> p (h n)"))
 
         o_ps, o_sb = {}, {}
 
+        def s2h(b, f, h):
+            if h == 0:
+                o_ps[b, f] = take_bank(("o", b, f), [P, 512])
+            cols = slice(P * h, P * h + P)
+            nc.tensor.matmul_mx(
+                out=o_ps[b, f][:],
+                lhsT=axc[b][:, cols].bitcast(FP8X4),
+                lhsT_scale=axs[b][:, cols],
+                rhs=w[:, h, 1024 * f : 1024 * f + 1024].bitcast(FP4X4),
+                rhs_scale=wsc[:, h, 512 * f : 512 * f + 512],
+                start=(h == 0),
+                stop=(h == 1),
+            )
+
         def s2(b, f):
-            acc = ps_o.tile([P, 512], F32, tag="acc")
-            for h in range(2):
-                cols = slice(P * h, P * h + P)
-                nc.tensor.matmul_mx(
-                    out=acc[:],
-                    lhsT=axc[b][:, cols].bitcast(FP8X4),
-                    lhsT_scale=axs[b][:, cols],
-                    rhs=w[:, h, 1024 * f : 1024 * f + 1024].bitcast(FP4X4),
-                    rhs_scale=wsc[:, h, 512 * f : 512 * f + 512],
-                    start=(h == 0),
-                    stop=(h == 1),
-                )
-            o_ps[b, f] = acc
+            s2h(b, f, 0)
+            s2h(b, f, 1)
 
-        def o_copy(b, f):
-            if f == 0:
-                ot = rot.tile([P, N], F32)
-                o_sb[b] = ot
-            if b == NB - 1 and f == 1:
-                for z in range(2):
-                    cols = slice(512 + 256 * z, 768 + 256 * z)
-                    part = o_ps[b, f][:, 256 * z : 256 * z + 256]
-                    if z == 0:
-                        nc.vector.tensor_copy(out=o_sb[b][:, cols], in_=part)
-                    else:
-                        nc.scalar.copy(o_sb[b][:, cols], part)
-                    nc.sync.dma_start(out=rows[b][:, cols], in_=o_sb[b][:, cols])
-                return
-            dst = o_sb[b][:, 512 * f : 512 * f + 512]
-            if f == 1:
-                nc.vector.tensor_copy(out=dst, in_=o_ps[b, f][:])
-            else:
-                nc.scalar.copy(dst, o_ps[b, f][:])
-            nc.sync.dma_start(out=rows[b][:, 512 * f : 512 * f + 512], in_=dst)
+        def o_copy(eng, b, f):
+            ot = rot.tile([P, 512], F32, bufs=6)
+            copy(eng, ot[:], o_ps[b, f][:])
+            give_bank(("o", b, f))
+            o_sb[b, f] = ot
 
-        def s_xi(g, h, lo, hi):
-            x_inter("S", g, h, lo, hi)
+        def store(b, f):
+            nc.sync.dma_start(out=rows[b][:, 512 * f : 512 * f + 512], in_=o_sb[b, f][:])
 
-        def v_xi(g, h, lo, hi):
-            x_inter("V", g, h, lo, hi)
+        def s2q(b, z):
+            acc = take_bank(("q", b, z), [P, 256])
+            for c in range(2):
+                n0 = 256 * z + P * c
+                for h in range(2):
+                    cols = slice(P * h, P * h + P)
+                    nc.tensor.matmul_mx(
+                        out=acc[:, P * c : P * c + P],
+                        lhsT=axc[b][:, cols].bitcast(FP8X4),
+                        lhsT_scale=axs[b][:, cols],
+                        rhs=w[:, h, 2 * n0 : 2 * n0 + 2 * P].bitcast(FP4X4),
+                        rhs_scale=wsc[:, h, n0 : n0 + P],
+                        start=(h == 0),
+                        stop=(h == 1),
+                    )
+            o_ps[b, "q", z] = acc
 
-        s_xi(0, 0, 0, 16)
-        sc_transposes()
-        v_xi(0, 0, 32, 64)
-        s_xi(0, 0, 16, 32)
-        sc_copy(0)
-        sc_copy(1)
-        x_quant(0, 0)
-        prod(0)
-        tp(0)
-        s_xi(1, 0, 16, 48)
-        s_xi(0, 1, 32, 48)
-        v_xi(0, 1, 48, 64)
-        s_xi(1, 0, 0, 16)
-        s_xi(0, 1, 0, 16)
-        s_xi(1, 1, 16, 32)
-        v_xi(1, 0, 48, 64)
-        prod(1)
-        tp(1)
-        prod(2)
-        tcopy(0)
-        prod(3)
-        tcopy(1)
-        aq(0)
-        s_xi(1, 1, 48, 64)
-        x_quant(1, 0)
-        tp(2)
-        v_xi(0, 1, 16, 32)
-        s_xi(1, 1, 0, 16)
-        aq(1)
-        tp(3)
-        s1(0, 0)
-        s1(1, 0)
-        x_quant(0, 1)
-        tcopy(2)
-        s_xi(1, 1, 32, 48)
-        aq(2)
-        s1(2, 0)
-        x_quant(1, 1)
-        ax_copy(0, 0)
-        s1(0, 1)
-        ax_copy(1, 0)
-        s1(1, 1)
-        prod(4)
-        axq(0, 0)
-        perm(4)
-        tp(4)
-        ax_copy(0, 1)
-        s1(2, 1)
-        ax_copy(1, 1)
-        tcopy(3)
-        axq(0, 1)
+        def q_copy(eng, b, z):
+            oq = rot.tile([P, 256], F32, bufs=2)
+            copy(eng, oq[:], o_ps[b, "q", z][:])
+            give_bank(("q", b, z))
+            o_sb[b, "q", z] = oq
 
-        def at(fn, b, *args):
-            if 0 <= b < NB:
-                fn(b, *args)
+        def q_store(b, z):
+            nc.sync.dma_start(out=rows[b][:, 256 * z : 256 * z + 256], in_=o_sb[b, "q", z][:])
 
-        for b in range(NB):
-            at(o_copy, b - 1, 0)
-            s2(b, 0)
-            at(axq, b + 1, 0)
-            at(axq, b + 1, 1)
-            s2(b, 1)
-            at(ax_copy, b + 2, 1)
-            at(aq, b + 3)
-            at(s1, b + 3, 1)
-            at(s1, b + 3, 0)
-            at(tcopy, b + 4)
-            at(prod, b + 5)
-            at(o_copy, b - 1, 1)
-            at(perm, b + 5)
-            at(tp, b + 5)
-            at(ax_copy, b + 2, 0)
-        o_copy(NB - 1, 0)
-        o_copy(NB - 1, 1)
+        def warm(g, h):
+            acc = take_bank(("warm", len(held)), [P, 512])
+            nc.tensor.matmul(acc[:], lhsT=xg[g, h][:, 0:P], rhs=xg[g, h][:, 0:512], start=True, stop=True)
+            give_bank(held[-1])
+
+        issued = set()
+        x_cols = {}
+
+        def ready(fn, *a):
+            if fn == xq or fn == warm:
+                return x_cols.get(a, 0) == 64 and (fn == xq or bank_is_free())
+            if fn == tp:
+                return (widen, a[0]) in issued and bank_is_free()
+            if fn == s1g:
+                b, h, g = a
+                return (aq, b) in issued and (xq, g, h) in issued and (g == 1 or bank_is_free())
+            if fn == s2h:
+                b, f, h = a
+                return (axq, b, h) in issued and (h == 1 or bank_is_free())
+            if fn == s2q:
+                return (axq, a[0], 1) in issued and bank_is_free()
+            if fn == axq:
+                return all((ax_copy, a[0], h) in issued for h in range(a[1], a[2]))
+            before = {scale: (tp,), aq: (scale,), ax_copy: (s1g,), o_copy: (s2h,), store: (o_copy,), q_copy: (s2q,), q_store: (q_copy,)}
+            if fn in before:
+                last = (1,) if fn in (ax_copy, o_copy) else ()
+                return before[fn] + tuple(v for v in a if isinstance(v, int)) + last in issued
+            return True
+
+        def issue(queues):
+            while any(queues):
+                moved = False
+                for q in queues:
+                    while q and ready(*q[0]):
+                        fn, a = q[0][0], q[0][1:]
+                        q.remove(q[0])
+                        fn(*a)
+                        moved = True
+                        if fn == xi:
+                            x_cols[a[1:3]] = x_cols.get(a[1:3], 0) + a[4] - a[3]
+                        elif fn == axq:
+                            for h in range(a[1], a[2]):
+                                issued.add((axq, a[0], h))
+                        else:
+                            issued.add((fn,) + tuple(v for v in a if isinstance(v, int)))
+                assert moved
+
+        load_adj(0, 1)
+        load_sc()
+        load_adj(1, 1)
+        load_adj(2, 2)
+        load_x(0, 0)
+        load_x(1, 0)
+        load_adj(4, 2)
+        load_x(0, 1)
+        load_x(1, 1)
+        nc.vector.memset(wsc[:].rearrange("p g n -> p (g n)").bitcast(I32), 0)
+        nc.vector.memset(one[:], 1.0)
+        load_w()
+        load_adj(6, 2)
+        make_identity(nc, ident[:])
+
+        A, B, C = 24, 16, 16
+        def S1(b):
+            return [(s1g, b, h, g) for h in range(2) for g in range(2)]
+
+        def S2(b, f):
+            return [(s2h, b, f, h) for h in range(2)]
+
+        pe = [(tp, b) for b in range(4)]
+        pe += [(warm, 0, 0)] * 0
+        pe += [(s1g, b, 0, g) for g in range(2) for b in range(3)]
+        pe += [(tp, 4)] + [(s1g, 3, 0, g) for g in range(2)]
+        pe += [(s1g, b, 1, g) for g in range(2) for b in range(4)]
+        pe += S1(4) + S2(0, 0) + S2(0, 1) + S2(1, 0) + [(tp, 5), (tp, 6), (tp, 7)] + S2(1, 1) + S2(2, 0) + S2(2, 1) + S1(5)
+        pe += S2(3, 0) + S2(3, 1) + S2(4, 0) + S1(6) + S2(4, 1) + S2(5, 0) + S1(7) + S2(5, 1) + S2(6, 0) + S2(6, 1) + S2(7, 0) + [(s2q, 7, 2), (s2q, 7, 3)]
+
+        v = [(widen, "V", 1), (widen, "V", 2), (scale, 0), (scale, 1), (aq, 0), (aq, 1), (scale, 2), (xq, 0, 0), (xi, "V", 1, 0, 0, A), (aq, 2), (xq, 1, 0)]
+        v += [(scale, 3), (xi, "V", 0, 1, 0, B), (aq, 3), (xq, 0, 1), (xi, "V", 1, 1, 0, C), (scale, 4), (xq, 1, 1), (aq, 4), (widen, "V", 5)]
+        v += [(widen, "V", 6), (axq, 0, 0, 2), (widen, "V", 7), (axq, 1, 0, 2), (ax_copy, "V", 4, 0), (axq, 2, 0, 2), (o_copy, "V", 0, 1), (scale, 5), (axq, 3, 0, 2), (aq, 5)]
+        v += [(scale, 6), (axq, 4, 0, 2), (aq, 6), (scale, 7), (o_copy, "V", 3, 0), (aq, 7), (axq, 5, 0, 2), (o_copy, "V", 4, 0), (ax_copy, "V", 6, 1), (o_copy, "V", 5, 0), (axq, 6, 0, 2), (ax_copy, "V", 7, 1), (axq, 7, 0, 1), (axq, 7, 1, 2), (o_copy, "V", 6, 1), (q_copy, "V", 7, 2)]
+
+        s = [(widen, "S", 0), (widen, "S", 3), (xi, "S", 0, 0, 0, 64), (xi, "S", 1, 0, A, 64), (widen, "S", 4), (xi, "S", 0, 1, B, 64), (xi, "S", 1, 1, C, 64)]
+        s += [(ax_copy, "S", 0, 0), (ax_copy, "S", 1, 0), (ax_copy, "S", 2, 0), (ax_copy, "S", 0, 1), (ax_copy, "S", 1, 1), (ax_copy, "S", 3, 0), (ax_copy, "S", 2, 1), (ax_copy, "S", 3, 1)]
+        s += [(ax_copy, "S", 4, 1), (o_copy, "S", 0, 0), (o_copy, "S", 1, 0), (o_copy, "S", 1, 1), (o_copy, "S", 2, 0), (o_copy, "S", 2, 1)]
+        s += [(ax_copy, "S", 5, 0), (ax_copy, "S", 5, 1), (o_copy, "S", 3, 1), (ax_copy, "S", 6, 0), (o_copy, "S", 4, 1), (ax_copy, "S", 7, 0), (o_copy, "S", 5, 1), (o_copy, "S", 6, 0), (o_copy, "S", 7, 0), (q_copy, "S", 7, 3)]
+        sp = [(store, b, f) for b in range(NB) for f in range(2)][:-1] + [(q_store, 7, 2), (q_store, 7, 3)]
+        issue([pe, v, s, sp])

@@ -237,17 +237,19 @@ def tile_graphconvolution_pb_w4_kernel(tc, adj_bytes, adj_scale, x, weight_words
         def q_store(b, z):
             nc.sync.dma_start(out=rows[b][:, 256 * z : 256 * z + 256], in_=o_sb[b, "q", z][:])
 
-        def warm(g, h):
-            acc = take_bank(("warm", len(held)), [P, 512])
-            nc.tensor.matmul(acc[:], lhsT=xg[g, h][:, 0:P], rhs=xg[g, h][:, 0:512], start=True, stop=True)
-            give_bank(held[-1])
+        def warm(b, n):
+            acc = psum.tile([P, 512], F32, name="bank%d" % (len(held) % 8))
+            for i in range(n):
+                nc.tensor.matmul(acc[:], lhsT=grouped[b][:, 0:P], rhs=grouped[b][:, 0:512], start=True, stop=True)
 
         issued = set()
         x_cols = {}
 
         def ready(fn, *a):
-            if fn == xq or fn == warm:
-                return x_cols.get(a, 0) == 64 and (fn == xq or bank_is_free())
+            if fn == xq:
+                return x_cols.get(a, 0) == 64
+            if fn == warm:
+                return (scale, a[0]) in issued and bank_is_free()
             if fn == tp:
                 return (widen, a[0]) in issued and bank_is_free()
             if fn == s1g:
@@ -307,21 +309,20 @@ def tile_graphconvolution_pb_w4_kernel(tc, adj_bytes, adj_scale, x, weight_words
             return [(s2h, b, f, h) for h in range(2)]
 
         pe = [(tp, b) for b in range(4)]
-        pe += [(warm, 0, 0)] * 0
-        pe += [(s1g, b, 0, g) for g in range(2) for b in range(3)]
-        pe += [(tp, 4)] + [(s1g, 3, 0, g) for g in range(2)]
-        pe += [(s1g, b, 1, g) for g in range(2) for b in range(4)]
-        pe += S1(4) + S2(0, 0) + S2(0, 1) + S2(1, 0) + [(tp, 5), (tp, 6), (tp, 7)] + S2(1, 1) + S2(2, 0) + S2(2, 1) + S1(5)
+        pe += [(warm, 1, 4)]
+        pe += [(s1g, b, 0, 0) for b in range(3)] + [(s1g, b, 0, 1) for b in range(3)]
+        pe += [(s1g, b, 1, 0) for b in range(3)] + [(s1g, 3, 0, 0), (s1g, 3, 0, 1), (s1g, 3, 1, 0)] + [(s1g, b, 1, 1) for b in range(4)]
+        pe += [(tp, 4), (tp, 5)] + S2(0, 0) + S2(0, 1) + S2(1, 0) + S2(1, 1) + S1(4) + S2(2, 0) + [(tp, 6), (tp, 7)] + S2(2, 1) + S1(5)
         pe += S2(3, 0) + S2(3, 1) + S2(4, 0) + S1(6) + S2(4, 1) + S2(5, 0) + S1(7) + S2(5, 1) + S2(6, 0) + S2(6, 1) + S2(7, 0) + [(s2q, 7, 2), (s2q, 7, 3)]
 
-        v = [(widen, "V", 1), (widen, "V", 2), (scale, 0), (scale, 1), (aq, 0), (aq, 1), (scale, 2), (xq, 0, 0), (xi, "V", 1, 0, 0, A), (aq, 2), (xq, 1, 0)]
-        v += [(scale, 3), (xi, "V", 0, 1, 0, B), (aq, 3), (xq, 0, 1), (xi, "V", 1, 1, 0, C), (scale, 4), (xq, 1, 1), (aq, 4), (widen, "V", 5)]
-        v += [(widen, "V", 6), (axq, 0, 0, 2), (widen, "V", 7), (axq, 1, 0, 2), (ax_copy, "V", 4, 0), (axq, 2, 0, 2), (o_copy, "V", 0, 1), (scale, 5), (axq, 3, 0, 2), (aq, 5)]
-        v += [(scale, 6), (axq, 4, 0, 2), (aq, 6), (scale, 7), (o_copy, "V", 3, 0), (aq, 7), (axq, 5, 0, 2), (o_copy, "V", 4, 0), (ax_copy, "V", 6, 1), (o_copy, "V", 5, 0), (axq, 6, 0, 2), (ax_copy, "V", 7, 1), (axq, 7, 0, 1), (axq, 7, 1, 2), (o_copy, "V", 6, 1), (q_copy, "V", 7, 2)]
+        v = [(widen, "V", 0), (widen, "V", 2), (scale, 0), (scale, 1), (aq, 0), (aq, 1), (scale, 2), (xq, 0, 0), (xi, "V", 1, 0, 0, A), (aq, 2), (xq, 1, 0)]
+        v += [(xi, "V", 0, 1, 0, B), (scale, 3), (xq, 0, 1), (aq, 3), (xi, "V", 1, 1, 0, C), (widen, "V", 4), (xq, 1, 1), (widen, "V", 5)]
+        v += [(axq, 0, 0, 1), (axq, 1, 0, 1), (widen, "V", 6), (axq, 0, 1, 2), (axq, 1, 1, 2), (scale, 4), (widen, "V", 7), (aq, 4), (axq, 2, 0, 2), (scale, 5), (axq, 3, 0, 2), (aq, 5)]
+        v += [(o_copy, "V", 1, 1), (scale, 6), (axq, 4, 0, 2), (aq, 6), (scale, 7), (o_copy, "V", 3, 0), (aq, 7), (axq, 5, 0, 2), (o_copy, "V", 4, 0), (ax_copy, "V", 6, 1), (o_copy, "V", 5, 0), (axq, 6, 0, 2), (ax_copy, "V", 7, 1), (axq, 7, 0, 1), (axq, 7, 1, 2), (o_copy, "V", 6, 1), (q_copy, "V", 7, 2)]
 
-        s = [(widen, "S", 0), (widen, "S", 3), (xi, "S", 0, 0, 0, 64), (xi, "S", 1, 0, A, 64), (widen, "S", 4), (xi, "S", 0, 1, B, 64), (xi, "S", 1, 1, C, 64)]
-        s += [(ax_copy, "S", 0, 0), (ax_copy, "S", 1, 0), (ax_copy, "S", 2, 0), (ax_copy, "S", 0, 1), (ax_copy, "S", 1, 1), (ax_copy, "S", 3, 0), (ax_copy, "S", 2, 1), (ax_copy, "S", 3, 1)]
-        s += [(ax_copy, "S", 4, 1), (o_copy, "S", 0, 0), (o_copy, "S", 1, 0), (o_copy, "S", 1, 1), (o_copy, "S", 2, 0), (o_copy, "S", 2, 1)]
+        s = [(widen, "S", 1), (widen, "S", 3), (xi, "S", 0, 0, 0, 64), (xi, "S", 1, 0, A, 64), (xi, "S", 0, 1, B, 64), (xi, "S", 1, 1, C, 64)]
+        s += [(ax_copy, "S", 0, 0), (ax_copy, "S", 1, 0), (ax_copy, "S", 2, 0), (ax_copy, "S", 0, 1), (ax_copy, "S", 1, 1), (ax_copy, "S", 2, 1), (ax_copy, "S", 3, 0), (ax_copy, "S", 3, 1)]
+        s += [(o_copy, "S", 0, 0), (o_copy, "S", 0, 1), (o_copy, "S", 1, 0), (ax_copy, "S", 4, 0), (ax_copy, "S", 4, 1), (o_copy, "S", 2, 0), (o_copy, "S", 2, 1)]
         s += [(ax_copy, "S", 5, 0), (ax_copy, "S", 5, 1), (o_copy, "S", 3, 1), (ax_copy, "S", 6, 0), (o_copy, "S", 4, 1), (ax_copy, "S", 7, 0), (o_copy, "S", 5, 1), (o_copy, "S", 6, 0), (o_copy, "S", 7, 0), (q_copy, "S", 7, 3)]
         sp = [(store, b, f) for b in range(NB) for f in range(2)][:-1] + [(q_store, 7, 2), (q_store, 7, 3)]
         issue([pe, v, s, sp])

@@ -80,18 +80,41 @@ def tile_graphconvolution_pb_w4_kernel(tc, adj_bytes, adj_scale, x, weight_words
 
         ident = keep.tile([P, P], F32)
         one = keep.tile([P, 1], F32)
+        ident16 = keep.tile([P, P], BF16, align_bytes=64)
 
         xcodes = keep.tile([P, 2, 2, 512], U32, align_bytes=64)
         xscales = keep.tile([P, 2, 2, 512], U8, align_bytes=64)
         xg = {}
 
-        def xi(eng, g, h, lo, hi):
+        def x_grouped(g, h):
             if (g, h) not in xg:
-                t = keep.tile([P, 2048], BF16, name="xg%d%d" % (g, h), align_bytes=64)
-                xg[g, h] = t
+                xg[g, h] = keep.tile([P, 2048], BF16, name="xg%d%d" % (g, h), align_bytes=64)
+            return xg[g, h]
+
+        def xi(eng, g, h, lo, hi):
             src = xraw[g, h][:].rearrange("p t (m i a) -> p m a i t", i=2, a=4)[:, lo:hi]
-            dst = xg[g, h][:].rearrange("p (a m i t) -> p m a i t", a=4, i=2, t=4)[:, lo:hi]
+            dst = x_grouped(g, h)[:].rearrange("p (a m i t) -> p m a i t", a=4, i=2, t=4)[:, lo:hi]
             copy(eng, dst, src)
+
+        x_ps = {}
+
+        def xp(g, h, j):
+            bank = take_bank(("x", g, h, j), [P, 512])
+            for c in range(2):
+                d0 = 256 * j + P * c
+                nc.tensor.matmul(
+                    bank[:].bitcast(BF16)[:, 512 * c : 512 * c + 512],
+                    lhsT=ident16[:],
+                    rhs=xraw[g, h][:, :, d0 : d0 + P].rearrange("p t d -> p d t"),
+                    start=True,
+                    stop=True,
+                )
+            x_ps[g, h, j] = bank
+
+        def xe(eng, g, h, j):
+            dst = x_grouped(g, h)[:].bitcast(F32).rearrange("p (a m z) -> p a m z", a=4, z=2)[:, :, 64 * j : 64 * j + 64, :]
+            copy(eng, dst, x_ps[g, h, j][:].rearrange("p (m a z) -> p a m z", a=4, z=2))
+            give_bank(("x", g, h, j))
 
         def xq(g, h):
             nc.vector.quantize_mx(out=xcodes[:, h, g, :].bitcast(FP8X4), scales=xscales[:, h, g, :], in_=xg[g, h][:])
@@ -250,6 +273,8 @@ def tile_graphconvolution_pb_w4_kernel(tc, adj_bytes, adj_scale, x, weight_words
                 return x_cols.get(a, 0) == 64
             if fn == warm:
                 return (scale, a[0]) in issued and bank_is_free()
+            if fn == xp:
+                return bank_is_free()
             if fn == tp:
                 return (widen, a[0]) in issued and bank_is_free()
             if fn == s1g:
@@ -262,7 +287,7 @@ def tile_graphconvolution_pb_w4_kernel(tc, adj_bytes, adj_scale, x, weight_words
                 return (axq, a[0], 1) in issued and bank_is_free()
             if fn == axq:
                 return all((ax_copy, a[0], h) in issued for h in range(a[1], a[2]))
-            before = {scale: (tp,), aq: (scale,), ax_copy: (s1g,), o_copy: (s2h,), store: (o_copy,), q_copy: (s2q,), q_store: (q_copy,)}
+            before = {xe: (xp,), scale: (tp,), aq: (scale,), ax_copy: (s1g,), o_copy: (s2h,), store: (o_copy,), q_copy: (s2q,), q_store: (q_copy,)}
             if fn in before:
                 last = (1,) if fn in (ax_copy, o_copy) else ()
                 return before[fn] + tuple(v for v in a if isinstance(v, int)) + last in issued
@@ -279,6 +304,8 @@ def tile_graphconvolution_pb_w4_kernel(tc, adj_bytes, adj_scale, x, weight_words
                         moved = True
                         if fn == xi:
                             x_cols[a[1:3]] = x_cols.get(a[1:3], 0) + a[4] - a[3]
+                        elif fn == xe:
+                            x_cols[a[1:3]] = x_cols.get(a[1:3], 0) + 32
                         elif fn == axq:
                             for h in range(a[1], a[2]):
                                 issued.add((axq, a[0], h))
@@ -287,42 +314,44 @@ def tile_graphconvolution_pb_w4_kernel(tc, adj_bytes, adj_scale, x, weight_words
                 assert moved
 
         load_adj(0, 1)
-        load_sc()
         load_adj(1, 1)
-        load_adj(2, 2)
+        load_adj(2, 1)
+        load_sc()
+        load_adj(3, 2)
         load_x(0, 0)
         load_x(1, 0)
-        load_adj(4, 2)
         load_x(0, 1)
         load_x(1, 1)
+        load_adj(5, 3)
         nc.vector.memset(wsc[:].rearrange("p g n -> p (g n)").bitcast(I32), 0)
         nc.vector.memset(one[:], 1.0)
         load_w()
-        load_adj(6, 2)
         make_identity(nc, ident[:])
+        nc.vector.tensor_copy(out=ident16[:], in_=ident[:])
 
-        A, B, C = 24, 16, 16
+        B, C = 16, 24
         def S1(b):
             return [(s1g, b, h, g) for h in range(2) for g in range(2)]
 
         def S2(b, f):
             return [(s2h, b, f, h) for h in range(2)]
 
-        pe = [(tp, b) for b in range(4)]
-        pe += [(warm, 1, 4)]
-        pe += [(s1g, b, 0, 0) for b in range(3)] + [(s1g, b, 0, 1) for b in range(3)]
-        pe += [(s1g, b, 1, 0) for b in range(3)] + [(s1g, 3, 0, 0), (s1g, 3, 0, 1), (s1g, 3, 1, 0)] + [(s1g, b, 1, 1) for b in range(4)]
-        pe += [(tp, 4), (tp, 5)] + S2(0, 0) + S2(0, 1) + S2(1, 0) + S2(1, 1) + S1(4) + S2(2, 0) + [(tp, 6), (tp, 7)] + S2(2, 1) + S1(5)
+        pe = [(tp, b) for b in range(3)] + [(xp, 0, 0, 1), (xp, 1, 0, 1), (xp, 0, 1, 1), (tp, 3)]
+
+        pe += [(s1g, b, 0, 0) for b in range(3)] + [(s1g, b, 0, 1) for b in range(3)] + [(tp, 4)]
+        pe += [(s1g, b, 1, g) for g in range(2) for b in range(3)] + S1(3)
+        pe += S1(4) + S2(0, 0) + S2(0, 1) + S2(1, 0) + [(tp, 5), (tp, 6), (tp, 7)] + S2(1, 1) + S2(2, 0) + S2(2, 1) + S1(5)
         pe += S2(3, 0) + S2(3, 1) + S2(4, 0) + S1(6) + S2(4, 1) + S2(5, 0) + S1(7) + S2(5, 1) + S2(6, 0) + S2(6, 1) + S2(7, 0) + [(s2q, 7, 2), (s2q, 7, 3)]
 
-        v = [(widen, "V", 0), (widen, "V", 2), (scale, 0), (scale, 1), (aq, 0), (aq, 1), (scale, 2), (xq, 0, 0), (xi, "V", 1, 0, 0, A), (aq, 2), (xq, 1, 0)]
-        v += [(xi, "V", 0, 1, 0, B), (scale, 3), (xq, 0, 1), (aq, 3), (xi, "V", 1, 1, 0, C), (widen, "V", 4), (xq, 1, 1), (widen, "V", 5)]
-        v += [(axq, 0, 0, 1), (axq, 1, 0, 1), (widen, "V", 6), (axq, 0, 1, 2), (axq, 1, 1, 2), (scale, 4), (widen, "V", 7), (aq, 4), (axq, 2, 0, 2), (scale, 5), (axq, 3, 0, 2), (aq, 5)]
-        v += [(o_copy, "V", 1, 1), (scale, 6), (axq, 4, 0, 2), (aq, 6), (scale, 7), (o_copy, "V", 3, 0), (aq, 7), (axq, 5, 0, 2), (o_copy, "V", 4, 0), (ax_copy, "V", 6, 1), (o_copy, "V", 5, 0), (axq, 6, 0, 2), (ax_copy, "V", 7, 1), (axq, 7, 0, 1), (axq, 7, 1, 2), (o_copy, "V", 6, 1), (q_copy, "V", 7, 2)]
+        v = [(widen, "V", 0), (widen, "V", 2), (widen, "V", 4), (scale, 0), (scale, 1), (aq, 0), (aq, 1), (scale, 2), (xi, "V", 0, 1, 0, B), (xq, 0, 0), (aq, 2), (xq, 1, 0)]
+        v += [(xi, "V", 1, 1, 0, C), (xq, 0, 1), (scale, 3), (xq, 1, 1), (aq, 3), (scale, 4), (axq, 0, 0, 1), (axq, 1, 0, 1), (aq, 4), (widen, "V", 5)]
+        v += [(axq, 0, 1, 2), (widen, "V", 6), (axq, 1, 1, 2), (widen, "V", 7)]
+        v += [(axq, 2, 0, 2), (ax_copy, "V", 4, 0), (o_copy, "V", 0, 1), (scale, 5), (axq, 3, 0, 2), (aq, 5)]
+        v += [(scale, 6), (scale, 7), (axq, 4, 0, 2), (aq, 6), (o_copy, "V", 3, 0), (aq, 7), (axq, 5, 0, 2), (o_copy, "V", 4, 0), (ax_copy, "V", 6, 1), (o_copy, "V", 5, 0), (axq, 6, 0, 2), (ax_copy, "V", 7, 1), (axq, 7, 0, 1), (axq, 7, 1, 2), (o_copy, "V", 6, 1), (q_copy, "V", 7, 2)]
 
-        s = [(widen, "S", 1), (widen, "S", 3), (xi, "S", 0, 0, 0, 64), (xi, "S", 1, 0, A, 64), (xi, "S", 0, 1, B, 64), (xi, "S", 1, 1, C, 64)]
-        s += [(ax_copy, "S", 0, 0), (ax_copy, "S", 1, 0), (ax_copy, "S", 2, 0), (ax_copy, "S", 0, 1), (ax_copy, "S", 1, 1), (ax_copy, "S", 2, 1), (ax_copy, "S", 3, 0), (ax_copy, "S", 3, 1)]
-        s += [(o_copy, "S", 0, 0), (o_copy, "S", 0, 1), (o_copy, "S", 1, 0), (ax_copy, "S", 4, 0), (ax_copy, "S", 4, 1), (o_copy, "S", 2, 0), (o_copy, "S", 2, 1)]
+        s = [(widen, "S", 1), (widen, "S", 3), (xi, "S", 0, 0, 0, 32), (xi, "S", 1, 0, 0, 32), (xe, "S", 0, 0, 1), (xe, "S", 1, 0, 1), (xi, "S", 0, 1, B, 32), (xe, "S", 0, 1, 1), (xi, "S", 1, 1, C, 64), (ax_copy, "S", 0, 0)]
+        s += [(ax_copy, "S", 1, 0), (ax_copy, "S", 2, 0), (ax_copy, "S", 0, 1), (ax_copy, "S", 1, 1), (ax_copy, "S", 2, 1), (ax_copy, "S", 3, 0), (ax_copy, "S", 3, 1)]
+        s += [(ax_copy, "S", 4, 1), (o_copy, "S", 0, 0), (o_copy, "S", 1, 0), (o_copy, "S", 1, 1), (o_copy, "S", 2, 0), (o_copy, "S", 2, 1)]
         s += [(ax_copy, "S", 5, 0), (ax_copy, "S", 5, 1), (o_copy, "S", 3, 1), (ax_copy, "S", 6, 0), (o_copy, "S", 4, 1), (ax_copy, "S", 7, 0), (o_copy, "S", 5, 1), (o_copy, "S", 6, 0), (o_copy, "S", 7, 0), (q_copy, "S", 7, 3)]
         sp = [(store, b, f) for b in range(NB) for f in range(2)][:-1] + [(q_store, 7, 2), (q_store, 7, 3)]
         issue([pe, v, s, sp])

@@ -103,9 +103,9 @@ def tile_graphconvolution_pb_w4_kernel(tc, adj_bytes, adj_scale, x, weight_words
             for c in range(2):
                 d0 = 256 * j + P * c
                 nc.tensor.matmul(
-                    bank[:].bitcast(BF16)[:, 512 * c : 512 * c + 512],
+                    bank[:].bitcast(BF16)[:, 512 * c : 512 * c + 512].rearrange("p (d t) -> p t d", t=4),
                     lhsT=ident16[:],
-                    rhs=xraw[g, h][:, :, d0 : d0 + P].rearrange("p t d -> p d t"),
+                    rhs=xraw[g, h][:, :, d0 : d0 + P],
                     start=True,
                     stop=True,
                 )

@@ -53,8 +53,8 @@ def tile_graphconvolution_pb_w4_kernel(tc, adj_bytes, adj_scale, x, weight_words
         wsc = keep.tile([P, 2, N], U8, align_bytes=64)
         w = keep.tile([P, 2, 2 * N], U8, align_bytes=64)
 
-        def load_sc():
-            nc.sync.dma_start(out=sc[:], in_=adj_scale.rearrange("o (g p c) -> p (o g) c", g=2, c=4))
+        def load_sc(queue):
+            queue.dma_start(out=sc[:], in_=adj_scale.rearrange("o (g p c) -> p (o g) c", g=2, c=4))
 
         def load_x(g, h):
             t = keep.tile([P, 4, 512], BF16, name="xraw%d%d" % (g, h), align_bytes=64)
@@ -80,6 +80,8 @@ def tile_graphconvolution_pb_w4_kernel(tc, adj_bytes, adj_scale, x, weight_words
 
         ident = keep.tile([P, P], F32)
         one = keep.tile([P, 1], F32)
+        ones = keep.tile([P, P], BF16, align_bytes=64)
+        nc.vector.memset(ones[:], 1.0)
         ident16 = keep.tile([P, P], BF16, align_bytes=64)
 
         xcodes = keep.tile([P, 2, 2, 512], U32, align_bytes=64)
@@ -98,23 +100,22 @@ def tile_graphconvolution_pb_w4_kernel(tc, adj_bytes, adj_scale, x, weight_words
 
         x_ps = {}
 
-        def xp(g, h, j):
-            bank = take_bank(("x", g, h, j), [P, 512])
-            for c in range(2):
-                d0 = 256 * j + P * c
+        def xp(g, h, first):
+            bank = take_bank(("x", g, h), [P, 512])
+            for c in range(first, 4):
                 nc.tensor.matmul(
-                    bank[:].bitcast(BF16)[:, 512 * c : 512 * c + 512].rearrange("p (d t) -> p t d", t=4),
+                    bank[:].bitcast(BF16)[:, 512 * (c - first) : 512 * (c - first + 1)].rearrange("p (d t) -> p t d", t=4),
                     lhsT=ident16[:],
-                    rhs=xraw[g, h][:, :, d0 : d0 + P],
+                    rhs=xraw[g, h][:, :, P * c : P * c + P],
                     start=True,
                     stop=True,
                 )
-            x_ps[g, h, j] = bank
+            x_ps[g, h] = bank
 
-        def xe(eng, g, h, j):
-            dst = x_grouped(g, h)[:].bitcast(F32).rearrange("p (a m z) -> p a m z", a=4, z=2)[:, :, 64 * j : 64 * j + 64, :]
-            copy(eng, dst, x_ps[g, h, j][:].rearrange("p (m a z) -> p a m z", a=4, z=2))
-            give_bank(("x", g, h, j))
+        def xe(eng, g, h, first):
+            dst = x_grouped(g, h)[:].bitcast(F32).rearrange("p (a m z) -> p a m z", a=4, z=2)[:, :, 32 * first :, :]
+            copy(eng, dst, x_ps[g, h][:, 0 : 256 * (4 - first)].rearrange("p (m a z) -> p a m z", a=4, z=2))
+            give_bank(("x", g, h))
 
         def xq(g, h):
             nc.vector.quantize_mx(out=xcodes[:, h, g, :].bitcast(FP8X4), scales=xscales[:, h, g, :], in_=xg[g, h][:])
@@ -260,10 +261,10 @@ def tile_graphconvolution_pb_w4_kernel(tc, adj_bytes, adj_scale, x, weight_words
         def q_store(b, z):
             nc.sync.dma_start(out=rows[b][:, 256 * z : 256 * z + 256], in_=o_sb[b, "q", z][:])
 
-        def warm(b, n):
-            acc = psum.tile([P, 512], F32, name="bank%d" % (len(held) % 8))
+        def warm(n):
+            acc = psum.tile([P, 4, P], F32, name="bank7")
             for i in range(n):
-                nc.tensor.matmul(acc[:], lhsT=grouped[b][:, 0:P], rhs=grouped[b][:, 0:512], start=True, stop=True)
+                nc.tensor.matmul(acc[:], lhsT=ones[:], rhs=ones[:].unsqueeze(1).to_broadcast([P, 4, P]), start=True, stop=True)
 
         issued = set()
         x_cols = {}
@@ -272,7 +273,7 @@ def tile_graphconvolution_pb_w4_kernel(tc, adj_bytes, adj_scale, x, weight_words
             if fn == xq:
                 return x_cols.get(a, 0) == 64
             if fn == warm:
-                return (scale, a[0]) in issued and bank_is_free()
+                return bank_is_free()
             if fn == xp:
                 return bank_is_free()
             if fn == tp:
@@ -305,7 +306,7 @@ def tile_graphconvolution_pb_w4_kernel(tc, adj_bytes, adj_scale, x, weight_words
                         if fn == xi:
                             x_cols[a[1:3]] = x_cols.get(a[1:3], 0) + a[4] - a[3]
                         elif fn == xe:
-                            x_cols[a[1:3]] = x_cols.get(a[1:3], 0) + 32
+                            x_cols[a[1:3]] = x_cols.get(a[1:3], 0) + 16 * (4 - a[3])
                         elif fn == axq:
                             for h in range(a[1], a[2]):
                                 issued.add((axq, a[0], h))
@@ -316,7 +317,7 @@ def tile_graphconvolution_pb_w4_kernel(tc, adj_bytes, adj_scale, x, weight_words
         load_adj(0, 1)
         load_adj(1, 1)
         load_adj(2, 1)
-        load_sc()
+        load_sc(nc.sync)
         load_adj(3, 2)
         load_x(0, 0)
         load_x(1, 0)
@@ -327,7 +328,7 @@ def tile_graphconvolution_pb_w4_kernel(tc, adj_bytes, adj_scale, x, weight_words
         nc.vector.memset(one[:], 1.0)
         load_w()
         make_identity(nc, ident[:])
-        nc.vector.tensor_copy(out=ident16[:], in_=ident[:])
+        make_identity(nc, ident16[:])
 
         B, C = 16, 24
         def S1(b):
@@ -336,8 +337,7 @@ def tile_graphconvolution_pb_w4_kernel(tc, adj_bytes, adj_scale, x, weight_words
         def S2(b, f):
             return [(s2h, b, f, h) for h in range(2)]
 
-        pe = [(tp, b) for b in range(3)] + [(xp, 0, 0, 1), (xp, 1, 0, 1), (xp, 0, 1, 1), (tp, 3)]
-
+        pe = [(warm, 4), (tp, 0), (tp, 2), (tp, 1), (xp, 0, 0, 2), (xp, 1, 0, 2), (xp, 0, 1, 2), (tp, 3)]
         pe += [(s1g, b, 0, 0) for b in range(3)] + [(s1g, b, 0, 1) for b in range(3)] + [(tp, 4)]
         pe += [(s1g, b, 1, g) for g in range(2) for b in range(3)] + S1(3)
         pe += S1(4) + S2(0, 0) + S2(0, 1) + S2(1, 0) + [(tp, 5), (tp, 6), (tp, 7)] + S2(1, 1) + S2(2, 0) + S2(2, 1) + S1(5)
@@ -349,7 +349,7 @@ def tile_graphconvolution_pb_w4_kernel(tc, adj_bytes, adj_scale, x, weight_words
         v += [(axq, 2, 0, 2), (ax_copy, "V", 4, 0), (o_copy, "V", 0, 1), (scale, 5), (axq, 3, 0, 2), (aq, 5)]
         v += [(scale, 6), (scale, 7), (axq, 4, 0, 2), (aq, 6), (o_copy, "V", 3, 0), (aq, 7), (axq, 5, 0, 2), (o_copy, "V", 4, 0), (ax_copy, "V", 6, 1), (o_copy, "V", 5, 0), (axq, 6, 0, 2), (ax_copy, "V", 7, 1), (axq, 7, 0, 1), (axq, 7, 1, 2), (o_copy, "V", 6, 1), (q_copy, "V", 7, 2)]
 
-        s = [(widen, "S", 1), (widen, "S", 3), (xi, "S", 0, 0, 0, 32), (xi, "S", 1, 0, 0, 32), (xe, "S", 0, 0, 1), (xe, "S", 1, 0, 1), (xi, "S", 0, 1, B, 32), (xe, "S", 0, 1, 1), (xi, "S", 1, 1, C, 64), (ax_copy, "S", 0, 0)]
+        s = [(widen, "S", 1), (widen, "S", 3), (xi, "S", 0, 0, 0, 32), (xi, "S", 1, 0, 0, 32), (xe, "S", 0, 0, 2), (xe, "S", 1, 0, 2), (xi, "S", 0, 1, B, 32), (xe, "S", 0, 1, 2), (xi, "S", 1, 1, C, 64), (ax_copy, "S", 0, 0)]
         s += [(ax_copy, "S", 1, 0), (ax_copy, "S", 2, 0), (ax_copy, "S", 0, 1), (ax_copy, "S", 1, 1), (ax_copy, "S", 2, 1), (ax_copy, "S", 3, 0), (ax_copy, "S", 3, 1)]
         s += [(ax_copy, "S", 4, 1), (o_copy, "S", 0, 0), (o_copy, "S", 1, 0), (o_copy, "S", 1, 1), (o_copy, "S", 2, 0), (o_copy, "S", 2, 1)]
         s += [(ax_copy, "S", 5, 0), (ax_copy, "S", 5, 1), (o_copy, "S", 3, 1), (ax_copy, "S", 6, 0), (o_copy, "S", 4, 1), (ax_copy, "S", 7, 0), (o_copy, "S", 5, 1), (o_copy, "S", 6, 0), (o_copy, "S", 7, 0), (q_copy, "S", 7, 3)]

@@ -15,343 +15,337 @@ MULT = mybir.AluOpType.mult
 
 P = 128
 N = 1024
-NB = 8
+HALF = 512
+BLOCKS = N // P
+LAST = BLOCKS - 1
+BANKS = 8
 FLOPS = 2 * 2 * N * N * N
+
+STRIPS = 64
+COPIED = STRIPS // 2
+V_STRIPS_01 = 16
+V_STRIPS_11 = 24
+EARLY = 3
+WARM_UPS = 4
 
 
 def tile_graphconvolution_pb_w4_kernel(tc, adj_bytes, adj_scale, x, weight_words, weight_scales, out):
     nc = tc.nc
     with ExitStack() as ctx:
         keep = ctx.enter_context(tc.tile_pool(name="keep", bufs=1))
-        rot = ctx.enter_context(tc.tile_pool(name="rot", bufs=8))
+        per_block = ctx.enter_context(tc.tile_pool(name="per_block", bufs=BLOCKS))
         psum = ctx.enter_context(tc.psum_pool(name="psum", bufs=1))
         ctx.enter_context(tc.manual_schedule())
 
-        def copy(eng, dst, src):
-            if eng == "V":
-                nc.vector.tensor_copy(out=dst, in_=src)
-            else:
-                nc.scalar.copy(dst, src)
+        def on_vector(dst, src):
+            nc.vector.tensor_copy(out=dst, in_=src)
 
-        held = []
+        def on_scalar(dst, src):
+            nc.scalar.copy(dst, src)
+
+        bank_order = []
         emptied = set()
 
-        def bank_is_free():
-            return len(held) < 8 or held[-8] in emptied
+        def bank_free(content):
+            i = bank_order.index(content)
+            return i < BANKS or bank_order[i - BANKS] in emptied
 
-        def take_bank(key, shape):
-            held.append(key)
-            return psum.tile(shape, F32, name="bank%d" % ((len(held) - 1) % 8))
+        def take_bank(content, shape):
+            return psum.tile(shape, F32, name="bank%d" % (bank_order.index(content) % BANKS))
 
-        def give_bank(key):
-            emptied.add(key)
-
-        sc = keep.tile([P, 2, 4], F32)
-        xraw = {}
-        adj8 = {}
-        rows = {}
-        wsc = keep.tile([P, 2, N], U8, align_bytes=64)
-        w = keep.tile([P, 2, 2 * N], U8, align_bytes=64)
-
-        def load_sc(queue):
-            queue.dma_start(out=sc[:], in_=adj_scale.rearrange("o (g p c) -> p (o g) c", g=2, c=4))
-
-        def load_x(g, h):
-            t = keep.tile([P, 4, 512], BF16, name="xraw%d%d" % (g, h), align_bytes=64)
-            nc.sync.dma_start(out=t[:], in_=x[512 * g : 512 * g + 512, 512 * h : 512 * h + 512].rearrange("(p t) d -> p t d", t=4))
-            xraw[g, h] = t
-
-        def load_adj(first, n):
-            t = keep.tile([P, n, N], U8, name="adjb%d" % first, align_bytes=64)
-            r = slice(P * first, P * (first + n))
-            nc.sync.dma_start(out=t[:], in_=adj_bytes[r, :].rearrange("(p k) j -> p k j", k=n))
-            o = out[r, :].rearrange("(p k) f -> p k f", k=n)
-            for i in range(n):
-                adj8[first + i] = t[:, i, :]
-                rows[first + i] = o[:, i, :]
-
-        def load_w():
-            for q in range(4):
-                nc.sync.dma_start(
-                    out=wsc[32 * q : 32 * q + 4, :, :].bitcast(I32),
-                    in_=weight_scales[:, 4 * q : 4 * q + 4, :].rearrange("g q n -> q g n").bitcast(I32),
-                )
-            nc.sync.dma_start(out=w[:].bitcast(I32), in_=weight_words.rearrange("g p n -> p g n").bitcast(I32))
-
+        col_scale = keep.tile([P, 2, 4], F32)
+        w_scales = keep.tile([P, 2, N], U8, align_bytes=64)
+        w_words = keep.tile([P, 2, 2 * N], U8, align_bytes=64)
         ident = keep.tile([P, P], F32)
         one = keep.tile([P, 1], F32)
         ones = keep.tile([P, P], BF16, align_bytes=64)
         nc.vector.memset(ones[:], 1.0)
         ident16 = keep.tile([P, P], BF16, align_bytes=64)
+        x_codes = keep.tile([P, 2, 2, HALF], U32, align_bytes=64)
+        x_scales = keep.tile([P, 2, 2, HALF], U8, align_bytes=64)
 
-        xcodes = keep.tile([P, 2, 2, 512], U32, align_bytes=64)
-        xscales = keep.tile([P, 2, 2, 512], U8, align_bytes=64)
-        xg = {}
+        x_rows, adj_rows, out_rows = {}, {}, {}
 
-        def x_grouped(g, h):
-            if (g, h) not in xg:
-                xg[g, h] = keep.tile([P, 2048], BF16, name="xg%d%d" % (g, h), align_bytes=64)
-            return xg[g, h]
+        def load_x(g, h):
+            tile = keep.tile([P, 4, HALF], BF16, name="x_rows%d%d" % (g, h), align_bytes=64)
+            quarter = x[HALF * g : HALF * (g + 1), HALF * h : HALF * (h + 1)]
+            nc.sync.dma_start(out=tile[:], in_=quarter.rearrange("(p t) d -> p t d", t=4))
+            x_rows[g, h] = tile
 
-        def xi(eng, g, h, lo, hi):
-            src = xraw[g, h][:].rearrange("p t (m i a) -> p m a i t", i=2, a=4)[:, lo:hi]
-            dst = x_grouped(g, h)[:].rearrange("p (a m i t) -> p m a i t", a=4, i=2, t=4)[:, lo:hi]
-            copy(eng, dst, src)
+        def load_adj(first, count):
+            tile = keep.tile([P, count, N], U8, name="adj_bytes%d" % first, align_bytes=64)
+            rows = slice(P * first, P * (first + count))
+            nc.sync.dma_start(out=tile[:], in_=adj_bytes[rows, :].rearrange("(p k) j -> p k j", k=count))
+            for k in range(count):
+                adj_rows[first + k] = tile[:, k, :]
+                out_rows[first + k] = out[rows, :].rearrange("(p k) f -> p k f", k=count)[:, k, :]
 
-        x_ps = {}
+        def load_weight():
+            for q in range(4):
+                nc.sync.dma_start(
+                    out=w_scales[32 * q : 32 * q + 4, :, :].bitcast(I32),
+                    in_=weight_scales[:, 4 * q : 4 * q + 4, :].rearrange("g q n -> q g n").bitcast(I32),
+                )
+            nc.sync.dma_start(out=w_words[:].bitcast(I32), in_=weight_words.rearrange("g p n -> p g n").bitcast(I32))
 
-        def xp(g, h, first):
-            bank = take_bank(("x", g, h), [P, 512])
-            for c in range(first, 4):
+        grouped_x, spread_x = {}, {}
+
+        def x_tile(g, h):
+            if (g, h) not in grouped_x:
+                grouped_x[g, h] = keep.tile([P, 4 * HALF], BF16, name="grouped_x%d%d" % (g, h), align_bytes=64)
+            return grouped_x[g, h]
+
+        def x_copy(copy, g, h, lo, hi):
+            src = x_rows[g, h][:].rearrange("p t (s i a) -> p s a i t", i=2, a=4)[:, lo:hi]
+            dst = x_tile(g, h)[:].rearrange("p (a s i t) -> p s a i t", a=4, i=2, t=4)[:, lo:hi]
+            copy(dst, src)
+
+        def x_spread(g, h):
+            bank = take_bank(("x", g, h), [P, HALF])
+            for c in range(2):
                 nc.tensor.matmul(
-                    bank[:].bitcast(BF16)[:, 512 * (c - first) : 512 * (c - first + 1)].rearrange("p (d t) -> p t d", t=4),
+                    bank[:].bitcast(BF16)[:, HALF * c : HALF * (c + 1)].rearrange("p (d t) -> p t d", t=4),
                     lhsT=ident16[:],
-                    rhs=xraw[g, h][:, :, P * c : P * c + P],
+                    rhs=x_rows[g, h][:, :, P * (2 + c) : P * (3 + c)],
                     start=True,
                     stop=True,
                 )
-            x_ps[g, h] = bank
+            spread_x[g, h] = bank
 
-        def xe(eng, g, h, first):
-            dst = x_grouped(g, h)[:].bitcast(F32).rearrange("p (a m z) -> p a m z", a=4, z=2)[:, :, 32 * first :, :]
-            copy(eng, dst, x_ps[g, h][:, 0 : 256 * (4 - first)].rearrange("p (m a z) -> p a m z", a=4, z=2))
-            give_bank(("x", g, h))
+        def x_collect(g, h):
+            dst = x_tile(g, h)[:].bitcast(F32).rearrange("p (a m z) -> p a m z", a=4, z=2)[:, :, P // 2 :, :]
+            on_scalar(dst, spread_x[g, h][:].rearrange("p (m a z) -> p a m z", a=4, z=2))
+            emptied.add(("x", g, h))
 
-        def xq(g, h):
-            nc.vector.quantize_mx(out=xcodes[:, h, g, :].bitcast(FP8X4), scales=xscales[:, h, g, :], in_=xg[g, h][:])
+        def x_quantise(g, h):
+            nc.vector.quantize_mx(out=x_codes[:, h, g, :].bitcast(FP8X4), scales=x_scales[:, h, g, :], in_=grouped_x[g, h][:])
 
-        wide, sorted_words, banks, grouped, acodes, ascales = {}, {}, {}, {}, {}, {}
+        word_sets, turned, grouped_adj, adj_codes, adj_scales = {}, {}, {}, {}, {}
 
-        def widen(eng, b):
-            wd = rot.tile([P, N], BF16, align_bytes=64)
-            src = adj8[b].bitcast(FP8)
-            if eng == "V":
-                nc.vector.tensor_scalar(
-                    out=wd[:].rearrange("q (u m e) -> q m u e", u=2, e=2),
-                    in0=src.rearrange("q (m u e) -> q m u e", u=2, e=2),
-                    scalar1=one[:],
-                    scalar2=None,
-                    op0=MULT,
-                )
-            else:
-                nc.scalar.copy(wd[:], src)
-            wide[b] = wd
-            sorted_words[b] = eng == "V"
+        def widen_sorted(b):
+            wide = per_block.tile([P, N], BF16, name="wide", align_bytes=64)
+            nc.vector.tensor_scalar(
+                out=wide[:].rearrange("r (u w e) -> r w u e", u=2, e=2),
+                in0=adj_rows[b].bitcast(FP8).rearrange("r (w u e) -> r w u e", u=2, e=2),
+                scalar1=one[:],
+                scalar2=None,
+                op0=MULT,
+            )
+            word_sets[b] = wide[:].bitcast(F32).rearrange("r (u g p) -> r u g p", u=2, g=2)
 
-        def tp(b):
-            bank = take_bank(("t", b), [P, 2, 2, P])
-            words = wide[b][:].bitcast(F32)
+        def widen_plain(b):
+            wide = per_block.tile([P, N], BF16, name="wide", align_bytes=64)
+            on_scalar(wide[:], adj_rows[b].bitcast(FP8))
+            word_sets[b] = wide[:].bitcast(F32).rearrange("r (g p u) -> r u g p", u=2, g=2)
+
+        def turn(b):
+            bank = take_bank(("adj", b), [P, 2, 2, P])
             for g in range(2):
                 for u in range(2):
-                    lo = 256 * g
-                    if sorted_words[b]:
-                        cols = slice(256 * u + 128 * g, 256 * u + 128 * g + 128)
-                    else:
-                        cols = slice(lo + u, lo + 256, 2)
-                    nc.tensor.transpose(bank[:, u, g, :], words[:, cols], ident[:])
-            banks[b] = bank
+                    nc.tensor.transpose(bank[:, u, g, :], word_sets[b][:, u, g, :], ident[:])
+            turned[b] = bank
 
-        def scale(b):
-            gr = rot.tile([P, N], BF16, align_bytes=64)
+        def scale_adj(b):
+            tile = per_block.tile([P, N], BF16, name="grouped_adj", align_bytes=64)
             nc.vector.tensor_tensor(
-                out=gr[:].rearrange("p (g r u e) -> p g r u e", g=2, u=2, e=2),
-                in0=banks[b][:].bitcast(BF16).rearrange("p u g (r e) -> p g r u e", e=2),
-                in1=sc[:].rearrange("p g (u e) -> p g u e", e=2).unsqueeze(2).to_broadcast([P, 2, P, 2, 2]),
+                out=tile[:].rearrange("p (g r u e) -> p g r u e", g=2, u=2, e=2),
+                in0=turned[b][:].bitcast(BF16).rearrange("p u g (r e) -> p g r u e", e=2),
+                in1=col_scale[:].rearrange("p g (u e) -> p g u e", e=2).unsqueeze(2).to_broadcast([P, 2, P, 2, 2]),
                 op=MULT,
             )
-            give_bank(("t", b))
-            grouped[b] = gr
+            emptied.add(("adj", b))
+            grouped_adj[b] = tile
 
-        def aq(b):
-            ac = rot.tile([P, 256], U32, align_bytes=64)
-            asc = rot.tile([P, 256], U8, align_bytes=64)
-            nc.vector.quantize_mx(out=ac[:].bitcast(FP8X4), scales=asc[:], in_=grouped[b][:])
-            acodes[b] = ac
-            ascales[b] = asc
+        def adj_quantise(b):
+            adj_codes[b] = per_block.tile([P, 2 * P], U32, name="adj_codes", align_bytes=64)
+            adj_scales[b] = per_block.tile([P, 2 * P], U8, name="adj_scales", align_bytes=64)
+            nc.vector.quantize_mx(out=adj_codes[b][:].bitcast(FP8X4), scales=adj_scales[b][:], in_=grouped_adj[b][:])
 
-        ax_ps, axg, axc, axs = {}, {}, {}, {}
+        ax_bank, grouped_ax, ax_codes, ax_scales = {}, {}, {}, {}
 
-        def s1g(b, h, g):
+        def stage1(blocks, h, g):
+            nodes = slice(P * g, P * (g + 1))
             if g == 0:
-                ax_ps[b, h] = take_bank(("a", b, h), [P, 4, P])
+                for b in blocks:
+                    ax_bank[b, h] = take_bank(("ax", b, h), [P, 4, P])
             for a in range(4):
-                cols = slice(P * a, P * a + P)
-                nc.tensor.matmul_mx(
-                    out=ax_ps[b, h][:, a, :],
-                    lhsT=xcodes[:, h, g, cols].bitcast(FP8X4),
-                    lhsT_scale=xscales[:, h, g, cols],
-                    rhs=acodes[b][:, P * g : P * g + P].bitcast(FP8X4),
-                    rhs_scale=ascales[b][:, P * g : P * g + P],
-                    start=(g == 0 and a == 0),
-                    stop=(g == 1 and a == 3),
-                )
+                group = slice(P * a, P * (a + 1))
+                for b in blocks:
+                    nc.tensor.matmul_mx(
+                        out=ax_bank[b, h][:, a, :],
+                        lhsT=x_codes[:, h, g, group].bitcast(FP8X4),
+                        lhsT_scale=x_scales[:, h, g, group],
+                        rhs=adj_codes[b][:, nodes].bitcast(FP8X4),
+                        rhs_scale=adj_scales[b][:, nodes],
+                        start=(g == 0 and a == 0),
+                        stop=(g == 1 and a == 3),
+                    )
 
-        def s1(b, h):
-            s1g(b, h, 0)
-            s1g(b, h, 1)
+        def ax_copy(copy, b, h):
+            if b not in grouped_ax:
+                grouped_ax[b] = per_block.tile([P, 2, HALF], BF16, name="grouped_ax", align_bytes=64)
+            copy(grouped_ax[b][:, h, :].rearrange("p (r a) -> p r a", a=4), ax_bank[b, h][:].rearrange("p a r -> p r a"))
+            emptied.add(("ax", b, h))
 
-        def ax_copy(eng, b, h):
-            if b not in axg:
-                axt = rot.tile([P, 2, 512], BF16, align_bytes=64)
-                axg[b] = axt
-            copy(eng, axg[b][:, h, :].rearrange("p (r a) -> p r a", a=4), ax_ps[b, h][:].rearrange("p a r -> p r a"))
-            give_bank(("a", b, h))
-
-        def axq(b, lo, hi):
-            if b not in axc:
-                cod = rot.tile([P, 256], U32, align_bytes=64)
-                sca = rot.tile([P, 256], U8, align_bytes=64)
-                axc[b] = cod
-                axs[b] = sca
-            cols = slice(P * lo, P * hi)
-            nc.vector.quantize_mx(out=axc[b][:, cols].bitcast(FP8X4), scales=axs[b][:, cols], in_=axg[b][:, lo:hi, :].rearrange("p h n -> p (h n)"))
-
-        o_ps, o_sb = {}, {}
-
-        def s2h(b, f, h):
-            if h == 0:
-                o_ps[b, f] = take_bank(("o", b, f), [P, 512])
-            cols = slice(P * h, P * h + P)
-            nc.tensor.matmul_mx(
-                out=o_ps[b, f][:],
-                lhsT=axc[b][:, cols].bitcast(FP8X4),
-                lhsT_scale=axs[b][:, cols],
-                rhs=w[:, h, 1024 * f : 1024 * f + 1024].bitcast(FP4X4),
-                rhs_scale=wsc[:, h, 512 * f : 512 * f + 512],
-                start=(h == 0),
-                stop=(h == 1),
+        def ax_quantise(b, lo, hi):
+            if b not in ax_codes:
+                ax_codes[b] = per_block.tile([P, 2 * P], U32, name="ax_codes", align_bytes=64)
+                ax_scales[b] = per_block.tile([P, 2 * P], U8, name="ax_scales", align_bytes=64)
+            nodes = slice(P * lo, P * hi)
+            nc.vector.quantize_mx(
+                out=ax_codes[b][:, nodes].bitcast(FP8X4),
+                scales=ax_scales[b][:, nodes],
+                in_=grouped_ax[b][:, lo:hi, :].rearrange("p h n -> p (h n)"),
             )
 
-        def s2(b, f):
-            s2h(b, f, 0)
-            s2h(b, f, 1)
+        out_bank, out_tile = {}, {}
 
-        def o_copy(eng, b, f):
-            ot = rot.tile([P, 512], F32, bufs=6)
-            copy(eng, ot[:], o_ps[b, f][:])
-            give_bank(("o", b, f))
-            o_sb[b, f] = ot
-
-        def store(b, f):
-            nc.sync.dma_start(out=rows[b][:, 512 * f : 512 * f + 512], in_=o_sb[b, f][:])
-
-        def s2q(b, z):
-            acc = take_bank(("q", b, z), [P, 256])
-            for c in range(2):
-                n0 = 256 * z + P * c
+        def stage2(b, lo, hi):
+            out_bank[b, lo] = take_bank(("out", b, lo), [P, hi - lo])
+            width = HALF if hi - lo == HALF else P
+            for first in range(lo, hi, width):
                 for h in range(2):
-                    cols = slice(P * h, P * h + P)
+                    nodes = slice(P * h, P * (h + 1))
                     nc.tensor.matmul_mx(
-                        out=acc[:, P * c : P * c + P],
-                        lhsT=axc[b][:, cols].bitcast(FP8X4),
-                        lhsT_scale=axs[b][:, cols],
-                        rhs=w[:, h, 2 * n0 : 2 * n0 + 2 * P].bitcast(FP4X4),
-                        rhs_scale=wsc[:, h, n0 : n0 + P],
+                        out=out_bank[b, lo][:, first - lo : first - lo + width],
+                        lhsT=ax_codes[b][:, nodes].bitcast(FP8X4),
+                        lhsT_scale=ax_scales[b][:, nodes],
+                        rhs=w_words[:, h, 2 * first : 2 * (first + width)].bitcast(FP4X4),
+                        rhs_scale=w_scales[:, h, first : first + width],
                         start=(h == 0),
                         stop=(h == 1),
                     )
-            o_ps[b, "q", z] = acc
 
-        def q_copy(eng, b, z):
-            oq = rot.tile([P, 256], F32, bufs=2)
-            copy(eng, oq[:], o_ps[b, "q", z][:])
-            give_bank(("q", b, z))
-            o_sb[b, "q", z] = oq
+        def out_copy(copy, b, lo, hi):
+            width = hi - lo
+            out_tile[b, lo] = per_block.tile([P, width], F32, name="out%d" % width, bufs=6 if width == HALF else 2)
+            copy(out_tile[b, lo][:], out_bank[b, lo][:])
+            emptied.add(("out", b, lo))
 
-        def q_store(b, z):
-            nc.sync.dma_start(out=rows[b][:, 256 * z : 256 * z + 256], in_=o_sb[b, "q", z][:])
+        def store(b, lo, hi):
+            nc.sync.dma_start(out=out_rows[b][:, lo:hi], in_=out_tile[b, lo][:])
 
-        def warm(n):
-            acc = psum.tile([P, 4, P], F32, name="bank7")
-            for i in range(n):
-                nc.tensor.matmul(acc[:], lhsT=ones[:], rhs=ones[:].unsqueeze(1).to_broadcast([P, 4, P]), start=True, stop=True)
+        def warm_up():
+            unread = psum.tile([P, 4, P], F32, name="bank%d" % (BANKS - 1))
+            for i in range(WARM_UPS):
+                nc.tensor.matmul(unread[:], lhsT=ones[:], rhs=ones[:].unsqueeze(1).to_broadcast([P, 4, P]), start=True, stop=True)
 
-        issued = set()
-        x_cols = {}
+        def results(fn, *args):
+            if fn in (widen_sorted, widen_plain):
+                return [("wide",) + args]
+            if fn == x_copy:
+                return [("strip", args[1], args[2], s) for s in range(args[3], args[4])]
+            if fn == x_collect:
+                return [("strip",) + args + (s,) for s in range(COPIED, STRIPS)]
+            if fn == stage1:
+                return [(stage1, b, args[1], args[2]) for b in args[0]]
+            if fn == ax_quantise:
+                return [(ax_quantise, args[0], h) for h in range(args[1], args[2])]
+            if fn in (ax_copy, out_copy):
+                return [(fn,) + args[1:]]
+            return [(fn,) + args]
 
-        def ready(fn, *a):
-            if fn == xq:
-                return x_cols.get(a, 0) == 64
-            if fn == warm:
-                return bank_is_free()
-            if fn == xp:
-                return bank_is_free()
-            if fn == tp:
-                return (widen, a[0]) in issued and bank_is_free()
-            if fn == s1g:
-                b, h, g = a
-                return (aq, b) in issued and (xq, g, h) in issued and (g == 1 or bank_is_free())
-            if fn == s2h:
-                b, f, h = a
-                return (axq, b, h) in issued and (h == 1 or bank_is_free())
-            if fn == s2q:
-                return (axq, a[0], 1) in issued and bank_is_free()
-            if fn == axq:
-                return all((ax_copy, a[0], h) in issued for h in range(a[1], a[2]))
-            before = {xe: (xp,), scale: (tp,), aq: (scale,), ax_copy: (s1g,), o_copy: (s2h,), store: (o_copy,), q_copy: (s2q,), q_store: (q_copy,)}
-            if fn in before:
-                last = (1,) if fn in (ax_copy, o_copy) else ()
-                return before[fn] + tuple(v for v in a if isinstance(v, int)) + last in issued
-            return True
+        def reads(fn, *args):
+            if fn == turn:
+                return [("wide",) + args]
+            if fn == x_quantise:
+                return [("strip",) + args + (s,) for s in range(STRIPS)]
+            if fn == stage1:
+                return [(x_quantise, args[2], args[1])] + [(adj_quantise, b) for b in args[0]]
+            if fn == ax_copy:
+                return [(stage1,) + args[1:] + (1,)]
+            if fn == ax_quantise:
+                return [(ax_copy, args[0], h) for h in range(args[1], args[2])]
+            if fn == stage2:
+                return [(ax_quantise, args[0], h) for h in range(2)]
+            if fn == out_copy:
+                return [(stage2,) + args[1:]]
+            source = {x_collect: x_spread, scale_adj: turn, adj_quantise: scale_adj, store: out_copy}
+            return [(source[fn],) + args] if fn in source else []
+
+        def banks_taken(fn, *args):
+            if fn == stage1 and args[2] == 0:
+                return [("ax", b, args[1]) for b in args[0]]
+            kind = {turn: "adj", x_spread: "x", stage2: "out"}
+            return [(kind[fn],) + args[:2]] if fn in kind else []
 
         def issue(queues):
+            done = set()
             while any(queues):
-                moved = False
-                for q in queues:
-                    while q and ready(*q[0]):
-                        fn, a = q[0][0], q[0][1:]
-                        q.remove(q[0])
-                        fn(*a)
-                        moved = True
-                        if fn == xi:
-                            x_cols[a[1:3]] = x_cols.get(a[1:3], 0) + a[4] - a[3]
-                        elif fn == xe:
-                            x_cols[a[1:3]] = x_cols.get(a[1:3], 0) + 16 * (4 - a[3])
-                        elif fn == axq:
-                            for h in range(a[1], a[2]):
-                                issued.add((axq, a[0], h))
-                        else:
-                            issued.add((fn,) + tuple(v for v in a if isinstance(v, int)))
-                assert moved
+                for queue in queues:
+                    while queue and all(r in done for r in reads(*queue[0])) and all(bank_free(c) for c in banks_taken(*queue[0])):
+                        step = queue[0]
+                        queue.remove(step)
+                        step[0](*step[1:])
+                        for r in results(*step):
+                            done.add(r)
 
-        load_adj(0, 1)
-        load_adj(1, 1)
-        load_adj(2, 1)
-        load_sc(nc.sync)
+        early = tuple(range(EARLY))
+
+        for b in early:
+            load_adj(b, 1)
         load_adj(3, 2)
+        nc.sync.dma_start(out=col_scale[:], in_=adj_scale.rearrange("o (g p t) -> p (o g) t", g=2, t=4))
         load_x(0, 0)
         load_x(1, 0)
         load_x(0, 1)
         load_x(1, 1)
         load_adj(5, 3)
-        nc.vector.memset(wsc[:].rearrange("p g n -> p (g n)").bitcast(I32), 0)
+        nc.vector.memset(w_scales[:].rearrange("p g n -> p (g n)").bitcast(I32), 0)
         nc.vector.memset(one[:], 1.0)
-        load_w()
+        load_weight()
         make_identity(nc, ident[:])
         make_identity(nc, ident16[:])
 
-        B, C = 16, 24
-        def S1(b):
-            return [(s1g, b, h, g) for h in range(2) for g in range(2)]
+        late = range(5, BLOCKS)
+        pieces = [(b, lo, lo + HALF) for b in range(BLOCKS) for lo in (0, HALF)][:-1]
+        pieces += [(LAST, HALF, HALF + 2 * P), (LAST, HALF + 2 * P, N)]
 
-        def S2(b, f):
-            return [(s2h, b, f, h) for h in range(2)]
+        def whole_stage1(b):
+            return [(stage1, (b,), h, g) for h in range(2) for g in range(2)]
 
-        pe = [(warm, 4), (tp, 0), (tp, 2), (tp, 1), (xp, 0, 0, 2), (xp, 1, 0, 2), (xp, 0, 1, 2), (tp, 3)]
-        pe += [(s1g, b, 0, 0) for b in range(3)] + [(s1g, b, 0, 1) for b in range(3)] + [(tp, 4)]
-        pe += [(s1g, b, 1, g) for g in range(2) for b in range(3)] + S1(3)
-        pe += S1(4) + S2(0, 0) + S2(0, 1) + S2(1, 0) + [(tp, 5), (tp, 6), (tp, 7)] + S2(1, 1) + S2(2, 0) + S2(2, 1) + S1(5)
-        pe += S2(3, 0) + S2(3, 1) + S2(4, 0) + S1(6) + S2(4, 1) + S2(5, 0) + S1(7) + S2(5, 1) + S2(6, 0) + S2(6, 1) + S2(7, 0) + [(s2q, 7, 2), (s2q, 7, 3)]
+        tensor = [(warm_up,), (turn, 0), (turn, 2), (turn, 1), (turn, 3)]
+        tensor += [(x_spread, 0, 0), (x_spread, 1, 0), (x_spread, 0, 1)]
+        tensor += [(stage1, (b,), 0, g) for g in range(2) for b in early] + [(turn, 4)]
+        tensor += [(stage1, (b,), 1, g) for g in range(2) for b in early]
+        tensor += whole_stage1(3) + whole_stage1(4)
+        between = [[(turn, b) for b in late]] + [whole_stage1(b) for b in late] + [[]]
+        first = 0
+        for count, other in zip((3, 3, 3, 2, 6), between):
+            tensor += [(stage2,) + piece for piece in pieces[first : first + count]] + other
+            first = first + count
 
-        v = [(widen, "V", 0), (widen, "V", 2), (widen, "V", 4), (scale, 0), (scale, 1), (aq, 0), (aq, 1), (scale, 2), (xi, "V", 0, 1, 0, B), (xq, 0, 0), (aq, 2), (xq, 1, 0)]
-        v += [(xi, "V", 1, 1, 0, C), (xq, 0, 1), (scale, 3), (xq, 1, 1), (aq, 3), (scale, 4), (axq, 0, 0, 1), (axq, 1, 0, 1), (aq, 4), (widen, "V", 5)]
-        v += [(axq, 0, 1, 2), (widen, "V", 6), (axq, 1, 1, 2), (widen, "V", 7)]
-        v += [(axq, 2, 0, 2), (ax_copy, "V", 4, 0), (o_copy, "V", 0, 1), (scale, 5), (axq, 3, 0, 2), (aq, 5)]
-        v += [(scale, 6), (scale, 7), (axq, 4, 0, 2), (aq, 6), (o_copy, "V", 3, 0), (aq, 7), (axq, 5, 0, 2), (o_copy, "V", 4, 0), (ax_copy, "V", 6, 1), (o_copy, "V", 5, 0), (axq, 6, 0, 2), (ax_copy, "V", 7, 1), (axq, 7, 0, 1), (axq, 7, 1, 2), (o_copy, "V", 6, 1), (q_copy, "V", 7, 2)]
+        for step in tensor:
+            bank_order.extend(banks_taken(*step))
+        bank_order.remove(("adj", 3))
+        bank_order.insert(bank_order.index(("x", 0, 1)) + 1, ("adj", 3))
 
-        s = [(widen, "S", 1), (widen, "S", 3), (xi, "S", 0, 0, 0, 32), (xi, "S", 1, 0, 0, 32), (xe, "S", 0, 0, 2), (xe, "S", 1, 0, 2), (xi, "S", 0, 1, B, 32), (xe, "S", 0, 1, 2), (xi, "S", 1, 1, C, 64), (ax_copy, "S", 0, 0)]
-        s += [(ax_copy, "S", 1, 0), (ax_copy, "S", 2, 0), (ax_copy, "S", 0, 1), (ax_copy, "S", 1, 1), (ax_copy, "S", 2, 1), (ax_copy, "S", 3, 0), (ax_copy, "S", 3, 1)]
-        s += [(ax_copy, "S", 4, 1), (o_copy, "S", 0, 0), (o_copy, "S", 1, 0), (o_copy, "S", 1, 1), (o_copy, "S", 2, 0), (o_copy, "S", 2, 1)]
-        s += [(ax_copy, "S", 5, 0), (ax_copy, "S", 5, 1), (o_copy, "S", 3, 1), (ax_copy, "S", 6, 0), (o_copy, "S", 4, 1), (ax_copy, "S", 7, 0), (o_copy, "S", 5, 1), (o_copy, "S", 6, 0), (o_copy, "S", 7, 0), (q_copy, "S", 7, 3)]
-        sp = [(store, b, f) for b in range(NB) for f in range(2)][:-1] + [(q_store, 7, 2), (q_store, 7, 3)]
-        issue([pe, v, s, sp])
+        filled = []
+        for step in tensor:
+            if step[0] == stage1 and step[3] == 1:
+                filled += [(ax_copy, b, step[2]) for b in step[1]]
+            if step[0] == stage2:
+                filled.append((out_copy,) + step[1:])
+        for_vector = [(ax_copy, 4, 0), (out_copy, 0, HALF, N)]
+        for_vector += [(out_copy, 3, 0, HALF), (out_copy, 4, 0, HALF), (ax_copy, 6, 1), (out_copy, 5, 0, HALF)]
+        for_vector += [(ax_copy, LAST, 1), (out_copy, 6, HALF, N), (out_copy,) + pieces[-2]]
+        v_empty = [(step[0], on_vector) + step[1:] for step in for_vector]
+
+        vector = [(widen_sorted, 0), (widen_sorted, 2), (widen_sorted, 3)]
+        vector += [(scale_adj, 0), (scale_adj, 1), (adj_quantise, 0), (adj_quantise, 1), (scale_adj, 2)]
+        vector += [(x_copy, on_vector, 0, 1, 0, V_STRIPS_01), (x_quantise, 0, 0), (adj_quantise, 2), (x_quantise, 1, 0)]
+        vector += [(x_copy, on_vector, 1, 1, 0, V_STRIPS_11), (x_quantise, 0, 1), (scale_adj, 3), (x_quantise, 1, 1)]
+        vector += [(adj_quantise, 3), (scale_adj, 4), (ax_quantise, 0, 0, 1), (ax_quantise, 1, 0, 1), (adj_quantise, 4)]
+        vector += [(widen_sorted, 5), (ax_quantise, 0, 1, 2), (widen_sorted, 6), (ax_quantise, 1, 1, 2), (widen_sorted, 7)]
+        vector += [(ax_quantise, 2, 0, 2), v_empty[0], v_empty[1], (scale_adj, 5), (ax_quantise, 3, 0, 2), (adj_quantise, 5)]
+        vector += [(scale_adj, 6), (scale_adj, 7), (ax_quantise, 4, 0, 2), (adj_quantise, 6), v_empty[2], (adj_quantise, 7)]
+        vector += [(ax_quantise, 5, 0, 2), v_empty[3], v_empty[4], v_empty[5], (ax_quantise, 6, 0, 2), v_empty[6]]
+        vector += [(ax_quantise, LAST, 0, 1), (ax_quantise, LAST, 1, 2), v_empty[7], v_empty[8]]
+
+        scalar = [(widen_plain, 1), (widen_plain, 4)]
+        scalar += [(x_copy, on_scalar, 0, 0, 0, COPIED), (x_copy, on_scalar, 1, 0, 0, COPIED), (x_collect, 0, 0), (x_collect, 1, 0)]
+        scalar += [(x_copy, on_scalar, 0, 1, V_STRIPS_01, COPIED), (x_collect, 0, 1), (x_copy, on_scalar, 1, 1, V_STRIPS_11, STRIPS)]
+        scalar += [(step[0], on_scalar) + step[1:] for step in filled if step not in for_vector]
+
+        stores = [(store,) + piece for piece in pieces]
+        issue([tensor, vector, scalar, stores])

@@ -24,9 +24,9 @@ FLOPS = 2 * 2 * N * N * N
 STRIPS = 64
 COPIED = STRIPS // 2
 V_STRIPS_01 = 16
-V_STRIPS_11 = 24
+V_STRIPS_11 = 20
 EARLY = 3
-WARM_UPS = 4
+WARM_UPS = 5
 
 
 def tile_graphconvolution_pb_w4_kernel(tc, adj_bytes, adj_scale, x, weight_words, weight_scales, out):

@@ -96,8 +96,8 @@ def tile_graphconvolution_pb_w4_kernel(tc, adj_bytes, adj_scale, x, weight_words
             return grouped_x[g, h]
 
         def x_copy(copy, g, h, lo, hi):
-            src = x_rows[g, h][:].rearrange("p t (s i a) -> p s a i t", i=2, a=4)[:, lo:hi]
-            dst = x_tile(g, h)[:].rearrange("p (a s i t) -> p s a i t", a=4, i=2, t=4)[:, lo:hi]
+            src = x_rows[g, h][:].rearrange("p t (s i a) -> p s a t i", i=2, a=4)[:, lo:hi]
+            dst = x_tile(g, h)[:].rearrange("p (a s i t) -> p s a t i", a=4, i=2, t=4)[:, lo:hi]
             copy(dst, src)
 
         def x_spread(g, h):

@@ -12,6 +12,7 @@ FP8 = mybir.dt.float8_e4m3fn
 FP8X4 = mybir.dt.float8_e4m3fn_x4
 FP4X4 = mybir.dt.float4_e2m1fn_x4
 MULT = mybir.AluOpType.mult
+ADD = mybir.AluOpType.add
 
 P = 128
 N = 1024
@@ -99,6 +100,11 @@ def tile_graphconvolution_pb_w4_kernel(tc, adj_bytes, adj_scale, x, weight_words
             src = x_rows[g, h][:].rearrange("p t (s i a) -> p s a t i", i=2, a=4)[:, lo:hi]
             dst = x_tile(g, h)[:].rearrange("p (a s i t) -> p s a t i", a=4, i=2, t=4)[:, lo:hi]
             copy(dst, src)
+
+        def x_pool(g, h, lo, hi):
+            src = x_rows[g, h][:].rearrange("p t (m a) -> p m a t", a=4)[:, 2 * lo : 2 * hi]
+            dst = x_tile(g, h)[:].rearrange("p (a m t) -> p m a t", a=4, t=4)[:, 2 * lo : 2 * hi]
+            nc.gpsimd.tensor_scalar(out=dst, in0=src, scalar1=1.0, scalar2=0.0, op0=MULT, op1=ADD)
 
         def x_spread(g, h):
             bank = take_bank(("x", g, h), [P, HALF])
@@ -225,9 +231,9 @@ def tile_graphconvolution_pb_w4_kernel(tc, adj_bytes, adj_scale, x, weight_words
         def store(b, lo, hi):
             nc.sync.dma_start(out=out_rows[b][:, lo:hi], in_=out_tile[b, lo][:])
 
-        def warm_up():
+        def warm_up(count):
             unread = psum.tile([P, 4, P], F32, name="bank%d" % (BANKS - 1))
-            for i in range(WARM_UPS):
+            for i in range(count):
                 nc.tensor.matmul(unread[:], lhsT=ones[:], rhs=ones[:].unsqueeze(1).to_broadcast([P, 4, P]), start=True, stop=True)
 
         def results(fn, *args):
@@ -235,6 +241,8 @@ def tile_graphconvolution_pb_w4_kernel(tc, adj_bytes, adj_scale, x, weight_words
                 return [("wide",) + args]
             if fn == x_copy:
                 return [("strip", args[1], args[2], s) for s in range(args[3], args[4])]
+            if fn == x_pool:
+                return [("strip", args[0], args[1], s) for s in range(args[2], args[3])]
             if fn == x_collect:
                 return [("strip",) + args + (s,) for s in range(COPIED, STRIPS)]
             if fn == stage1:
@@ -282,43 +290,45 @@ def tile_graphconvolution_pb_w4_kernel(tc, adj_bytes, adj_scale, x, weight_words
 
         early = tuple(range(EARLY))
 
-        for b in early:
+        for b in range(3):
             load_adj(b, 1)
-        load_adj(3, 2)
         nc.sync.dma_start(out=col_scale[:], in_=adj_scale.rearrange("o (g p t) -> p (o g) t", g=2, t=4))
+        load_adj(3, 2)
         load_x(0, 0)
         load_x(1, 0)
+        load_adj(5, 1)
         load_x(0, 1)
         load_x(1, 1)
-        load_adj(5, 3)
+        load_adj(6, 2)
         nc.vector.memset(w_scales[:].rearrange("p g n -> p (g n)").bitcast(I32), 0)
         nc.vector.memset(one[:], 1.0)
         load_weight()
         make_identity(nc, ident[:])
         make_identity(nc, ident16[:])
 
-        late = range(5, BLOCKS)
         pieces = [(b, lo, lo + HALF) for b in range(BLOCKS) for lo in (0, HALF)][:-1]
         pieces += [(LAST, HALF, HALF + 2 * P), (LAST, HALF + 2 * P, N)]
 
         def whole_stage1(b):
             return [(stage1, (b,), h, g) for h in range(2) for g in range(2)]
 
-        tensor = [(warm_up,), (turn, 0), (turn, 2), (turn, 1), (turn, 3)]
-        tensor += [(x_spread, 0, 0), (x_spread, 1, 0), (x_spread, 0, 1)]
-        tensor += [(stage1, (b,), 0, g) for g in range(2) for b in early] + [(turn, 4)]
-        tensor += [(stage1, (b,), 1, g) for g in range(2) for b in early]
-        tensor += whole_stage1(3) + whole_stage1(4)
-        between = [[(turn, b) for b in late]] + [whole_stage1(b) for b in late] + [[]]
+        tensor = [(warm_up, 5), (turn, 0), (turn, 2), (warm_up, 2), (turn, 1), (turn, 3), (warm_up, 1), (turn, 4)]
+        tensor += [(x_spread, 1, 0), (x_spread, 0, 1), (turn, 5)]
+        tensor += [(stage1, (b,), 0, g) for g in range(2) for b in (0, 2)]
+        tensor += [(stage1, (b,), 0, g) for b in (1, 3) for g in range(2)]
+        tensor += [(stage1, (b,), 1, g) for g in range(2) for b in (0, 2, 1, 3)]
+        tensor += whole_stage1(4)
+        between = [[(turn, 6), (turn, 7)]] + [whole_stage1(b) for b in (5, 6, 7)] + [[]]
         first = 0
-        for count, other in zip((3, 3, 3, 2, 6), between):
+        for count, other in zip((2, 3, 3, 3, 6), between):
             tensor += [(stage2,) + piece for piece in pieces[first : first + count]] + other
             first = first + count
 
         for step in tensor:
             bank_order.extend(banks_taken(*step))
-        bank_order.remove(("adj", 3))
-        bank_order.insert(bank_order.index(("x", 0, 1)) + 1, ("adj", 3))
+        for content, after in ((("adj", 4), ("x", 0, 1)), (("adj", 5), ("ax", 3, 0))):
+            bank_order.remove(content)
+            bank_order.insert(bank_order.index(after) + 1, content)
 
         filled = []
         for step in tensor:
@@ -326,26 +336,25 @@ def tile_graphconvolution_pb_w4_kernel(tc, adj_bytes, adj_scale, x, weight_words
                 filled += [(ax_copy, b, step[2]) for b in step[1]]
             if step[0] == stage2:
                 filled.append((out_copy,) + step[1:])
-        for_vector = [(ax_copy, 4, 0), (out_copy, 0, HALF, N)]
+        for_vector = [(ax_copy, 4, 0), (out_copy, 1, 0, HALF)]
         for_vector += [(out_copy, 3, 0, HALF), (out_copy, 4, 0, HALF), (ax_copy, 6, 1), (out_copy, 5, 0, HALF)]
         for_vector += [(ax_copy, LAST, 1), (out_copy, 6, HALF, N), (out_copy,) + pieces[-2]]
         v_empty = [(step[0], on_vector) + step[1:] for step in for_vector]
 
-        vector = [(widen_sorted, 0), (widen_sorted, 2), (widen_sorted, 3)]
-        vector += [(scale_adj, 0), (scale_adj, 1), (adj_quantise, 0), (adj_quantise, 1), (scale_adj, 2)]
-        vector += [(x_copy, on_vector, 0, 1, 0, V_STRIPS_01), (x_quantise, 0, 0), (adj_quantise, 2), (x_quantise, 1, 0)]
-        vector += [(x_copy, on_vector, 1, 1, 0, V_STRIPS_11), (x_quantise, 0, 1), (scale_adj, 3), (x_quantise, 1, 1)]
-        vector += [(adj_quantise, 3), (scale_adj, 4), (ax_quantise, 0, 0, 1), (ax_quantise, 1, 0, 1), (adj_quantise, 4)]
-        vector += [(widen_sorted, 5), (ax_quantise, 0, 1, 2), (widen_sorted, 6), (ax_quantise, 1, 1, 2), (widen_sorted, 7)]
-        vector += [(ax_quantise, 2, 0, 2), v_empty[0], v_empty[1], (scale_adj, 5), (ax_quantise, 3, 0, 2), (adj_quantise, 5)]
+        vector = [(widen_sorted, 0), (widen_sorted, 2)]
+        vector += [(scale_adj, 0), (scale_adj, 2), (scale_adj, 1), (scale_adj, 3)]
+        vector += [(x_quantise, 0, 0), (adj_quantise, 0), (adj_quantise, 2), (x_quantise, 1, 0), (adj_quantise, 1), (adj_quantise, 3)]
+        vector += [(x_copy, on_vector, 1, 1, 0, V_STRIPS_11), (x_quantise, 0, 1), (scale_adj, 4), (x_quantise, 1, 1)]
+        vector += [(adj_quantise, 4), (widen_sorted, 6), (ax_quantise, 0, 0, 1), (widen_sorted, 7), (scale_adj, 5), (ax_quantise, 0, 1, 2)]
+        vector += [(ax_quantise, 2, 0, 2), (adj_quantise, 5), (ax_quantise, 1, 0, 2), v_empty[0], (ax_quantise, 3, 0, 2), v_empty[1]]
         vector += [(scale_adj, 6), (scale_adj, 7), (ax_quantise, 4, 0, 2), (adj_quantise, 6), v_empty[2], (adj_quantise, 7)]
         vector += [(ax_quantise, 5, 0, 2), v_empty[3], v_empty[4], v_empty[5], (ax_quantise, 6, 0, 2), v_empty[6]]
         vector += [(ax_quantise, LAST, 0, 1), (ax_quantise, LAST, 1, 2), v_empty[7], v_empty[8]]
 
-        scalar = [(widen_plain, 1), (widen_plain, 4)]
-        scalar += [(x_copy, on_scalar, 0, 0, 0, COPIED), (x_copy, on_scalar, 1, 0, 0, COPIED), (x_collect, 0, 0), (x_collect, 1, 0)]
-        scalar += [(x_copy, on_scalar, 0, 1, V_STRIPS_01, COPIED), (x_collect, 0, 1), (x_copy, on_scalar, 1, 1, V_STRIPS_11, STRIPS)]
+        scalar = [(widen_plain, 1), (widen_plain, 3), (widen_plain, 4)]
+        scalar += [(x_copy, on_scalar, 1, 0, 0, COPIED), (widen_plain, 5), (x_collect, 1, 0)]
+        scalar += [(x_copy, on_scalar, 0, 1, 0, COPIED), (x_collect, 0, 1), (x_copy, on_scalar, 1, 1, V_STRIPS_11, STRIPS)]
         scalar += [(step[0], on_scalar) + step[1:] for step in filled if step not in for_vector]
 
         stores = [(store,) + piece for piece in pieces]
-        issue([tensor, vector, scalar, stores])
+        issue([tensor, vector, scalar, [(x_pool, 0, 0, 0, STRIPS)], stores])

@@ -26,6 +26,7 @@ STRIPS = 64
 COPIED = STRIPS // 2
 V_STRIPS_01 = 16
 V_STRIPS_11 = 20
+G_STRIPS = 48
 EARLY = 3
 WARM_UPS = 5
 
@@ -44,15 +45,17 @@ def tile_graphconvolution_pb_w4_kernel(tc, adj_bytes, adj_scale, x, weight_words
         def on_scalar(dst, src):
             nc.scalar.copy(dst, src)
 
-        bank_order = []
+        taken, freed, bank_of = [], [], {}
         emptied = set()
 
         def bank_free(content):
-            i = bank_order.index(content)
-            return i < BANKS or bank_order[i - BANKS] in emptied
+            n = taken.index(content)
+            return n < BANKS or freed[n - BANKS] in emptied
 
         def take_bank(content, shape):
-            return psum.tile(shape, F32, name="bank%d" % (bank_order.index(content) % BANKS))
+            n = taken.index(content)
+            bank_of[content] = n if n < BANKS else bank_of[freed[n - BANKS]]
+            return psum.tile(shape, F32, name="bank%d" % bank_of[content])
 
         col_scale = keep.tile([P, 2, 4], F32)
         w_scales = keep.tile([P, 2, N], U8, align_bytes=64)
@@ -224,7 +227,7 @@ def tile_graphconvolution_pb_w4_kernel(tc, adj_bytes, adj_scale, x, weight_words
 
         def out_copy(copy, b, lo, hi):
             width = hi - lo
-            out_tile[b, lo] = per_block.tile([P, width], F32, name="out%d" % width, bufs=6 if width == HALF else 2)
+            out_tile[b, lo] = per_block.tile([P, width], F32, name="out%d" % width, bufs=8 if width == HALF else 2)
             copy(out_tile[b, lo][:], out_bank[b, lo][:])
             emptied.add(("out", b, lo))
 
@@ -290,13 +293,14 @@ def tile_graphconvolution_pb_w4_kernel(tc, adj_bytes, adj_scale, x, weight_words
 
         early = tuple(range(EARLY))
 
-        for b in range(3):
-            load_adj(b, 1)
+        load_adj(0, 1)
+        load_adj(1, 1)
+        load_adj(2, 2)
         nc.sync.dma_start(out=col_scale[:], in_=adj_scale.rearrange("o (g p t) -> p (o g) t", g=2, t=4))
-        load_adj(3, 2)
+        load_adj(4, 1)
         load_x(0, 0)
-        load_x(1, 0)
         load_adj(5, 1)
+        load_x(1, 0)
         load_x(0, 1)
         load_x(1, 1)
         load_adj(6, 2)
@@ -312,11 +316,10 @@ def tile_graphconvolution_pb_w4_kernel(tc, adj_bytes, adj_scale, x, weight_words
         def whole_stage1(b):
             return [(stage1, (b,), h, g) for h in range(2) for g in range(2)]
 
-        tensor = [(warm_up, 5), (turn, 0), (turn, 2), (warm_up, 2), (turn, 1), (turn, 3), (warm_up, 1), (turn, 4)]
-        tensor += [(x_spread, 1, 0), (x_spread, 0, 1), (turn, 5)]
-        tensor += [(stage1, (b,), 0, g) for g in range(2) for b in (0, 2)]
-        tensor += [(stage1, (b,), 0, g) for b in (1, 3) for g in range(2)]
-        tensor += [(stage1, (b,), 1, g) for g in range(2) for b in (0, 2, 1, 3)]
+        tensor = [(warm_up, 5), (turn, 0), (warm_up, 1), (turn, 1), (turn, 3), (turn, 2), (warm_up, 2), (turn, 4)]
+        tensor += [(x_spread, 1, 0), (turn, 5), (x_spread, 0, 1)]
+        tensor += [(stage1, (b,), 0, g) for g in range(2) for b in range(4)]
+        tensor += [(stage1, (b,), 1, g) for g in range(2) for b in range(4)]
         tensor += whole_stage1(4)
         between = [[(turn, 6), (turn, 7)]] + [whole_stage1(b) for b in (5, 6, 7)] + [[]]
         first = 0
@@ -325,10 +328,11 @@ def tile_graphconvolution_pb_w4_kernel(tc, adj_bytes, adj_scale, x, weight_words
             first = first + count
 
         for step in tensor:
-            bank_order.extend(banks_taken(*step))
+            taken.extend(banks_taken(*step))
+        freed.extend(taken)
         for content, after in ((("adj", 4), ("x", 0, 1)), (("adj", 5), ("ax", 3, 0))):
-            bank_order.remove(content)
-            bank_order.insert(bank_order.index(after) + 1, content)
+            freed.remove(content)
+            freed.insert(freed.index(after) + 1, content)
 
         filled = []
         for step in tensor:
@@ -341,20 +345,20 @@ def tile_graphconvolution_pb_w4_kernel(tc, adj_bytes, adj_scale, x, weight_words
         for_vector += [(ax_copy, LAST, 1), (out_copy, 6, HALF, N), (out_copy,) + pieces[-2]]
         v_empty = [(step[0], on_vector) + step[1:] for step in for_vector]
 
-        vector = [(widen_sorted, 0), (widen_sorted, 2)]
-        vector += [(scale_adj, 0), (scale_adj, 2), (scale_adj, 1), (scale_adj, 3)]
-        vector += [(x_quantise, 0, 0), (adj_quantise, 0), (adj_quantise, 2), (x_quantise, 1, 0), (adj_quantise, 1), (adj_quantise, 3)]
+        vector = [(widen_sorted, 0), (widen_sorted, 1), (widen_sorted, 3)]
+        vector += [(scale_adj, 0), (scale_adj, 1), (scale_adj, 3), (scale_adj, 2)]
+        vector += [(adj_quantise, 0), (adj_quantise, 1), (x_quantise, 0, 0), (adj_quantise, 2), (adj_quantise, 3), (x_quantise, 1, 0)]
         vector += [(x_copy, on_vector, 1, 1, 0, V_STRIPS_11), (x_quantise, 0, 1), (scale_adj, 4), (x_quantise, 1, 1)]
         vector += [(adj_quantise, 4), (widen_sorted, 6), (ax_quantise, 0, 0, 1), (widen_sorted, 7), (scale_adj, 5), (ax_quantise, 0, 1, 2)]
-        vector += [(ax_quantise, 2, 0, 2), (adj_quantise, 5), (ax_quantise, 1, 0, 2), v_empty[0], (ax_quantise, 3, 0, 2), v_empty[1]]
+        vector += [(ax_quantise, 1, 0, 2), (adj_quantise, 5), (ax_quantise, 2, 0, 2), v_empty[0], (ax_quantise, 3, 0, 2), v_empty[1]]
         vector += [(scale_adj, 6), (scale_adj, 7), (ax_quantise, 4, 0, 2), (adj_quantise, 6), v_empty[2], (adj_quantise, 7)]
         vector += [(ax_quantise, 5, 0, 2), v_empty[3], v_empty[4], v_empty[5], (ax_quantise, 6, 0, 2), v_empty[6]]
         vector += [(ax_quantise, LAST, 0, 1), (ax_quantise, LAST, 1, 2), v_empty[7], v_empty[8]]
 
-        scalar = [(widen_plain, 1), (widen_plain, 3), (widen_plain, 4)]
-        scalar += [(x_copy, on_scalar, 1, 0, 0, COPIED), (widen_plain, 5), (x_collect, 1, 0)]
+        scalar = [(widen_plain, 2), (widen_plain, 4), (x_copy, on_scalar, 0, 0, G_STRIPS, G_STRIPS + 8), (widen_plain, 5), (x_copy, on_scalar, 0, 0, G_STRIPS + 8, STRIPS)]
+        scalar += [(x_copy, on_scalar, 1, 0, 0, COPIED), (x_collect, 1, 0)]
         scalar += [(x_copy, on_scalar, 0, 1, 0, COPIED), (x_collect, 0, 1), (x_copy, on_scalar, 1, 1, V_STRIPS_11, STRIPS)]
         scalar += [(step[0], on_scalar) + step[1:] for step in filled if step not in for_vector]
 
         stores = [(store,) + piece for piece in pieces]
-        issue([tensor, vector, scalar, [(x_pool, 0, 0, 0, STRIPS)], stores])
+        issue([tensor, vector, scalar, [(x_pool, 0, 0, 0, G_STRIPS)], stores])

@@ -25,8 +25,9 @@ FLOPS = 2 * 2 * N * N * N
 STRIPS = 64
 COPIED = STRIPS // 2
 V_STRIPS_01 = 16
-V_STRIPS_11 = 20
-G_STRIPS = 48
+V_STRIPS_11 = 24
+G_STRIPS = 64
+G_STRIPS_11 = 8
 EARLY = 3
 WARM_UPS = 5
 
@@ -96,7 +97,7 @@ def tile_graphconvolution_pb_w4_kernel(tc, adj_bytes, adj_scale, x, weight_words
 
         def x_tile(g, h):
             if (g, h) not in grouped_x:
-                grouped_x[g, h] = keep.tile([P, 4 * HALF], BF16, name="grouped_x%d%d" % (g, h), align_bytes=64)
+                grouped_x[g, h] = keep.tile([P, 4 * HALF], BF16, name="grouped_x%d%d" % (g, 0 if g else h), align_bytes=64)
             return grouped_x[g, h]
 
         def x_copy(copy, g, h, lo, hi):
@@ -129,7 +130,10 @@ def tile_graphconvolution_pb_w4_kernel(tc, adj_bytes, adj_scale, x, weight_words
         def x_quantise(g, h):
             nc.vector.quantize_mx(out=x_codes[:, h, g, :].bitcast(FP8X4), scales=x_scales[:, h, g, :], in_=grouped_x[g, h][:])
 
-        word_sets, turned, grouped_adj, adj_codes, adj_scales = {}, {}, {}, {}, {}
+        word_sets, turned = {}, {}
+        grouped_adj = keep.tile([P, BLOCKS * N], BF16, align_bytes=64)
+        adj_codes = keep.tile([P, BLOCKS * 2 * P], U32, align_bytes=64)
+        adj_scales = keep.tile([P, BLOCKS * 2 * P], U8, align_bytes=64)
 
         def widen_sorted(b):
             wide = per_block.tile([P, N], BF16, name="wide", align_bytes=64)
@@ -142,9 +146,9 @@ def tile_graphconvolution_pb_w4_kernel(tc, adj_bytes, adj_scale, x, weight_words
             )
             word_sets[b] = wide[:].bitcast(F32).rearrange("r (u g p) -> r u g p", u=2, g=2)
 
-        def widen_plain(b):
+        def widen_plain(copy, b):
             wide = per_block.tile([P, N], BF16, name="wide", align_bytes=64)
-            on_scalar(wide[:], adj_rows[b].bitcast(FP8))
+            copy(wide[:], adj_rows[b].bitcast(FP8))
             word_sets[b] = wide[:].bitcast(F32).rearrange("r (g p u) -> r u g p", u=2, g=2)
 
         def turn(b):
@@ -155,37 +159,36 @@ def tile_graphconvolution_pb_w4_kernel(tc, adj_bytes, adj_scale, x, weight_words
             turned[b] = bank
 
         def scale_adj(b):
-            tile = per_block.tile([P, N], BF16, name="grouped_adj", align_bytes=64)
             nc.vector.tensor_tensor(
-                out=tile[:].rearrange("p (g r u e) -> p g r u e", g=2, u=2, e=2),
+                out=grouped_adj[:, N * b : N * (b + 1)].rearrange("p (g r u e) -> p g r u e", g=2, u=2, e=2),
                 in0=turned[b][:].bitcast(BF16).rearrange("p u g (r e) -> p g r u e", e=2),
                 in1=col_scale[:].rearrange("p g (u e) -> p g u e", e=2).unsqueeze(2).to_broadcast([P, 2, P, 2, 2]),
                 op=MULT,
             )
             emptied.add(("adj", b))
-            grouped_adj[b] = tile
 
-        def adj_quantise(b):
-            adj_codes[b] = per_block.tile([P, 2 * P], U32, name="adj_codes", align_bytes=64)
-            adj_scales[b] = per_block.tile([P, 2 * P], U8, name="adj_scales", align_bytes=64)
-            nc.vector.quantize_mx(out=adj_codes[b][:].bitcast(FP8X4), scales=adj_scales[b][:], in_=grouped_adj[b][:])
+        def adj_quantise(first, count):
+            words = slice(2 * P * first, 2 * P * (first + count))
+            nc.vector.quantize_mx(
+                out=adj_codes[:, words].bitcast(FP8X4), scales=adj_scales[:, words], in_=grouped_adj[:, N * first : N * (first + count)]
+            )
 
         ax_bank, grouped_ax, ax_codes, ax_scales = {}, {}, {}, {}
 
         def stage1(blocks, h, g):
-            nodes = slice(P * g, P * (g + 1))
             if g == 0:
                 for b in blocks:
                     ax_bank[b, h] = take_bank(("ax", b, h), [P, 4, P])
             for a in range(4):
                 group = slice(P * a, P * (a + 1))
                 for b in blocks:
+                    nodes = slice(P * (2 * b + g), P * (2 * b + g + 1))
                     nc.tensor.matmul_mx(
                         out=ax_bank[b, h][:, a, :],
                         lhsT=x_codes[:, h, g, group].bitcast(FP8X4),
                         lhsT_scale=x_scales[:, h, g, group],
-                        rhs=adj_codes[b][:, nodes].bitcast(FP8X4),
-                        rhs_scale=adj_scales[b][:, nodes],
+                        rhs=adj_codes[:, nodes].bitcast(FP8X4),
+                        rhs_scale=adj_scales[:, nodes],
                         start=(g == 0 and a == 0),
                         stop=(g == 1 and a == 3),
                     )
@@ -241,7 +244,9 @@ def tile_graphconvolution_pb_w4_kernel(tc, adj_bytes, adj_scale, x, weight_words
 
         def results(fn, *args):
             if fn in (widen_sorted, widen_plain):
-                return [("wide",) + args]
+                return [("wide", args[-1])]
+            if fn == adj_quantise:
+                return [(adj_quantise, b) for b in range(args[0], args[0] + args[1])]
             if fn == x_copy:
                 return [("strip", args[1], args[2], s) for s in range(args[3], args[4])]
             if fn == x_pool:
@@ -257,8 +262,12 @@ def tile_graphconvolution_pb_w4_kernel(tc, adj_bytes, adj_scale, x, weight_words
             return [(fn,) + args]
 
         def reads(fn, *args):
+            if fn in (x_copy, x_pool) and args[-4:-2] == (1, 1):
+                return [(x_quantise, 1, 0)]
             if fn == turn:
                 return [("wide",) + args]
+            if fn == adj_quantise:
+                return [(scale_adj, b) for b in range(args[0], args[0] + args[1])]
             if fn == x_quantise:
                 return [("strip",) + args + (s,) for s in range(STRIPS)]
             if fn == stage1:
@@ -271,7 +280,7 @@ def tile_graphconvolution_pb_w4_kernel(tc, adj_bytes, adj_scale, x, weight_words
                 return [(ax_quantise, args[0], h) for h in range(2)]
             if fn == out_copy:
                 return [(stage2,) + args[1:]]
-            source = {x_collect: x_spread, scale_adj: turn, adj_quantise: scale_adj, store: out_copy}
+            source = {x_collect: x_spread, scale_adj: turn, store: out_copy}
             return [(source[fn],) + args] if fn in source else []
 
         def banks_taken(fn, *args):
@@ -291,19 +300,15 @@ def tile_graphconvolution_pb_w4_kernel(tc, adj_bytes, adj_scale, x, weight_words
                         for r in results(*step):
                             done.add(r)
 
-        early = tuple(range(EARLY))
-
-        load_adj(0, 1)
-        load_adj(1, 1)
-        load_adj(2, 2)
+        for b in (0, 2, 1, 3):
+            load_adj(b, 1)
+        load_adj(4, 2)
         nc.sync.dma_start(out=col_scale[:], in_=adj_scale.rearrange("o (g p t) -> p (o g) t", g=2, t=4))
-        load_adj(4, 1)
         load_x(0, 0)
-        load_adj(5, 1)
+        load_adj(6, 2)
         load_x(1, 0)
         load_x(0, 1)
         load_x(1, 1)
-        load_adj(6, 2)
         nc.vector.memset(w_scales[:].rearrange("p g n -> p (g n)").bitcast(I32), 0)
         nc.vector.memset(one[:], 1.0)
         load_weight()
@@ -313,24 +318,28 @@ def tile_graphconvolution_pb_w4_kernel(tc, adj_bytes, adj_scale, x, weight_words
         pieces = [(b, lo, lo + HALF) for b in range(BLOCKS) for lo in (0, HALF)][:-1]
         pieces += [(LAST, HALF, HALF + 2 * P), (LAST, HALF + 2 * P, N)]
 
-        def whole_stage1(b):
-            return [(stage1, (b,), h, g) for h in range(2) for g in range(2)]
+        def half_stage1(b, h):
+            return [(stage1, (b,), h, g) for g in range(2)]
 
-        tensor = [(warm_up, 5), (turn, 0), (warm_up, 1), (turn, 1), (turn, 3), (turn, 2), (warm_up, 2), (turn, 4)]
-        tensor += [(x_spread, 1, 0), (turn, 5), (x_spread, 0, 1)]
-        tensor += [(stage1, (b,), 0, g) for g in range(2) for b in range(4)]
-        tensor += [(stage1, (b,), 1, g) for g in range(2) for b in range(4)]
-        tensor += whole_stage1(4)
-        between = [[(turn, 6), (turn, 7)]] + [whole_stage1(b) for b in (5, 6, 7)] + [[]]
+        def whole_stage1(b):
+            return half_stage1(b, 0) + half_stage1(b, 1)
+
+        tensor = [(warm_up, 5), (turn, 0), (warm_up, 1), (turn, 1), (turn, 2), (warm_up, 1), (turn, 3), (warm_up, 1), (turn, 4), (turn, 5)]
+        tensor += [(x_spread, 1, 0), (turn, 6), (x_spread, 0, 1), (turn, 7)]
+        tensor += [(stage1, (b,), 0, g) for g in range(2) for b in range(3)]
+        tensor += half_stage1(3, 0) + half_stage1(4, 0)
+        tensor += [(stage1, (b,), 1, g) for g in range(2) for b in range(2)]
+        tensor += half_stage1(2, 1) + half_stage1(3, 1) + half_stage1(4, 1)
+        between = [whole_stage1(b) for b in (5, 6, 7)] + [[]]
         first = 0
-        for count, other in zip((2, 3, 3, 3, 6), between):
+        for count, other in zip((2, 5, 4, 6), between):
             tensor += [(stage2,) + piece for piece in pieces[first : first + count]] + other
             first = first + count
 
         for step in tensor:
             taken.extend(banks_taken(*step))
         freed.extend(taken)
-        for content, after in ((("adj", 4), ("x", 0, 1)), (("adj", 5), ("ax", 3, 0))):
+        for content, after in ((("adj", 4), ("x", 0, 1)), (("adj", 5), ("ax", 3, 0)), (("adj", 6), ("ax", 1, 1)), (("adj", 7), ("out", 0, HALF))):
             freed.remove(content)
             freed.insert(freed.index(after) + 1, content)
 
@@ -340,25 +349,25 @@ def tile_graphconvolution_pb_w4_kernel(tc, adj_bytes, adj_scale, x, weight_words
                 filled += [(ax_copy, b, step[2]) for b in step[1]]
             if step[0] == stage2:
                 filled.append((out_copy,) + step[1:])
-        for_vector = [(ax_copy, 4, 0), (out_copy, 1, 0, HALF)]
-        for_vector += [(out_copy, 3, 0, HALF), (out_copy, 4, 0, HALF), (ax_copy, 6, 1), (out_copy, 5, 0, HALF)]
+        for_vector = [(out_copy, 0, HALF, N), (ax_copy, 5, 1), (out_copy, 2, 0, HALF), (ax_copy, 6, 0), (out_copy, 3, HALF, N), (out_copy, 4, HALF, N)]
         for_vector += [(ax_copy, LAST, 1), (out_copy, 6, HALF, N), (out_copy,) + pieces[-2]]
         v_empty = [(step[0], on_vector) + step[1:] for step in for_vector]
 
         vector = [(widen_sorted, 0), (widen_sorted, 1), (widen_sorted, 3)]
-        vector += [(scale_adj, 0), (scale_adj, 1), (scale_adj, 3), (scale_adj, 2)]
-        vector += [(adj_quantise, 0), (adj_quantise, 1), (x_quantise, 0, 0), (adj_quantise, 2), (adj_quantise, 3), (x_quantise, 1, 0)]
-        vector += [(x_copy, on_vector, 1, 1, 0, V_STRIPS_11), (x_quantise, 0, 1), (scale_adj, 4), (x_quantise, 1, 1)]
-        vector += [(adj_quantise, 4), (widen_sorted, 6), (ax_quantise, 0, 0, 1), (widen_sorted, 7), (scale_adj, 5), (ax_quantise, 0, 1, 2)]
-        vector += [(ax_quantise, 1, 0, 2), (adj_quantise, 5), (ax_quantise, 2, 0, 2), v_empty[0], (ax_quantise, 3, 0, 2), v_empty[1]]
-        vector += [(scale_adj, 6), (scale_adj, 7), (ax_quantise, 4, 0, 2), (adj_quantise, 6), v_empty[2], (adj_quantise, 7)]
-        vector += [(ax_quantise, 5, 0, 2), v_empty[3], v_empty[4], v_empty[5], (ax_quantise, 6, 0, 2), v_empty[6]]
+        vector += [(scale_adj, b) for b in range(4)]
+        vector += [(adj_quantise, 0, 2), (x_quantise, 0, 0)]
+        vector += [(adj_quantise, 2, 2), (x_quantise, 1, 0), (scale_adj, 4), (x_copy, on_vector, 0, 1, 0, V_STRIPS_01), (adj_quantise, 4, 1)]
+        vector += [(x_copy, on_vector, 1, 1, G_STRIPS_11, V_STRIPS_11), (x_quantise, 0, 1), (x_quantise, 1, 1), (scale_adj, 5)]
+        vector += [(ax_quantise, 0, 0, 1), (adj_quantise, 5, 1), (ax_quantise, 0, 1, 2), (scale_adj, 6), (ax_quantise, 1, 0, 2), (adj_quantise, 6, 1)]
+        vector += [(ax_quantise, 2, 0, 2), (ax_quantise, 3, 0, 2), v_empty[0], (scale_adj, 7), v_empty[1], (ax_quantise, 4, 0, 2), (adj_quantise, 7, 1)]
+        vector += [v_empty[2], (ax_quantise, 5, 0, 2), v_empty[3], v_empty[4], (ax_quantise, 6, 0, 2), v_empty[5], v_empty[6]]
         vector += [(ax_quantise, LAST, 0, 1), (ax_quantise, LAST, 1, 2), v_empty[7], v_empty[8]]
 
-        scalar = [(widen_plain, 2), (widen_plain, 4), (x_copy, on_scalar, 0, 0, G_STRIPS, G_STRIPS + 8), (widen_plain, 5), (x_copy, on_scalar, 0, 0, G_STRIPS + 8, STRIPS)]
-        scalar += [(x_copy, on_scalar, 1, 0, 0, COPIED), (x_collect, 1, 0)]
-        scalar += [(x_copy, on_scalar, 0, 1, 0, COPIED), (x_collect, 0, 1), (x_copy, on_scalar, 1, 1, V_STRIPS_11, STRIPS)]
+        scalar = [(widen_plain, on_scalar, 2), (widen_plain, on_scalar, 4), (widen_plain, on_scalar, 5), (widen_plain, on_scalar, 6)]
+        scalar += [(x_copy, on_scalar, 1, 0, 0, COPIED), (widen_plain, on_scalar, 7), (x_collect, 1, 0)]
+        scalar += [(x_copy, on_scalar, 0, 1, V_STRIPS_01, COPIED), (x_collect, 0, 1), (x_copy, on_scalar, 1, 1, V_STRIPS_11, STRIPS)]
         scalar += [(step[0], on_scalar) + step[1:] for step in filled if step not in for_vector]
 
+        pool = [(x_pool, 0, 0, 0, G_STRIPS), (x_pool, 1, 1, 0, G_STRIPS_11)]
         stores = [(store,) + piece for piece in pieces]
-        issue([tensor, vector, scalar, [(x_pool, 0, 0, 0, G_STRIPS)], stores])
+        issue([tensor, vector, scalar, pool, stores])

@@ -131,9 +131,16 @@ def tile_graphconvolution_pb_w4_kernel(tc, adj_bytes, adj_scale, x, weight_words
             nc.vector.quantize_mx(out=x_codes[:, h, g, :].bitcast(FP8X4), scales=x_scales[:, h, g, :], in_=grouped_x[g, h][:])
 
         word_sets, turned = {}, {}
-        grouped_adj = keep.tile([P, BLOCKS * N], BF16, align_bytes=64)
-        adj_codes = keep.tile([P, BLOCKS * 2 * P], U32, align_bytes=64)
-        adj_scales = keep.tile([P, BLOCKS * 2 * P], U8, align_bytes=64)
+        adj_sets = {}
+
+        def adj_set(b):
+            first, count = (b - b % 2, 2) if b < 4 else (b, 1)
+            if first not in adj_sets:
+                grouped = keep.tile([P, count * N], BF16, name="grouped_adj%d" % first, align_bytes=64)
+                codes = keep.tile([P, count * 2 * P], U32, name="adj_codes%d" % first, align_bytes=64)
+                scales = keep.tile([P, count * 2 * P], U8, name="adj_scales%d" % first, align_bytes=64)
+                adj_sets[first] = (grouped, codes, scales)
+            return adj_sets[first] + (b - first,)
 
         def widen_sorted(b):
             wide = per_block.tile([P, N], BF16, name="wide", align_bytes=64)
@@ -159,8 +166,9 @@ def tile_graphconvolution_pb_w4_kernel(tc, adj_bytes, adj_scale, x, weight_words
             turned[b] = bank
 
         def scale_adj(b):
+            grouped, codes, scales, k = adj_set(b)
             nc.vector.tensor_tensor(
-                out=grouped_adj[:, N * b : N * (b + 1)].rearrange("p (g r u e) -> p g r u e", g=2, u=2, e=2),
+                out=grouped[:, N * k : N * (k + 1)].rearrange("p (g r u e) -> p g r u e", g=2, u=2, e=2),
                 in0=turned[b][:].bitcast(BF16).rearrange("p u g (r e) -> p g r u e", e=2),
                 in1=col_scale[:].rearrange("p g (u e) -> p g u e", e=2).unsqueeze(2).to_broadcast([P, 2, P, 2, 2]),
                 op=MULT,
@@ -168,10 +176,8 @@ def tile_graphconvolution_pb_w4_kernel(tc, adj_bytes, adj_scale, x, weight_words
             emptied.add(("adj", b))
 
         def adj_quantise(first, count):
-            words = slice(2 * P * first, 2 * P * (first + count))
-            nc.vector.quantize_mx(
-                out=adj_codes[:, words].bitcast(FP8X4), scales=adj_scales[:, words], in_=grouped_adj[:, N * first : N * (first + count)]
-            )
+            grouped, codes, scales, k = adj_set(first)
+            nc.vector.quantize_mx(out=codes[:].bitcast(FP8X4), scales=scales[:], in_=grouped[:])
 
         ax_bank, grouped_ax, ax_codes, ax_scales = {}, {}, {}, {}
 
@@ -182,13 +188,14 @@ def tile_graphconvolution_pb_w4_kernel(tc, adj_bytes, adj_scale, x, weight_words
             for a in range(4):
                 group = slice(P * a, P * (a + 1))
                 for b in blocks:
-                    nodes = slice(P * (2 * b + g), P * (2 * b + g + 1))
+                    grouped, codes, scales, k = adj_set(b)
+                    nodes = slice(P * (2 * k + g), P * (2 * k + g + 1))
                     nc.tensor.matmul_mx(
                         out=ax_bank[b, h][:, a, :],
                         lhsT=x_codes[:, h, g, group].bitcast(FP8X4),
                         lhsT_scale=x_scales[:, h, g, group],
-                        rhs=adj_codes[:, nodes].bitcast(FP8X4),
-                        rhs_scale=adj_scales[:, nodes],
+                        rhs=codes[:, nodes].bitcast(FP8X4),
+                        rhs_scale=scales[:, nodes],
                         start=(g == 0 and a == 0),
                         stop=(g == 1 and a == 3),
                     )
@@ -264,6 +271,8 @@ def tile_graphconvolution_pb_w4_kernel(tc, adj_bytes, adj_scale, x, weight_words
         def reads(fn, *args):
             if fn in (x_copy, x_pool) and args[-4:-2] == (1, 1):
                 return [(x_quantise, 1, 0)]
+            if fn == x_copy and args[:3] == (on_vector, 0, 1):
+                return [("strip", 0, 1, COPIED)]
             if fn == turn:
                 return [("wide",) + args]
             if fn == adj_quantise:

@@ -27,8 +27,8 @@ COPIED = STRIPS // 2
 V_STRIPS_01 = 16
 V_STRIPS_11 = 24
 G_STRIPS = 64
-G_STRIPS_11 = 8
-EARLY = 3
+S_CUT = 44
+COUNTS = (2, 3, 3, 3, 6)
 WARM_UPS = 5
 
 
@@ -97,7 +97,7 @@ def tile_graphconvolution_pb_w4_kernel(tc, adj_bytes, adj_scale, x, weight_words
 
         def x_tile(g, h):
             if (g, h) not in grouped_x:
-                grouped_x[g, h] = keep.tile([P, 4 * HALF], BF16, name="grouped_x%d%d" % (g, 0 if g else h), align_bytes=64)
+                grouped_x[g, h] = keep.tile([P, 4 * HALF], BF16, name="grouped_x%d%d" % (g, h), align_bytes=64)
             return grouped_x[g, h]
 
         def x_copy(copy, g, h, lo, hi):
@@ -269,8 +269,6 @@ def tile_graphconvolution_pb_w4_kernel(tc, adj_bytes, adj_scale, x, weight_words
             return [(fn,) + args]
 
         def reads(fn, *args):
-            if fn in (x_copy, x_pool) and args[-4:-2] == (1, 1):
-                return [(x_quantise, 1, 0)]
             if fn == x_copy and args[:3] == (on_vector, 0, 1):
                 return [("strip", 0, 1, COPIED)]
             if fn == turn:
@@ -309,15 +307,16 @@ def tile_graphconvolution_pb_w4_kernel(tc, adj_bytes, adj_scale, x, weight_words
                         for r in results(*step):
                             done.add(r)
 
-        for b in (0, 2, 1, 3):
+        for b in (0, 2, 1):
             load_adj(b, 1)
-        load_adj(4, 2)
+        load_adj(3, 2)
         nc.sync.dma_start(out=col_scale[:], in_=adj_scale.rearrange("o (g p t) -> p (o g) t", g=2, t=4))
         load_x(0, 0)
-        load_adj(6, 2)
+        load_adj(5, 1)
         load_x(1, 0)
         load_x(0, 1)
         load_x(1, 1)
+        load_adj(6, 2)
         nc.vector.memset(w_scales[:].rearrange("p g n -> p (g n)").bitcast(I32), 0)
         nc.vector.memset(one[:], 1.0)
         load_weight()
@@ -333,22 +332,21 @@ def tile_graphconvolution_pb_w4_kernel(tc, adj_bytes, adj_scale, x, weight_words
         def whole_stage1(b):
             return half_stage1(b, 0) + half_stage1(b, 1)
 
-        tensor = [(warm_up, 5), (turn, 0), (warm_up, 1), (turn, 1), (turn, 2), (warm_up, 1), (turn, 3), (warm_up, 1), (turn, 4), (turn, 5)]
-        tensor += [(x_spread, 1, 0), (turn, 6), (x_spread, 0, 1), (turn, 7)]
-        tensor += [(stage1, (b,), 0, g) for g in range(2) for b in range(3)]
-        tensor += half_stage1(3, 0) + half_stage1(4, 0)
-        tensor += [(stage1, (b,), 1, g) for g in range(2) for b in range(2)]
-        tensor += half_stage1(2, 1) + half_stage1(3, 1) + half_stage1(4, 1)
-        between = [whole_stage1(b) for b in (5, 6, 7)] + [[]]
+        tensor = [(warm_up, WARM_UPS), (turn, 0), (warm_up, 1), (turn, 1), (warm_up, 1), (turn, 3), (turn, 2), (turn, 4)]
+        tensor += [(x_spread, 1, 0), (turn, 5), (x_spread, 0, 1)]
+        for h in range(2):
+            tensor += [(stage1, (b,), h, g) for g in range(2) for b in range(4)]
+        tensor += whole_stage1(4)
+        between = [[(turn, 6), (turn, 7)]] + [whole_stage1(b) for b in (5, 6, 7)] + [[]]
         first = 0
-        for count, other in zip((2, 5, 4, 6), between):
+        for count, other in zip(COUNTS, between):
             tensor += [(stage2,) + piece for piece in pieces[first : first + count]] + other
             first = first + count
 
         for step in tensor:
             taken.extend(banks_taken(*step))
         freed.extend(taken)
-        for content, after in ((("adj", 4), ("x", 0, 1)), (("adj", 5), ("ax", 3, 0)), (("adj", 6), ("ax", 1, 1)), (("adj", 7), ("out", 0, HALF))):
+        for content, after in ((("adj", 4), ("ax", 1, 0)), (("adj", 5), ("ax", 4, 0))):
             freed.remove(content)
             freed.insert(freed.index(after) + 1, content)
 
@@ -358,25 +356,25 @@ def tile_graphconvolution_pb_w4_kernel(tc, adj_bytes, adj_scale, x, weight_words
                 filled += [(ax_copy, b, step[2]) for b in step[1]]
             if step[0] == stage2:
                 filled.append((out_copy,) + step[1:])
-        for_vector = [(out_copy, 0, HALF, N), (ax_copy, 5, 1), (out_copy, 2, 0, HALF), (ax_copy, 6, 0), (out_copy, 3, HALF, N), (out_copy, 4, HALF, N)]
+        for_vector = [(out_copy, 1, 0, HALF), (out_copy, 2, HALF, N), (out_copy, 4, 0, HALF), (ax_copy, 6, 1), (out_copy, 5, 0, HALF)]
         for_vector += [(ax_copy, LAST, 1), (out_copy, 6, HALF, N), (out_copy,) + pieces[-2]]
         v_empty = [(step[0], on_vector) + step[1:] for step in for_vector]
 
         vector = [(widen_sorted, 0), (widen_sorted, 1), (widen_sorted, 3)]
-        vector += [(scale_adj, b) for b in range(4)]
-        vector += [(adj_quantise, 0, 2), (x_quantise, 0, 0)]
-        vector += [(adj_quantise, 2, 2), (x_quantise, 1, 0), (scale_adj, 4), (x_copy, on_vector, 0, 1, 0, V_STRIPS_01), (adj_quantise, 4, 1)]
-        vector += [(x_copy, on_vector, 1, 1, G_STRIPS_11, V_STRIPS_11), (x_quantise, 0, 1), (x_quantise, 1, 1), (scale_adj, 5)]
-        vector += [(ax_quantise, 0, 0, 1), (adj_quantise, 5, 1), (ax_quantise, 0, 1, 2), (scale_adj, 6), (ax_quantise, 1, 0, 2), (adj_quantise, 6, 1)]
-        vector += [(ax_quantise, 2, 0, 2), (ax_quantise, 3, 0, 2), v_empty[0], (scale_adj, 7), v_empty[1], (ax_quantise, 4, 0, 2), (adj_quantise, 7, 1)]
-        vector += [v_empty[2], (ax_quantise, 5, 0, 2), v_empty[3], v_empty[4], (ax_quantise, 6, 0, 2), v_empty[5], v_empty[6]]
-        vector += [(ax_quantise, LAST, 0, 1), (ax_quantise, LAST, 1, 2), v_empty[7], v_empty[8]]
+        vector += [(scale_adj, 0), (scale_adj, 1), (scale_adj, 3), (scale_adj, 2)]
+        vector += [(adj_quantise, 0, 2), (x_quantise, 0, 0), (adj_quantise, 2, 2), (x_quantise, 1, 0)]
+        vector += [(x_copy, on_vector, 1, 1, 0, V_STRIPS_11), (x_quantise, 0, 1), (x_quantise, 1, 1), (scale_adj, 4)]
+        vector += [(ax_quantise, 0, 0, 1), (adj_quantise, 4, 1), (widen_sorted, 6), (widen_sorted, 7), (ax_quantise, 0, 1, 2), (ax_quantise, 1, 0, 2)]
+        vector += [(scale_adj, 5), (ax_quantise, 2, 0, 2), (adj_quantise, 5, 1), (ax_quantise, 3, 0, 2), (scale_adj, 6), v_empty[0]]
+        vector += [(adj_quantise, 6, 1), (ax_quantise, 4, 0, 2), (scale_adj, 7), v_empty[1], (adj_quantise, 7, 1)]
+        vector += [(ax_quantise, 5, 0, 2), v_empty[2], v_empty[3], v_empty[4], (ax_quantise, 6, 0, 2), v_empty[5]]
+        vector += [(ax_quantise, LAST, 0, 1), (ax_quantise, LAST, 1, 2), v_empty[6], v_empty[7]]
 
-        scalar = [(widen_plain, on_scalar, 2), (widen_plain, on_scalar, 4), (widen_plain, on_scalar, 5), (widen_plain, on_scalar, 6)]
-        scalar += [(x_copy, on_scalar, 1, 0, 0, COPIED), (widen_plain, on_scalar, 7), (x_collect, 1, 0)]
-        scalar += [(x_copy, on_scalar, 0, 1, V_STRIPS_01, COPIED), (x_collect, 0, 1), (x_copy, on_scalar, 1, 1, V_STRIPS_11, STRIPS)]
+        scalar = [(widen_plain, on_scalar, 2), (widen_plain, on_scalar, 4), (widen_plain, on_scalar, 5)]
+        scalar += [(x_copy, on_scalar, 1, 0, 0, COPIED), (x_copy, on_scalar, 0, 1, 0, COPIED)]
+        scalar += [(x_collect, 1, 0), (x_copy, on_scalar, 1, 1, V_STRIPS_11, S_CUT), (x_collect, 0, 1), (x_copy, on_scalar, 1, 1, S_CUT, STRIPS)]
         scalar += [(step[0], on_scalar) + step[1:] for step in filled if step not in for_vector]
 
-        pool = [(x_pool, 0, 0, 0, G_STRIPS), (x_pool, 1, 1, 0, G_STRIPS_11)]
+        pool = [(x_pool, 0, 0, 0, STRIPS)]
         stores = [(store,) + piece for piece in pieces]
         issue([tensor, vector, scalar, pool, stores])

@@ -28,6 +28,8 @@ V_STRIPS_01 = 16
 V_STRIPS_11 = 24
 G_STRIPS = 64
 S_CUT = 44
+SPLIT = 4
+SPREAD_FROM = {(1, 0): 32, (0, 1): 32}
 COUNTS = (2, 3, 3, 3, 6)
 WARM_UPS = 5
 
@@ -111,24 +113,28 @@ def tile_graphconvolution_pb_w4_kernel(tc, adj_bytes, adj_scale, x, weight_words
             nc.gpsimd.tensor_scalar(out=dst, in0=src, scalar1=1.0, scalar2=0.0, op0=MULT, op1=ADD)
 
         def x_spread(g, h):
-            bank = take_bank(("x", g, h), [P, HALF])
-            for c in range(2):
+            first = 8 * SPREAD_FROM[g, h]
+            bank = take_bank(("x", g, h), [P, 2 * (HALF - first)])
+            for c in range(0, HALF - first, P):
                 nc.tensor.matmul(
-                    bank[:].bitcast(BF16)[:, HALF * c : HALF * (c + 1)].rearrange("p (d t) -> p t d", t=4),
+                    bank[:].bitcast(BF16)[:, 4 * c : 4 * (c + P)].rearrange("p (d t) -> p t d", t=4),
                     lhsT=ident16[:],
-                    rhs=x_rows[g, h][:, :, P * (2 + c) : P * (3 + c)],
+                    rhs=x_rows[g, h][:, :, first + c : first + c + P],
                     start=True,
                     stop=True,
                 )
             spread_x[g, h] = bank
 
         def x_collect(g, h):
-            dst = x_tile(g, h)[:].bitcast(F32).rearrange("p (a m z) -> p a m z", a=4, z=2)[:, :, P // 2 :, :]
+            dst = x_tile(g, h)[:].bitcast(F32).rearrange("p (a m z) -> p a m z", a=4, z=2)[:, :, 2 * SPREAD_FROM[g, h] :, :]
             on_scalar(dst, spread_x[g, h][:].rearrange("p (m a z) -> p a m z", a=4, z=2))
             emptied.add(("x", g, h))
 
-        def x_quantise(g, h):
-            nc.vector.quantize_mx(out=x_codes[:, h, g, :].bitcast(FP8X4), scales=x_scales[:, h, g, :], in_=grouped_x[g, h][:])
+        def x_quantise(g, h, lo, hi):
+            words = slice(P * lo, P * hi)
+            nc.vector.quantize_mx(
+                out=x_codes[:, h, g, words].bitcast(FP8X4), scales=x_scales[:, h, g, words], in_=grouped_x[g, h][:, HALF * lo : HALF * hi]
+            )
 
         word_sets, turned = {}, {}
         adj_sets = {}
@@ -181,11 +187,11 @@ def tile_graphconvolution_pb_w4_kernel(tc, adj_bytes, adj_scale, x, weight_words
 
         ax_bank, grouped_ax, ax_codes, ax_scales = {}, {}, {}, {}
 
-        def stage1(blocks, h, g):
-            if g == 0:
+        def stage1(blocks, h, g, lo, hi):
+            if g == 0 and lo == 0:
                 for b in blocks:
                     ax_bank[b, h] = take_bank(("ax", b, h), [P, 4, P])
-            for a in range(4):
+            for a in range(lo, hi):
                 group = slice(P * a, P * (a + 1))
                 for b in blocks:
                     grouped, codes, scales, k = adj_set(b)
@@ -219,25 +225,26 @@ def tile_graphconvolution_pb_w4_kernel(tc, adj_bytes, adj_scale, x, weight_words
 
         out_bank, out_tile = {}, {}
 
-        def stage2(b, lo, hi):
-            out_bank[b, lo] = take_bank(("out", b, lo), [P, hi - lo])
+        def stage2(b, lo, hi, passes=(0, 1)):
+            if passes[0] == 0:
+                out_bank[b, lo] = take_bank(("out", b, lo), [P, hi - lo])
             width = HALF if hi - lo == HALF else P
-            for first in range(lo, hi, width):
-                for h in range(2):
-                    nodes = slice(P * h, P * (h + 1))
+            for h in passes:
+                nodes = slice(P * h, P * (h + 1))
+                for first in range(lo, hi, width):
                     nc.tensor.matmul_mx(
                         out=out_bank[b, lo][:, first - lo : first - lo + width],
                         lhsT=ax_codes[b][:, nodes].bitcast(FP8X4),
                         lhsT_scale=ax_scales[b][:, nodes],
                         rhs=w_words[:, h, 2 * first : 2 * (first + width)].bitcast(FP4X4),
                         rhs_scale=w_scales[:, h, first : first + width],
-                        start=(h == 0),
-                        stop=(h == 1),
+                        start=(h == 0 and first == lo),
+                        stop=(h == 1 and first + width == hi),
                     )
 
         def out_copy(copy, b, lo, hi):
             width = hi - lo
-            out_tile[b, lo] = per_block.tile([P, width], F32, name="out%d" % width, bufs=8 if width == HALF else 2)
+            out_tile[b, lo] = per_block.tile([P, width], F32, name="out%d" % width, bufs=8 if width == HALF else 2 * SPLIT)
             copy(out_tile[b, lo][:], out_bank[b, lo][:])
             emptied.add(("out", b, lo))
 
@@ -259,40 +266,44 @@ def tile_graphconvolution_pb_w4_kernel(tc, adj_bytes, adj_scale, x, weight_words
             if fn == x_pool:
                 return [("strip", args[0], args[1], s) for s in range(args[2], args[3])]
             if fn == x_collect:
-                return [("strip",) + args + (s,) for s in range(COPIED, STRIPS)]
+                return [("strip",) + args + (s,) for s in range(SPREAD_FROM[args], STRIPS)]
+            if fn == x_quantise:
+                return [(x_quantise, args[0], args[1], a) for a in range(args[2], args[3])]
             if fn == stage1:
-                return [(stage1, b, args[1], args[2]) for b in args[0]]
+                return [(stage1, b, args[1], args[2], a) for b in args[0] for a in range(args[3], args[4])]
             if fn == ax_quantise:
                 return [(ax_quantise, args[0], h) for h in range(args[1], args[2])]
+            if fn == stage2:
+                return [(stage2,) + args[:3]] if args[3:] != ((0,),) else []
             if fn in (ax_copy, out_copy):
                 return [(fn,) + args[1:]]
             return [(fn,) + args]
 
         def reads(fn, *args):
-            if fn == x_copy and args[:3] == (on_vector, 0, 1):
-                return [("strip", 0, 1, COPIED)]
             if fn == turn:
                 return [("wide",) + args]
             if fn == adj_quantise:
                 return [(scale_adj, b) for b in range(args[0], args[0] + args[1])]
             if fn == x_quantise:
-                return [("strip",) + args + (s,) for s in range(STRIPS)]
+                return [("strip",) + args[:2] + (s,) for s in range(STRIPS)]
             if fn == stage1:
-                return [(x_quantise, args[2], args[1])] + [(adj_quantise, b) for b in args[0]]
+                return [(x_quantise, args[2], args[1], a) for a in range(args[3], args[4])] + [(adj_quantise, b) for b in args[0]]
             if fn == ax_copy:
-                return [(stage1,) + args[1:] + (1,)]
+                return [(stage1,) + args[1:] + (1, 3)]
             if fn == ax_quantise:
                 return [(ax_copy, args[0], h) for h in range(args[1], args[2])]
             if fn == stage2:
-                return [(ax_quantise, args[0], h) for h in range(2)]
+                return [(ax_quantise, args[0], h) for h in (args[3] if args[3:] else range(2))]
             if fn == out_copy:
                 return [(stage2,) + args[1:]]
             source = {x_collect: x_spread, scale_adj: turn, store: out_copy}
             return [(source[fn],) + args] if fn in source else []
 
         def banks_taken(fn, *args):
-            if fn == stage1 and args[2] == 0:
+            if fn == stage1 and args[2:4] == (0, 0):
                 return [("ax", b, args[1]) for b in args[0]]
+            if fn == stage2 and args[3:] == ((1,),):
+                return []
             kind = {turn: "adj", x_spread: "x", stage2: "out"}
             return [(kind[fn],) + args[:2]] if fn in kind else []
 
@@ -323,11 +334,12 @@ def tile_graphconvolution_pb_w4_kernel(tc, adj_bytes, adj_scale, x, weight_words
         make_identity(nc, ident[:])
         make_identity(nc, ident16[:])
 
-        pieces = [(b, lo, lo + HALF) for b in range(BLOCKS) for lo in (0, HALF)][:-1]
-        pieces += [(LAST, HALF, HALF + 2 * P), (LAST, HALF + 2 * P, N)]
+        halves = [(b, lo) for b in range(BLOCKS) for lo in (0, HALF)]
+        pieces = [(b, lo, lo + HALF) for b, lo in halves[:-SPLIT]]
+        pieces += [(b, lo + q, lo + q + 2 * P) for b, lo in halves[-SPLIT:] for q in (0, 2 * P)]
 
         def half_stage1(b, h):
-            return [(stage1, (b,), h, g) for g in range(2)]
+            return [(stage1, (b,), h, g, 0, 4) for g in range(2)]
 
         def whole_stage1(b):
             return half_stage1(b, 0) + half_stage1(b, 1)
@@ -335,13 +347,15 @@ def tile_graphconvolution_pb_w4_kernel(tc, adj_bytes, adj_scale, x, weight_words
         tensor = [(warm_up, WARM_UPS), (turn, 0), (warm_up, 1), (turn, 1), (warm_up, 1), (turn, 3), (turn, 2), (turn, 4)]
         tensor += [(x_spread, 1, 0), (turn, 5), (x_spread, 0, 1)]
         for h in range(2):
-            tensor += [(stage1, (b,), h, g) for g in range(2) for b in range(4)]
+            tensor += [(stage1, (b,), h, g, 0, 4) for g in range(2) for b in range(4)]
         tensor += whole_stage1(4)
-        between = [[(turn, 6), (turn, 7)]] + [whole_stage1(b) for b in (5, 6, 7)] + [[]]
+        between = [[(turn, 6), (turn, 7)], whole_stage1(5), whole_stage1(6), half_stage1(LAST, 0), half_stage1(LAST, 1), []]
         first = 0
-        for count, other in zip(COUNTS, between):
+        for count, other in zip((2, 3, 3, 3, 1, 4), between):
             tensor += [(stage2,) + piece for piece in pieces[first : first + count]] + other
             first = first + count
+        tensor += [(stage2,) + piece + ((h,),) for h in range(2) for piece in pieces[first : first + 2]]
+        tensor += [(stage2,) + piece for piece in pieces[first + 2 :]]
 
         for step in tensor:
             taken.extend(banks_taken(*step))
@@ -352,26 +366,26 @@ def tile_graphconvolution_pb_w4_kernel(tc, adj_bytes, adj_scale, x, weight_words
 
         filled = []
         for step in tensor:
-            if step[0] == stage1 and step[3] == 1:
+            if step[0] == stage1 and step[3] == 1 and step[5] == 4:
                 filled += [(ax_copy, b, step[2]) for b in step[1]]
-            if step[0] == stage2:
-                filled.append((out_copy,) + step[1:])
+            if step[0] == stage2 and step[4:] != ((0,),):
+                filled.append((out_copy,) + step[1:4])
         for_vector = [(out_copy, 1, 0, HALF), (out_copy, 2, HALF, N), (out_copy, 4, 0, HALF), (ax_copy, 6, 1), (out_copy, 5, 0, HALF)]
-        for_vector += [(ax_copy, LAST, 1), (out_copy, 6, HALF, N), (out_copy,) + pieces[-2]]
+        for_vector += [(ax_copy, LAST, 1)] + [(out_copy,) + piece for piece in pieces[14::2]]
         v_empty = [(step[0], on_vector) + step[1:] for step in for_vector]
 
         vector = [(widen_sorted, 0), (widen_sorted, 1), (widen_sorted, 3)]
         vector += [(scale_adj, 0), (scale_adj, 1), (scale_adj, 3), (scale_adj, 2)]
-        vector += [(adj_quantise, 0, 2), (x_quantise, 0, 0), (adj_quantise, 2, 2), (x_quantise, 1, 0)]
-        vector += [(x_copy, on_vector, 1, 1, 0, V_STRIPS_11), (x_quantise, 0, 1), (x_quantise, 1, 1), (scale_adj, 4)]
+        vector += [(adj_quantise, 0, 2), (x_quantise, 0, 0, 0, 4), (adj_quantise, 2, 2), (x_quantise, 1, 0, 0, 4)]
+        vector += [(x_copy, on_vector, 1, 1, 0, V_STRIPS_11), (x_quantise, 0, 1, 0, 4), (x_quantise, 1, 1, 0, 4), (scale_adj, 4)]
         vector += [(ax_quantise, 0, 0, 1), (adj_quantise, 4, 1), (widen_sorted, 6), (widen_sorted, 7), (ax_quantise, 0, 1, 2), (ax_quantise, 1, 0, 2)]
         vector += [(scale_adj, 5), (ax_quantise, 2, 0, 2), (adj_quantise, 5, 1), (ax_quantise, 3, 0, 2), (scale_adj, 6), v_empty[0]]
         vector += [(adj_quantise, 6, 1), (ax_quantise, 4, 0, 2), (scale_adj, 7), v_empty[1], (adj_quantise, 7, 1)]
-        vector += [(ax_quantise, 5, 0, 2), v_empty[2], v_empty[3], v_empty[4], (ax_quantise, 6, 0, 2), v_empty[5]]
-        vector += [(ax_quantise, LAST, 0, 1), (ax_quantise, LAST, 1, 2), v_empty[6], v_empty[7]]
+        vector += [(ax_quantise, 5, 0, 2), v_empty[2], v_empty[3], v_empty[4], (ax_quantise, 6, 0, 2), (ax_quantise, LAST, 0, 1), v_empty[5]]
+        vector += [(ax_quantise, LAST, 1, 2)] + v_empty[6:]
 
         scalar = [(widen_plain, on_scalar, 2), (widen_plain, on_scalar, 4), (widen_plain, on_scalar, 5)]
-        scalar += [(x_copy, on_scalar, 1, 0, 0, COPIED), (x_copy, on_scalar, 0, 1, 0, COPIED)]
+        scalar += [(x_copy, on_scalar, 1, 0, 0, SPREAD_FROM[1, 0]), (x_copy, on_scalar, 0, 1, 0, SPREAD_FROM[0, 1])]
         scalar += [(x_collect, 1, 0), (x_copy, on_scalar, 1, 1, V_STRIPS_11, S_CUT), (x_collect, 0, 1), (x_copy, on_scalar, 1, 1, S_CUT, STRIPS)]
         scalar += [(step[0], on_scalar) + step[1:] for step in filled if step not in for_vector]
 

@@ -24,13 +24,9 @@ FLOPS = 2 * 2 * N * N * N
 
 STRIPS = 64
 COPIED = STRIPS // 2
-V_STRIPS_01 = 16
-V_STRIPS_11 = 24
-G_STRIPS = 64
+V_STRIPS = 24
 S_CUT = 44
-SPLIT = 4
-SPREAD_FROM = {(1, 0): 32, (0, 1): 32}
-COUNTS = (2, 3, 3, 3, 6)
+EARLY = 4
 WARM_UPS = 5
 
 
@@ -107,40 +103,36 @@ def tile_graphconvolution_pb_w4_kernel(tc, adj_bytes, adj_scale, x, weight_words
             dst = x_tile(g, h)[:].rearrange("p (a s i t) -> p s a t i", a=4, i=2, t=4)[:, lo:hi]
             copy(dst, src)
 
-        def x_pool(g, h, lo, hi):
-            src = x_rows[g, h][:].rearrange("p t (m a) -> p m a t", a=4)[:, 2 * lo : 2 * hi]
-            dst = x_tile(g, h)[:].rearrange("p (a m t) -> p m a t", a=4, t=4)[:, 2 * lo : 2 * hi]
+        def x_pool(g, h):
+            src = x_rows[g, h][:].rearrange("p t (m a) -> p m a t", a=4)
+            dst = x_tile(g, h)[:].rearrange("p (a m t) -> p m a t", a=4, t=4)
             nc.gpsimd.tensor_scalar(out=dst, in0=src, scalar1=1.0, scalar2=0.0, op0=MULT, op1=ADD)
 
         def x_spread(g, h):
-            first = 8 * SPREAD_FROM[g, h]
-            bank = take_bank(("x", g, h), [P, 2 * (HALF - first)])
-            for c in range(0, HALF - first, P):
+            bank = take_bank(("x", g, h), [P, HALF])
+            for c in range(2):
                 nc.tensor.matmul(
-                    bank[:].bitcast(BF16)[:, 4 * c : 4 * (c + P)].rearrange("p (d t) -> p t d", t=4),
+                    bank[:].bitcast(BF16)[:, HALF * c : HALF * (c + 1)].rearrange("p (d t) -> p t d", t=4),
                     lhsT=ident16[:],
-                    rhs=x_rows[g, h][:, :, first + c : first + c + P],
+                    rhs=x_rows[g, h][:, :, P * (2 + c) : P * (3 + c)],
                     start=True,
                     stop=True,
                 )
             spread_x[g, h] = bank
 
         def x_collect(g, h):
-            dst = x_tile(g, h)[:].bitcast(F32).rearrange("p (a m z) -> p a m z", a=4, z=2)[:, :, 2 * SPREAD_FROM[g, h] :, :]
+            dst = x_tile(g, h)[:].bitcast(F32).rearrange("p (a m z) -> p a m z", a=4, z=2)[:, :, P // 2 :, :]
             on_scalar(dst, spread_x[g, h][:].rearrange("p (m a z) -> p a m z", a=4, z=2))
             emptied.add(("x", g, h))
 
-        def x_quantise(g, h, lo, hi):
-            words = slice(P * lo, P * hi)
-            nc.vector.quantize_mx(
-                out=x_codes[:, h, g, words].bitcast(FP8X4), scales=x_scales[:, h, g, words], in_=grouped_x[g, h][:, HALF * lo : HALF * hi]
-            )
+        def x_quantise(g, h):
+            nc.vector.quantize_mx(out=x_codes[:, h, g, :].bitcast(FP8X4), scales=x_scales[:, h, g, :], in_=grouped_x[g, h][:])
 
         word_sets, turned = {}, {}
         adj_sets = {}
 
         def adj_set(b):
-            first, count = (b - b % 2, 2) if b < 4 else (b, 1)
+            first, count = (b - b % 2, 2) if b < EARLY else (b, 1)
             if first not in adj_sets:
                 grouped = keep.tile([P, count * N], BF16, name="grouped_adj%d" % first, align_bytes=64)
                 codes = keep.tile([P, count * 2 * P], U32, name="adj_codes%d" % first, align_bytes=64)
@@ -159,9 +151,9 @@ def tile_graphconvolution_pb_w4_kernel(tc, adj_bytes, adj_scale, x, weight_words
             )
             word_sets[b] = wide[:].bitcast(F32).rearrange("r (u g p) -> r u g p", u=2, g=2)
 
-        def widen_plain(copy, b):
+        def widen_plain(b):
             wide = per_block.tile([P, N], BF16, name="wide", align_bytes=64)
-            copy(wide[:], adj_rows[b].bitcast(FP8))
+            on_scalar(wide[:], adj_rows[b].bitcast(FP8))
             word_sets[b] = wide[:].bitcast(F32).rearrange("r (g p u) -> r u g p", u=2, g=2)
 
         def turn(b):
@@ -187,24 +179,22 @@ def tile_graphconvolution_pb_w4_kernel(tc, adj_bytes, adj_scale, x, weight_words
 
         ax_bank, grouped_ax, ax_codes, ax_scales = {}, {}, {}, {}
 
-        def stage1(blocks, h, g, lo, hi):
-            if g == 0 and lo == 0:
-                for b in blocks:
-                    ax_bank[b, h] = take_bank(("ax", b, h), [P, 4, P])
-            for a in range(lo, hi):
+        def stage1(b, h, g):
+            if g == 0:
+                ax_bank[b, h] = take_bank(("ax", b, h), [P, 4, P])
+            grouped, codes, scales, k = adj_set(b)
+            nodes = slice(P * (2 * k + g), P * (2 * k + g + 1))
+            for a in range(4):
                 group = slice(P * a, P * (a + 1))
-                for b in blocks:
-                    grouped, codes, scales, k = adj_set(b)
-                    nodes = slice(P * (2 * k + g), P * (2 * k + g + 1))
-                    nc.tensor.matmul_mx(
-                        out=ax_bank[b, h][:, a, :],
-                        lhsT=x_codes[:, h, g, group].bitcast(FP8X4),
-                        lhsT_scale=x_scales[:, h, g, group],
-                        rhs=codes[:, nodes].bitcast(FP8X4),
-                        rhs_scale=scales[:, nodes],
-                        start=(g == 0 and a == 0),
-                        stop=(g == 1 and a == 3),
-                    )
+                nc.tensor.matmul_mx(
+                    out=ax_bank[b, h][:, a, :],
+                    lhsT=x_codes[:, h, g, group].bitcast(FP8X4),
+                    lhsT_scale=x_scales[:, h, g, group],
+                    rhs=codes[:, nodes].bitcast(FP8X4),
+                    rhs_scale=scales[:, nodes],
+                    start=(g == 0 and a == 0),
+                    stop=(g == 1 and a == 3),
+                )
 
         def ax_copy(copy, b, h):
             if b not in grouped_ax:
@@ -244,33 +234,29 @@ def tile_graphconvolution_pb_w4_kernel(tc, adj_bytes, adj_scale, x, weight_words
 
         def out_copy(copy, b, lo, hi):
             width = hi - lo
-            out_tile[b, lo] = per_block.tile([P, width], F32, name="out%d" % width, bufs=8 if width == HALF else 2 * SPLIT)
+            out_tile[b, lo] = per_block.tile([P, width], F32, name="out%d" % width, bufs=8)
             copy(out_tile[b, lo][:], out_bank[b, lo][:])
             emptied.add(("out", b, lo))
 
         def store(b, lo, hi):
             nc.sync.dma_start(out=out_rows[b][:, lo:hi], in_=out_tile[b, lo][:])
 
-        def warm_up(count):
+        def warm_up():
             unread = psum.tile([P, 4, P], F32, name="bank%d" % (BANKS - 1))
-            for i in range(count):
+            for i in range(WARM_UPS):
                 nc.tensor.matmul(unread[:], lhsT=ones[:], rhs=ones[:].unsqueeze(1).to_broadcast([P, 4, P]), start=True, stop=True)
 
         def results(fn, *args):
             if fn in (widen_sorted, widen_plain):
-                return [("wide", args[-1])]
+                return [("wide",) + args]
             if fn == adj_quantise:
                 return [(adj_quantise, b) for b in range(args[0], args[0] + args[1])]
             if fn == x_copy:
                 return [("strip", args[1], args[2], s) for s in range(args[3], args[4])]
             if fn == x_pool:
-                return [("strip", args[0], args[1], s) for s in range(args[2], args[3])]
+                return [("strip",) + args + (s,) for s in range(STRIPS)]
             if fn == x_collect:
-                return [("strip",) + args + (s,) for s in range(SPREAD_FROM[args], STRIPS)]
-            if fn == x_quantise:
-                return [(x_quantise, args[0], args[1], a) for a in range(args[2], args[3])]
-            if fn == stage1:
-                return [(stage1, b, args[1], args[2], a) for b in args[0] for a in range(args[3], args[4])]
+                return [("strip",) + args + (s,) for s in range(COPIED, STRIPS)]
             if fn == ax_quantise:
                 return [(ax_quantise, args[0], h) for h in range(args[1], args[2])]
             if fn == stage2:
@@ -285,11 +271,11 @@ def tile_graphconvolution_pb_w4_kernel(tc, adj_bytes, adj_scale, x, weight_words
             if fn == adj_quantise:
                 return [(scale_adj, b) for b in range(args[0], args[0] + args[1])]
             if fn == x_quantise:
-                return [("strip",) + args[:2] + (s,) for s in range(STRIPS)]
+                return [("strip",) + args + (s,) for s in range(STRIPS)]
             if fn == stage1:
-                return [(x_quantise, args[2], args[1], a) for a in range(args[3], args[4])] + [(adj_quantise, b) for b in args[0]]
+                return [(x_quantise, args[2], args[1]), (adj_quantise, args[0])]
             if fn == ax_copy:
-                return [(stage1,) + args[1:] + (1, 3)]
+                return [(stage1,) + args[1:] + (1,)]
             if fn == ax_quantise:
                 return [(ax_copy, args[0], h) for h in range(args[1], args[2])]
             if fn == stage2:
@@ -300,8 +286,8 @@ def tile_graphconvolution_pb_w4_kernel(tc, adj_bytes, adj_scale, x, weight_words
             return [(source[fn],) + args] if fn in source else []
 
         def banks_taken(fn, *args):
-            if fn == stage1 and args[2:4] == (0, 0):
-                return [("ax", b, args[1]) for b in args[0]]
+            if fn == stage1 and args[2] == 0:
+                return [("ax",) + args[:2]]
             if fn == stage2 and args[3:] == ((1,),):
                 return []
             kind = {turn: "adj", x_spread: "x", stage2: "out"}
@@ -334,61 +320,59 @@ def tile_graphconvolution_pb_w4_kernel(tc, adj_bytes, adj_scale, x, weight_words
         make_identity(nc, ident[:])
         make_identity(nc, ident16[:])
 
-        halves = [(b, lo) for b in range(BLOCKS) for lo in (0, HALF)]
-        pieces = [(b, lo, lo + HALF) for b, lo in halves[:-SPLIT]]
-        pieces += [(b, lo + q, lo + q + 2 * P) for b, lo in halves[-SPLIT:] for q in (0, 2 * P)]
+        halves = [(b, lo, lo + HALF) for b in range(LAST - 1) for lo in (0, HALF)]
+        quarters = [(b, lo, lo + 2 * P) for b in (LAST - 1, LAST) for lo in range(0, N, 2 * P)]
 
         def half_stage1(b, h):
-            return [(stage1, (b,), h, g, 0, 4) for g in range(2)]
+            return [(stage1, b, h, g) for g in range(2)]
 
-        def whole_stage1(b):
-            return half_stage1(b, 0) + half_stage1(b, 1)
+        def out_halves(first, count):
+            return [(stage2,) + piece for piece in halves[first : first + count]]
 
-        tensor = [(warm_up, WARM_UPS), (turn, 0), (warm_up, 1), (turn, 1), (warm_up, 1), (turn, 3), (turn, 2), (turn, 4)]
+        tensor = [(warm_up,), (turn, 0), (turn, 1), (turn, 3), (turn, 2), (turn, 4)]
         tensor += [(x_spread, 1, 0), (turn, 5), (x_spread, 0, 1)]
-        for h in range(2):
-            tensor += [(stage1, (b,), h, g, 0, 4) for g in range(2) for b in range(4)]
-        tensor += whole_stage1(4)
-        between = [[(turn, 6), (turn, 7)], whole_stage1(5), whole_stage1(6), half_stage1(LAST, 0), half_stage1(LAST, 1), []]
-        first = 0
-        for count, other in zip((2, 3, 3, 3, 1, 4), between):
-            tensor += [(stage2,) + piece for piece in pieces[first : first + count]] + other
-            first = first + count
-        tensor += [(stage2,) + piece + ((h,),) for h in range(2) for piece in pieces[first : first + 2]]
-        tensor += [(stage2,) + piece for piece in pieces[first + 2 :]]
+        tensor += [(stage1, b, h, g) for h in range(2) for g in range(2) for b in range(EARLY)]
+        tensor += half_stage1(4, 0) + half_stage1(4, 1)
+        tensor += out_halves(0, 2) + [(turn, 6), (turn, 7)]
+        tensor += out_halves(2, 3) + half_stage1(5, 0) + half_stage1(5, 1)
+        tensor += out_halves(5, 3) + half_stage1(6, 0) + half_stage1(6, 1)
+        tensor += out_halves(8, 3) + half_stage1(7, 0) + out_halves(11, 1) + half_stage1(7, 1)
+        tensor += [(stage2,) + piece for piece in quarters[:4]]
+        tensor += [(stage2,) + piece + ((h,),) for h in range(2) for piece in quarters[4:6]]
+        tensor += [(stage2,) + piece for piece in quarters[6:]]
 
         for step in tensor:
             taken.extend(banks_taken(*step))
         freed.extend(taken)
-        for content, after in ((("adj", 4), ("ax", 1, 0)), (("adj", 5), ("ax", 4, 0))):
-            freed.remove(content)
-            freed.insert(freed.index(after) + 1, content)
+        for b, after in ((4, ("ax", 1, 0)), (5, ("ax", 4, 0))):
+            freed.remove(("adj", b))
+            freed.insert(freed.index(after) + 1, ("adj", b))
 
         filled = []
         for step in tensor:
-            if step[0] == stage1 and step[3] == 1 and step[5] == 4:
-                filled += [(ax_copy, b, step[2]) for b in step[1]]
+            if step[0] == stage1 and step[3] == 1:
+                filled.append((ax_copy,) + step[1:3])
             if step[0] == stage2 and step[4:] != ((0,),):
                 filled.append((out_copy,) + step[1:4])
-        for_vector = [(out_copy, 1, 0, HALF), (out_copy, 2, HALF, N), (out_copy, 4, 0, HALF), (ax_copy, 6, 1), (out_copy, 5, 0, HALF)]
-        for_vector += [(ax_copy, LAST, 1)] + [(out_copy,) + piece for piece in pieces[14::2]]
+        for_vector = [(out_copy,) + halves[k] for k in (2, 5, 8)]
+        for_vector += [(ax_copy, LAST - 1, 1), (out_copy,) + halves[10], (ax_copy, LAST, 1)]
+        for_vector += [(out_copy,) + piece for piece in quarters[2::2]]
         v_empty = [(step[0], on_vector) + step[1:] for step in for_vector]
 
         vector = [(widen_sorted, 0), (widen_sorted, 1), (widen_sorted, 3)]
         vector += [(scale_adj, 0), (scale_adj, 1), (scale_adj, 3), (scale_adj, 2)]
-        vector += [(adj_quantise, 0, 2), (x_quantise, 0, 0, 0, 4), (adj_quantise, 2, 2), (x_quantise, 1, 0, 0, 4)]
-        vector += [(x_copy, on_vector, 1, 1, 0, V_STRIPS_11), (x_quantise, 0, 1, 0, 4), (x_quantise, 1, 1, 0, 4), (scale_adj, 4)]
-        vector += [(ax_quantise, 0, 0, 1), (adj_quantise, 4, 1), (widen_sorted, 6), (widen_sorted, 7), (ax_quantise, 0, 1, 2), (ax_quantise, 1, 0, 2)]
-        vector += [(scale_adj, 5), (ax_quantise, 2, 0, 2), (adj_quantise, 5, 1), (ax_quantise, 3, 0, 2), (scale_adj, 6), v_empty[0]]
-        vector += [(adj_quantise, 6, 1), (ax_quantise, 4, 0, 2), (scale_adj, 7), v_empty[1], (adj_quantise, 7, 1)]
-        vector += [(ax_quantise, 5, 0, 2), v_empty[2], v_empty[3], v_empty[4], (ax_quantise, 6, 0, 2), (ax_quantise, LAST, 0, 1), v_empty[5]]
-        vector += [(ax_quantise, LAST, 1, 2)] + v_empty[6:]
+        vector += [(adj_quantise, 0, 2), (x_quantise, 0, 0), (adj_quantise, 2, 2), (x_quantise, 1, 0)]
+        vector += [(x_copy, on_vector, 1, 1, 0, V_STRIPS), (x_quantise, 0, 1), (x_quantise, 1, 1), (scale_adj, 4)]
+        vector += [(ax_quantise, 0, 0, 1), (adj_quantise, 4, 1), (widen_sorted, 6), (widen_sorted, 7), (ax_quantise, 0, 1, 2)]
+        vector += [(ax_quantise, 1, 0, 2), (scale_adj, 5), (ax_quantise, 2, 0, 2), (adj_quantise, 5, 1), (ax_quantise, 3, 0, 2)]
+        vector += [(scale_adj, 6), v_empty[0], (adj_quantise, 6, 1), (ax_quantise, 4, 0, 2), (scale_adj, 7), v_empty[1]]
+        vector += [(adj_quantise, 7, 1), (ax_quantise, 5, 0, 2), v_empty[2], v_empty[3], v_empty[4], (ax_quantise, 6, 0, 2)]
+        vector += [(ax_quantise, LAST, 0, 1), v_empty[5], (ax_quantise, LAST, 1, 2)] + v_empty[6:]
 
-        scalar = [(widen_plain, on_scalar, 2), (widen_plain, on_scalar, 4), (widen_plain, on_scalar, 5)]
-        scalar += [(x_copy, on_scalar, 1, 0, 0, SPREAD_FROM[1, 0]), (x_copy, on_scalar, 0, 1, 0, SPREAD_FROM[0, 1])]
-        scalar += [(x_collect, 1, 0), (x_copy, on_scalar, 1, 1, V_STRIPS_11, S_CUT), (x_collect, 0, 1), (x_copy, on_scalar, 1, 1, S_CUT, STRIPS)]
+        scalar = [(widen_plain, 2), (widen_plain, 4), (widen_plain, 5)]
+        scalar += [(x_copy, on_scalar, 1, 0, 0, COPIED), (x_copy, on_scalar, 0, 1, 0, COPIED), (x_collect, 1, 0)]
+        scalar += [(x_copy, on_scalar, 1, 1, V_STRIPS, S_CUT), (x_collect, 0, 1), (x_copy, on_scalar, 1, 1, S_CUT, STRIPS)]
         scalar += [(step[0], on_scalar) + step[1:] for step in filled if step not in for_vector]
 
-        pool = [(x_pool, 0, 0, 0, STRIPS)]
-        stores = [(store,) + piece for piece in pieces]
-        issue([tensor, vector, scalar, pool, stores])
+        stores = [(store,) + piece for piece in halves + quarters]
+        issue([tensor, vector, scalar, [(x_pool, 0, 0)], stores])

@@ -140,27 +140,29 @@ def tile_graphconvolution_pb_w4_kernel(tc, adj_bytes, adj_scale, x, weight_words
                 adj_sets[first] = (grouped, codes, scales)
             return adj_sets[first] + (b - first,)
 
-        def widen_sorted(b):
-            wide = per_block.tile([P, N], BF16, name="wide", align_bytes=64)
+        def widen_sorted(b, lo, hi):
+            wide = per_block.tile([P, HALF * (hi - lo)], BF16, name="wide", bufs=BLOCKS + 1, align_bytes=64)
             nc.vector.tensor_scalar(
                 out=wide[:].rearrange("r (u w e) -> r w u e", u=2, e=2),
-                in0=adj_rows[b].bitcast(FP8).rearrange("r (w u e) -> r w u e", u=2, e=2),
+                in0=adj_rows[b][:, HALF * lo : HALF * hi].bitcast(FP8).rearrange("r (w u e) -> r w u e", u=2, e=2),
                 scalar1=one[:],
                 scalar2=None,
                 op0=MULT,
             )
-            word_sets[b] = wide[:].bitcast(F32).rearrange("r (u g p) -> r u g p", u=2, g=2)
+            for g in range(lo, hi):
+                word_sets[b, g] = wide[:].bitcast(F32).rearrange("r (u g p) -> r g u p", u=2, p=P)[:, g - lo]
 
-        def widen_plain(b):
-            wide = per_block.tile([P, N], BF16, name="wide", align_bytes=64)
-            on_scalar(wide[:], adj_rows[b].bitcast(FP8))
-            word_sets[b] = wide[:].bitcast(F32).rearrange("r (g p u) -> r u g p", u=2, g=2)
+        def widen_plain(b, lo, hi):
+            wide = per_block.tile([P, HALF * (hi - lo)], BF16, name="wide", bufs=BLOCKS + 1, align_bytes=64)
+            on_scalar(wide[:], adj_rows[b][:, HALF * lo : HALF * hi].bitcast(FP8))
+            for g in range(lo, hi):
+                word_sets[b, g] = wide[:].bitcast(F32).rearrange("r (g p u) -> r g u p", u=2, p=P)[:, g - lo]
 
         def turn(b):
             bank = take_bank(("adj", b), [P, 2, 2, P])
             for g in range(2):
                 for u in range(2):
-                    nc.tensor.transpose(bank[:, u, g, :], word_sets[b][:, u, g, :], ident[:])
+                    nc.tensor.transpose(bank[:, u, g, :], word_sets[b, g][:, u, :], ident[:])
             turned[b] = bank
 
         def scale_adj(b):
@@ -248,7 +250,7 @@ def tile_graphconvolution_pb_w4_kernel(tc, adj_bytes, adj_scale, x, weight_words
 
         def results(fn, *args):
             if fn in (widen_sorted, widen_plain):
-                return [("wide",) + args]
+                return [("wide", args[0], g) for g in range(args[1], args[2])]
             if fn == adj_quantise:
                 return [(adj_quantise, b) for b in range(args[0], args[0] + args[1])]
             if fn == x_copy:
@@ -267,7 +269,7 @@ def tile_graphconvolution_pb_w4_kernel(tc, adj_bytes, adj_scale, x, weight_words
 
         def reads(fn, *args):
             if fn == turn:
-                return [("wide",) + args]
+                return [("wide", args[0], g) for g in range(2)]
             if fn == adj_quantise:
                 return [(scale_adj, b) for b in range(args[0], args[0] + args[1])]
             if fn == x_quantise:
@@ -329,7 +331,7 @@ def tile_graphconvolution_pb_w4_kernel(tc, adj_bytes, adj_scale, x, weight_words
         def out_halves(first, count):
             return [(stage2,) + piece for piece in halves[first : first + count]]
 
-        tensor = [(warm_up,), (turn, 0), (turn, 1), (turn, 3), (turn, 2), (turn, 4)]
+        tensor = [(warm_up,)] + [(turn, b) for b in range(5)]
         tensor += [(x_spread, 1, 0), (turn, 5), (x_spread, 0, 1)]
         tensor += [(stage1, b, h, g) for h in range(2) for g in range(2) for b in range(EARLY)]
         tensor += half_stage1(4, 0) + half_stage1(4, 1)
@@ -359,17 +361,17 @@ def tile_graphconvolution_pb_w4_kernel(tc, adj_bytes, adj_scale, x, weight_words
         for_vector += [(out_copy,) + piece for piece in quarters[2::2]]
         v_empty = [(step[0], on_vector) + step[1:] for step in for_vector]
 
-        vector = [(widen_sorted, 0), (widen_sorted, 1), (widen_sorted, 3)]
-        vector += [(scale_adj, 0), (scale_adj, 1), (scale_adj, 3), (scale_adj, 2)]
+        vector = [(widen_sorted, 0, 0, 2), (widen_sorted, 1, 0, 2), (widen_sorted, 3, 0, 1)]
+        vector += [(scale_adj, b) for b in range(EARLY)]
         vector += [(adj_quantise, 0, 2), (x_quantise, 0, 0), (adj_quantise, 2, 2), (x_quantise, 1, 0)]
         vector += [(x_copy, on_vector, 1, 1, 0, V_STRIPS), (x_quantise, 0, 1), (x_quantise, 1, 1), (scale_adj, 4)]
-        vector += [(ax_quantise, 0, 0, 1), (adj_quantise, 4, 1), (widen_sorted, 6), (widen_sorted, 7), (ax_quantise, 0, 1, 2)]
+        vector += [(ax_quantise, 0, 0, 1), (adj_quantise, 4, 1), (widen_sorted, 6, 0, 2), (widen_sorted, 7, 0, 2), (ax_quantise, 0, 1, 2)]
         vector += [(ax_quantise, 1, 0, 2), (scale_adj, 5), (ax_quantise, 2, 0, 2), (adj_quantise, 5, 1), (ax_quantise, 3, 0, 2)]
         vector += [(scale_adj, 6), v_empty[0], (adj_quantise, 6, 1), (ax_quantise, 4, 0, 2), (scale_adj, 7), v_empty[1]]
         vector += [(adj_quantise, 7, 1), (ax_quantise, 5, 0, 2), v_empty[2], v_empty[3], v_empty[4], (ax_quantise, 6, 0, 2)]
         vector += [(ax_quantise, LAST, 0, 1), v_empty[5], (ax_quantise, LAST, 1, 2)] + v_empty[6:]
 
-        scalar = [(widen_plain, 2), (widen_plain, 4), (widen_plain, 5)]
+        scalar = [(widen_plain, 2, 0, 2), (widen_plain, 3, 1, 2), (widen_plain, 4, 0, 2), (widen_plain, 5, 0, 2)]
         scalar += [(x_copy, on_scalar, 1, 0, 0, COPIED), (x_copy, on_scalar, 0, 1, 0, COPIED), (x_collect, 1, 0)]
         scalar += [(x_copy, on_scalar, 1, 1, V_STRIPS, S_CUT), (x_collect, 0, 1), (x_copy, on_scalar, 1, 1, S_CUT, STRIPS)]
         scalar += [(step[0], on_scalar) + step[1:] for step in filled if step not in for_vector]

@@ -220,19 +220,17 @@ def tile_graphconvolution_pb_w4_kernel(tc, adj_bytes, adj_scale, x, weight_words
         def stage2(b, lo, hi, passes=(0, 1)):
             if passes[0] == 0:
                 out_bank[b, lo] = take_bank(("out", b, lo), [P, hi - lo])
-            width = HALF if hi - lo == HALF else P
             for h in passes:
                 nodes = slice(P * h, P * (h + 1))
-                for first in range(lo, hi, width):
-                    nc.tensor.matmul_mx(
-                        out=out_bank[b, lo][:, first - lo : first - lo + width],
-                        lhsT=ax_codes[b][:, nodes].bitcast(FP8X4),
-                        lhsT_scale=ax_scales[b][:, nodes],
-                        rhs=w_words[:, h, 2 * first : 2 * (first + width)].bitcast(FP4X4),
-                        rhs_scale=w_scales[:, h, first : first + width],
-                        start=(h == 0 and first == lo),
-                        stop=(h == 1 and first + width == hi),
-                    )
+                nc.tensor.matmul_mx(
+                    out=out_bank[b, lo][:],
+                    lhsT=ax_codes[b][:, nodes].bitcast(FP8X4),
+                    lhsT_scale=ax_scales[b][:, nodes],
+                    rhs=w_words[:, h, 2 * lo : 2 * hi].bitcast(FP4X4),
+                    rhs_scale=w_scales[:, h, lo:hi],
+                    start=(h == 0),
+                    stop=(h == 1),
+                )
 
         def out_copy(copy, b, lo, hi):
             width = hi - lo

from contextlib import ExitStack

import concourse.mybir as mybir
from concourse.masks import make_identity

F32 = mybir.dt.float32
BF16 = mybir.dt.bfloat16
U32 = mybir.dt.uint32
I32 = mybir.dt.int32
U8 = mybir.dt.uint8
FP8 = mybir.dt.float8_e4m3fn
FP8X4 = mybir.dt.float8_e4m3fn_x4
FP4X4 = mybir.dt.float4_e2m1fn_x4
MULT = mybir.AluOpType.mult
ADD = mybir.AluOpType.add

P = 128
N = 1024
HALF = 512
BLOCKS = N // P
LAST = BLOCKS - 1
BANKS = 8
FLOPS = 2 * 2 * N * N * N

STRIPS = 64
COPIED = STRIPS // 2
V_STRIPS = 24
S_CUT = 44
EARLY = 4
WARM_UPS = 5


def tile_graphconvolution_pb_w4_kernel(tc, adj_bytes, adj_scale, x, weight_words, weight_scales, out):
    nc = tc.nc
    with ExitStack() as ctx:
        keep = ctx.enter_context(tc.tile_pool(name="keep", bufs=1))
        per_block = ctx.enter_context(tc.tile_pool(name="per_block", bufs=BLOCKS))
        psum = ctx.enter_context(tc.psum_pool(name="psum", bufs=1))
        ctx.enter_context(tc.manual_schedule())

        def on_vector(dst, src):
            nc.vector.tensor_copy(out=dst, in_=src)

        def on_scalar(dst, src):
            nc.scalar.copy(dst, src)

        taken, freed, bank_of = [], [], {}
        emptied = set()

        def bank_free(content):
            n = taken.index(content)
            return n < BANKS or freed[n - BANKS] in emptied

        def take_bank(content, shape):
            n = taken.index(content)
            bank_of[content] = n if n < BANKS else bank_of[freed[n - BANKS]]
            return psum.tile(shape, F32, name="bank%d" % bank_of[content])

        col_scale = keep.tile([P, 2, 4], F32)
        w_scales = keep.tile([P, 2, N], U8, align_bytes=64)
        w_words = keep.tile([P, 2, 2 * N], U8, align_bytes=64)
        ident = keep.tile([P, P], F32)
        one = keep.tile([P, 1], F32)
        ones = keep.tile([P, P], BF16, align_bytes=64)
        nc.vector.memset(ones[:], 1.0)
        ident16 = keep.tile([P, P], BF16, align_bytes=64)
        x_codes = keep.tile([P, 2, 2, HALF], U32, align_bytes=64)
        x_scales = keep.tile([P, 2, 2, HALF], U8, align_bytes=64)

        x_rows, adj_rows, out_rows = {}, {}, {}

        def load_x(g, h):
            tile = keep.tile([P, 4, HALF], BF16, name="x_rows%d%d" % (g, h), align_bytes=64)
            quarter = x[HALF * g : HALF * (g + 1), HALF * h : HALF * (h + 1)]
            nc.sync.dma_start(out=tile[:], in_=quarter.rearrange("(p t) d -> p t d", t=4))
            x_rows[g, h] = tile

        def load_adj(first, count):
            tile = keep.tile([P, count, N], U8, name="adj_bytes%d" % first, align_bytes=64)
            rows = slice(P * first, P * (first + count))
            nc.sync.dma_start(out=tile[:], in_=adj_bytes[rows, :].rearrange("(p k) j -> p k j", k=count))
            for k in range(count):
                adj_rows[first + k] = tile[:, k, :]
                out_rows[first + k] = out[rows, :].rearrange("(p k) f -> p k f", k=count)[:, k, :]

        def load_weight():
            for q in range(4):
                nc.sync.dma_start(
                    out=w_scales[32 * q : 32 * q + 4, :, :].bitcast(I32),
                    in_=weight_scales[:, 4 * q : 4 * q + 4, :].rearrange("g q n -> q g n").bitcast(I32),
                )
            nc.sync.dma_start(out=w_words[:].bitcast(I32), in_=weight_words.rearrange("g p n -> p g n").bitcast(I32))

        grouped_x, spread_x = {}, {}

        def x_tile(g, h):
            if (g, h) not in grouped_x:
                grouped_x[g, h] = keep.tile([P, 4 * HALF], BF16, name="grouped_x%d%d" % (g, h), align_bytes=64)
            return grouped_x[g, h]

        def x_copy(copy, g, h, lo, hi):
            src = x_rows[g, h][:].rearrange("p t (s i a) -> p s a t i", i=2, a=4)[:, lo:hi]
            dst = x_tile(g, h)[:].rearrange("p (a s i t) -> p s a t i", a=4, i=2, t=4)[:, lo:hi]
            copy(dst, src)

        def x_pool(g, h):
            src = x_rows[g, h][:].rearrange("p t (m a) -> p m a t", a=4)
            dst = x_tile(g, h)[:].rearrange("p (a m t) -> p m a t", a=4, t=4)
            nc.gpsimd.tensor_scalar(out=dst, in0=src, scalar1=1.0, scalar2=0.0, op0=MULT, op1=ADD)

        def x_spread(g, h):
            bank = take_bank(("x", g, h), [P, HALF])
            for c in range(2):
                nc.tensor.matmul(
                    bank[:].bitcast(BF16)[:, HALF * c : HALF * (c + 1)].rearrange("p (d t) -> p t d", t=4),
                    lhsT=ident16[:],
                    rhs=x_rows[g, h][:, :, P * (2 + c) : P * (3 + c)],
                    start=True,
                    stop=True,
                )
            spread_x[g, h] = bank

        def x_collect(g, h):
            dst = x_tile(g, h)[:].bitcast(F32).rearrange("p (a m z) -> p a m z", a=4, z=2)[:, :, P // 2 :, :]
            on_scalar(dst, spread_x[g, h][:].rearrange("p (m a z) -> p a m z", a=4, z=2))
            emptied.add(("x", g, h))

        def x_quantise(g, h):
            nc.vector.quantize_mx(out=x_codes[:, h, g, :].bitcast(FP8X4), scales=x_scales[:, h, g, :], in_=grouped_x[g, h][:])

        word_sets, turned = {}, {}
        adj_sets = {}

        def adj_set(b):
            first, count = (b - b % 2, 2) if b < EARLY else (b, 1)
            if first not in adj_sets:
                grouped = keep.tile([P, count * N], BF16, name="grouped_adj%d" % first, align_bytes=64)
                codes = keep.tile([P, count * 2 * P], U32, name="adj_codes%d" % first, align_bytes=64)
                scales = keep.tile([P, count * 2 * P], U8, name="adj_scales%d" % first, align_bytes=64)
                adj_sets[first] = (grouped, codes, scales)
            return adj_sets[first] + (b - first,)

        def widen_sorted(b, lo, hi):
            wide = per_block.tile([P, HALF * (hi - lo)], BF16, name="wide", bufs=BLOCKS + 1, align_bytes=64)
            nc.vector.tensor_scalar(
                out=wide[:].rearrange("r (u w e) -> r w u e", u=2, e=2),
                in0=adj_rows[b][:, HALF * lo : HALF * hi].bitcast(FP8).rearrange("r (w u e) -> r w u e", u=2, e=2),
                scalar1=one[:],
                scalar2=None,
                op0=MULT,
            )
            for g in range(lo, hi):
                word_sets[b, g] = wide[:].bitcast(F32).rearrange("r (u g p) -> r g u p", u=2, p=P)[:, g - lo]

        def widen_plain(b, lo, hi):
            wide = per_block.tile([P, HALF * (hi - lo)], BF16, name="wide", bufs=BLOCKS + 1, align_bytes=64)
            on_scalar(wide[:], adj_rows[b][:, HALF * lo : HALF * hi].bitcast(FP8))
            for g in range(lo, hi):
                word_sets[b, g] = wide[:].bitcast(F32).rearrange("r (g p u) -> r g u p", u=2, p=P)[:, g - lo]

        def turn(b):
            bank = take_bank(("adj", b), [P, 2, 2, P])
            for g in range(2):
                for u in range(2):
                    nc.tensor.transpose(bank[:, u, g, :], word_sets[b, g][:, u, :], ident[:])
            turned[b] = bank

        def scale_adj(b):
            grouped, codes, scales, k = adj_set(b)
            nc.vector.tensor_tensor(
                out=grouped[:, N * k : N * (k + 1)].rearrange("p (g r u e) -> p g r u e", g=2, u=2, e=2),
                in0=turned[b][:].bitcast(BF16).rearrange("p u g (r e) -> p g r u e", e=2),
                in1=col_scale[:].rearrange("p g (u e) -> p g u e", e=2).unsqueeze(2).to_broadcast([P, 2, P, 2, 2]),
                op=MULT,
            )
            emptied.add(("adj", b))

        def adj_quantise(first, count):
            grouped, codes, scales, k = adj_set(first)
            nc.vector.quantize_mx(out=codes[:].bitcast(FP8X4), scales=scales[:], in_=grouped[:])

        ax_bank, grouped_ax, ax_codes, ax_scales = {}, {}, {}, {}

        def stage1(b, h, g):
            if g == 0:
                ax_bank[b, h] = take_bank(("ax", b, h), [P, 4, P])
            grouped, codes, scales, k = adj_set(b)
            nodes = slice(P * (2 * k + g), P * (2 * k + g + 1))
            for a in range(4):
                group = slice(P * a, P * (a + 1))
                nc.tensor.matmul_mx(
                    out=ax_bank[b, h][:, a, :],
                    lhsT=x_codes[:, h, g, group].bitcast(FP8X4),
                    lhsT_scale=x_scales[:, h, g, group],
                    rhs=codes[:, nodes].bitcast(FP8X4),
                    rhs_scale=scales[:, nodes],
                    start=(g == 0 and a == 0),
                    stop=(g == 1 and a == 3),
                )

        def ax_copy(copy, b, h):
            if b not in grouped_ax:
                grouped_ax[b] = per_block.tile([P, 2, HALF], BF16, name="grouped_ax", align_bytes=64)
            copy(grouped_ax[b][:, h, :].rearrange("p (r a) -> p r a", a=4), ax_bank[b, h][:].rearrange("p a r -> p r a"))
            emptied.add(("ax", b, h))

        def ax_quantise(b, lo, hi):
            if b not in ax_codes:
                ax_codes[b] = per_block.tile([P, 2 * P], U32, name="ax_codes", align_bytes=64)
                ax_scales[b] = per_block.tile([P, 2 * P], U8, name="ax_scales", align_bytes=64)
            nodes = slice(P * lo, P * hi)
            nc.vector.quantize_mx(
                out=ax_codes[b][:, nodes].bitcast(FP8X4),
                scales=ax_scales[b][:, nodes],
                in_=grouped_ax[b][:, lo:hi, :].rearrange("p h n -> p (h n)"),
            )

        out_bank, out_tile = {}, {}

        def stage2(b, lo, hi, passes=(0, 1)):
            if passes[0] == 0:
                out_bank[b, lo] = take_bank(("out", b, lo), [P, hi - lo])
            for h in passes:
                nodes = slice(P * h, P * (h + 1))
                nc.tensor.matmul_mx(
                    out=out_bank[b, lo][:],
                    lhsT=ax_codes[b][:, nodes].bitcast(FP8X4),
                    lhsT_scale=ax_scales[b][:, nodes],
                    rhs=w_words[:, h, 2 * lo : 2 * hi].bitcast(FP4X4),
                    rhs_scale=w_scales[:, h, lo:hi],
                    start=(h == 0),
                    stop=(h == 1),
                )

        def out_copy(copy, b, lo, hi):
            width = hi - lo
            out_tile[b, lo] = per_block.tile([P, width], F32, name="out%d" % width, bufs=8)
            copy(out_tile[b, lo][:], out_bank[b, lo][:])
            emptied.add(("out", b, lo))

        def store(b, lo, hi):
            nc.sync.dma_start(out=out_rows[b][:, lo:hi], in_=out_tile[b, lo][:])

        def warm_up():
            unread = psum.tile([P, 4, P], F32, name="bank%d" % (BANKS - 1))
            for i in range(WARM_UPS):
                nc.tensor.matmul(unread[:], lhsT=ones[:], rhs=ones[:].unsqueeze(1).to_broadcast([P, 4, P]), start=True, stop=True)

        def results(fn, *args):
            if fn in (widen_sorted, widen_plain):
                return [("wide", args[0], g) for g in range(args[1], args[2])]
            if fn == adj_quantise:
                return [(adj_quantise, b) for b in range(args[0], args[0] + args[1])]
            if fn == x_copy:
                return [("strip", args[1], args[2], s) for s in range(args[3], args[4])]
            if fn == x_pool:
                return [("strip",) + args + (s,) for s in range(STRIPS)]
            if fn == x_collect:
                return [("strip",) + args + (s,) for s in range(COPIED, STRIPS)]
            if fn == ax_quantise:
                return [(ax_quantise, args[0], h) for h in range(args[1], args[2])]
            if fn == stage2:
                return [(stage2,) + args[:3]] if args[3:] != ((0,),) else []
            if fn in (ax_copy, out_copy):
                return [(fn,) + args[1:]]
            return [(fn,) + args]

        def reads(fn, *args):
            if fn == turn:
                return [("wide", args[0], g) for g in range(2)]
            if fn == adj_quantise:
                return [(scale_adj, b) for b in range(args[0], args[0] + args[1])]
            if fn == x_quantise:
                return [("strip",) + args + (s,) for s in range(STRIPS)]
            if fn == stage1:
                return [(x_quantise, args[2], args[1]), (adj_quantise, args[0])]
            if fn == ax_copy:
                return [(stage1,) + args[1:] + (1,)]
            if fn == ax_quantise:
                return [(ax_copy, args[0], h) for h in range(args[1], args[2])]
            if fn == stage2:
                return [(ax_quantise, args[0], h) for h in (args[3] if args[3:] else range(2))]
            if fn == out_copy:
                return [(stage2,) + args[1:]]
            source = {x_collect: x_spread, scale_adj: turn, store: out_copy}
            return [(source[fn],) + args] if fn in source else []

        def banks_taken(fn, *args):
            if fn == stage1 and args[2] == 0:
                return [("ax",) + args[:2]]
            if fn == stage2 and args[3:] == ((1,),):
                return []
            kind = {turn: "adj", x_spread: "x", stage2: "out"}
            return [(kind[fn],) + args[:2]] if fn in kind else []

        def issue(queues):
            done = set()
            while any(queues):
                for queue in queues:
                    while queue and all(r in done for r in reads(*queue[0])) and all(bank_free(c) for c in banks_taken(*queue[0])):
                        step = queue[0]
                        queue.remove(step)
                        step[0](*step[1:])
                        for r in results(*step):
                            done.add(r)

        for b in (0, 2, 1):
            load_adj(b, 1)
        load_adj(3, 2)
        nc.sync.dma_start(out=col_scale[:], in_=adj_scale.rearrange("o (g p t) -> p (o g) t", g=2, t=4))
        load_x(0, 0)
        load_adj(5, 1)
        load_x(1, 0)
        load_x(0, 1)
        load_x(1, 1)
        load_adj(6, 2)
        nc.vector.memset(w_scales[:].rearrange("p g n -> p (g n)").bitcast(I32), 0)
        nc.vector.memset(one[:], 1.0)
        load_weight()
        make_identity(nc, ident[:])
        make_identity(nc, ident16[:])

        halves = [(b, lo, lo + HALF) for b in range(LAST - 1) for lo in (0, HALF)]
        quarters = [(b, lo, lo + 2 * P) for b in (LAST - 1, LAST) for lo in range(0, N, 2 * P)]

        def half_stage1(b, h):
            return [(stage1, b, h, g) for g in range(2)]

        def out_halves(first, count):
            return [(stage2,) + piece for piece in halves[first : first + count]]

        tensor = [(warm_up,)] + [(turn, b) for b in range(5)]
        tensor += [(x_spread, 1, 0), (turn, 5), (x_spread, 0, 1)]
        tensor += [(stage1, b, h, g) for h in range(2) for g in range(2) for b in range(EARLY)]
        tensor += half_stage1(4, 0) + half_stage1(4, 1)
        tensor += out_halves(0, 2) + [(turn, 6), (turn, 7)]
        tensor += out_halves(2, 3) + half_stage1(5, 0) + half_stage1(5, 1)
        tensor += out_halves(5, 3) + half_stage1(6, 0) + half_stage1(6, 1)
        tensor += out_halves(8, 3) + half_stage1(7, 0) + out_halves(11, 1) + half_stage1(7, 1)
        tensor += [(stage2,) + piece for piece in quarters[:4]]
        tensor += [(stage2,) + piece + ((h,),) for h in range(2) for piece in quarters[4:6]]
        tensor += [(stage2,) + piece for piece in quarters[6:]]

        for step in tensor:
            taken.extend(banks_taken(*step))
        freed.extend(taken)
        for b, after in ((4, ("ax", 1, 0)), (5, ("ax", 4, 0))):
            freed.remove(("adj", b))
            freed.insert(freed.index(after) + 1, ("adj", b))

        filled = []
        for step in tensor:
            if step[0] == stage1 and step[3] == 1:
                filled.append((ax_copy,) + step[1:3])
            if step[0] == stage2 and step[4:] != ((0,),):
                filled.append((out_copy,) + step[1:4])
        for_vector = [(out_copy,) + halves[k] for k in (2, 5, 8)]
        for_vector += [(ax_copy, LAST - 1, 1), (out_copy,) + halves[10], (ax_copy, LAST, 1)]
        for_vector += [(out_copy,) + piece for piece in quarters[2::2]]
        v_empty = [(step[0], on_vector) + step[1:] for step in for_vector]

        vector = [(widen_sorted, 0, 0, 2), (widen_sorted, 1, 0, 2), (widen_sorted, 3, 0, 1)]
        vector += [(scale_adj, b) for b in range(EARLY)]
        vector += [(adj_quantise, 0, 2), (x_quantise, 0, 0), (adj_quantise, 2, 2), (x_quantise, 1, 0)]
        vector += [(x_copy, on_vector, 1, 1, 0, V_STRIPS), (x_quantise, 0, 1), (x_quantise, 1, 1), (scale_adj, 4)]
        vector += [(ax_quantise, 0, 0, 1), (adj_quantise, 4, 1), (widen_sorted, 6, 0, 2), (widen_sorted, 7, 0, 2), (ax_quantise, 0, 1, 2)]
        vector += [(ax_quantise, 1, 0, 2), (scale_adj, 5), (ax_quantise, 2, 0, 2), (adj_quantise, 5, 1), (ax_quantise, 3, 0, 2)]
        vector += [(scale_adj, 6), v_empty[0], (adj_quantise, 6, 1), (ax_quantise, 4, 0, 2), (scale_adj, 7), v_empty[1]]
        vector += [(adj_quantise, 7, 1), (ax_quantise, 5, 0, 2), v_empty[2], v_empty[3], v_empty[4], (ax_quantise, 6, 0, 2)]
        vector += [(ax_quantise, LAST, 0, 1), v_empty[5], (ax_quantise, LAST, 1, 2)] + v_empty[6:]

        scalar = [(widen_plain, 2, 0, 2), (widen_plain, 3, 1, 2), (widen_plain, 4, 0, 2), (widen_plain, 5, 0, 2)]
        scalar += [(x_copy, on_scalar, 1, 0, 0, COPIED), (x_copy, on_scalar, 0, 1, 0, COPIED), (x_collect, 1, 0)]
        scalar += [(x_copy, on_scalar, 1, 1, V_STRIPS, S_CUT), (x_collect, 0, 1), (x_copy, on_scalar, 1, 1, S_CUT, STRIPS)]
        scalar += [(step[0], on_scalar) + step[1:] for step in filled if step not in for_vector]

        stores = [(store,) + piece for piece in halves + quarters]
        issue([tensor, vector, scalar, [(x_pool, 0, 0)], stores])
